import numpy as np
import ml_dtypes


def mxq(x, axis, fmt="e4m3"):
    dtype, down = {"e4m3": (ml_dtypes.float8_e4m3fn, 7), "e5m2": (ml_dtypes.float8_e5m2, 14)}[fmt]
    v = np.moveaxis(np.asarray(x, np.float32).astype(ml_dtypes.bfloat16).astype(np.float64), axis, -1)
    blocks = v.reshape(v.shape[:-1] + (-1, 32))
    amax = np.abs(blocks).max(-1, keepdims=True)
    byte = np.maximum(np.where(amax > 0, np.frexp(amax)[1] - 1 + 127, 0) - down, 1)
    scale = np.exp2(byte - 127.0)
    codes = (blocks / scale).astype(np.float32).astype(dtype).astype(np.float64)
    return np.moveaxis((codes * scale).reshape(v.shape), -1, axis)


WIDE = False


def mx_kscale(k):
    if not WIDE:
        return np.ones(k)
    levels = np.array([10, -10, 5, -5, 0])
    a = np.random.permutation(np.resize(levels, k // 512 * 4)).reshape(k // 512, 4)
    idx = np.arange(k)
    return np.exp2(a[idx // 512, idx % 128 // 32])


BF16 = ml_dtypes.bfloat16


def bf(x):
    return np.asarray(x, np.float32).astype(BF16)


def f64(x):
    return np.asarray(x).astype(np.float64)


E2M1 = np.array([0.0, 0.5, 1.0, 1.5, 2.0, 3.0, 4.0, 6.0, -0.0, -0.5, -1.0, -1.5, -2.0, -3.0, -4.0, -6.0])


def pack_weight(w, fmt):
    k, n = w.shape
    w = f64(bf(w)).reshape(k // 32, 32, n)
    amax = np.abs(w).max(1)
    if fmt == "e4m3":
        byte = np.frexp(amax)[1] - 1 + 127 - 7
    else:
        mant, ex = np.frexp(amax / 6.0)
        byte = np.where(mant > 0.5, ex, ex - 1) + 127
    byte = np.clip(np.where(amax > 0, byte, 1), 1, 254)
    scaled = (w * np.exp2(127.0 - byte)[:, None, :]).reshape(k, n).astype(np.float32)
    by_word = np.ascontiguousarray(scaled.reshape(k // 512, 128, 4, n).transpose(0, 1, 3, 2))
    if fmt == "e4m3":
        words = by_word.astype(ml_dtypes.float8_e4m3fn).view(np.uint8)
    else:
        c = by_word.astype(ml_dtypes.float4_e2m1fn).view(np.uint8) & 0xF
        words = c[..., 0::2] | (c[..., 1::2] << 4)
    return np.ascontiguousarray(words), np.ascontiguousarray(byte.astype(np.uint8).reshape(k // 512, 16, n))


def unpack_weight(words, scales, fmt):
    g, p, n, _ = words.shape
    if fmt == "e4m3":
        vals = np.ascontiguousarray(words).view(ml_dtypes.float8_e4m3fn).astype(np.float64)
    else:
        nib = np.empty((g, p, n, 4), np.uint8)
        nib[..., 0::2] = words & 0xF
        nib[..., 1::2] = words >> 4
        vals = E2M1[nib]
    vals = vals * np.repeat(np.exp2(scales.astype(np.float64) - 127.0), 8, axis=1)[..., None]
    return vals.transpose(0, 1, 3, 2).reshape(g * 512, n)

def pack4(w):
    words, scales = pack_weight(w, "e2m1")
    return words.reshape(words.shape[0], 128, -1), scales


def unpack4(words, scales):
    return unpack_weight(words.reshape(words.shape[0], 128, -1, 2), scales, "e2m1")


B, I, H, AH, AI, G = 512, 1024, 1024, 128, 128, 4
EPS = 1e-5


def sigmoid(v):
    return 1.0 / (1.0 + np.exp(-v))


def ln(v, w, b):
    mu = v.mean(-1, keepdims=True)
    var = ((v - mu) ** 2).mean(-1, keepdims=True)
    return (v - mu) / np.sqrt(var + EPS) * w + b


def setup_inputs():
    n = np.random.standard_normal
    s, t = mx_kscale(I), mx_kscale(H)
    x = bf(n((B, I)) * s)
    hx = bf(n((B, H)) * t)
    cx = bf(n((B, H)))
    zw = bf(1.0 + 0.5 * n((B, 2 * G, AI)))
    zb = bf(0.7 * n((B, 2 * G, AI)))
    w_ih_words, w_ih_scales = pack4((n((G * H, I)) / np.sqrt(I) / s).T)
    w_hh_words, w_hh_scales = pack4((n((G * H, H)) / np.sqrt(H) / t).T)
    return {
        "x": x,
        "hx": hx,
        "cx": cx,
        "zw": zw,
        "zb": zb,
        "w_ih_words": w_ih_words,
        "w_ih_scales": w_ih_scales,
        "w_hh_words": w_hh_words,
        "w_hh_scales": w_hh_scales,
        "b_ih": bf(0.2 * n(G * H)),
        "b_hh": bf(0.2 * n(G * H)),
        "norm_alpha_w": bf(n((2 * G, H, AI)) / np.sqrt(AI)),
        "bias_beta_w": bf(0.7 * n((2 * G, H, AI)) / np.sqrt(AI)),
        "ln_i_w": bf(1.0 + 0.1 * n(G * H)),
        "ln_i_b": bf(0.2 * n(G * H)),
        "ln_h_w": bf(1.0 + 0.1 * n(G * H)),
        "ln_h_b": bf(0.2 * n(G * H)),
        "ln_c_w": bf(1.0 + 0.1 * n(H)),
        "ln_c_b": bf(0.2 * n(H)),
    }


def reference(x, hx, cx, zw, zb, w_ih_words, w_ih_scales, w_hh_words, w_hh_scales, b_ih, b_hh, norm_alpha_w, bias_beta_w, ln_i_w, ln_i_b, ln_h_w, ln_h_b, ln_c_w, ln_c_b):
    alpha = (f64(zw).transpose(1, 0, 2) @ f64(norm_alpha_w).transpose(0, 2, 1)).transpose(1, 0, 2)
    beta = (f64(zb).transpose(1, 0, 2) @ f64(bias_beta_w).transpose(0, 2, 1)).transpose(1, 0, 2)
    xh = (mxq(f64(x), 1, "e4m3") @ unpack4(w_ih_words, w_ih_scales)).reshape(-1, G, H)
    hh = (mxq(f64(hx), 1, "e4m3") @ unpack4(w_hh_words, w_hh_scales)).reshape(-1, G, H)
    in_g = (xh * alpha[:, :G] + f64(b_ih).reshape(G, H) + beta[:, :G]).reshape(-1, G * H)
    hid_g = (hh * alpha[:, G:] + f64(b_hh).reshape(G, H) + beta[:, G:]).reshape(-1, G * H)
    gates = ln(in_g, f64(ln_i_w), f64(ln_i_b)) + ln(hid_g, f64(ln_h_w), f64(ln_h_b))
    i, j, f, o = np.split(gates, G, axis=1)
    cy = ln(sigmoid(f) * f64(cx) + sigmoid(i) * np.tanh(j), f64(ln_c_w), f64(ln_c_b))
    hy = sigmoid(o) * np.tanh(cy)
    return hy, cy

@@ -1,0 +1,466 @@
+from contextlib import ExitStack
+
+import concourse.mybir as mybir
+from concourse.masks import make_identity
+
+F32 = mybir.dt.float32
+BF16 = mybir.dt.bfloat16
+I32 = mybir.dt.int32
+U32 = mybir.dt.uint32
+U8 = mybir.dt.uint8
+FP8X4 = mybir.dt.float8_e4m3fn_x4
+FP4X4 = mybir.dt.float4_e2m1fn_x4
+ALU = mybir.AluOpType
+FUNC = mybir.ActivationFunctionType
+AXIS = mybir.AxisListType
+
+P = 128
+BATCH = 512
+WIDTH = 1024
+GATES = 4
+PATHS = 2
+ROW = GATES * WIDTH
+EMB = 128
+K_PASS = 512
+PASSES = WIDTH // K_PASS
+BANK = 512
+HALVES = WIDTH // BANK
+BLOCKS = WIDTH // P
+BATCH_TILES = BATCH // P
+SLABS = PATHS * GATES
+ALL_SLABS = BATCH_TILES * SLABS
+EPS = 1e-5
+
+FLOPS = 2 * BATCH * WIDTH * ROW * PATHS + 2 * SLABS * 2 * BATCH * EMB * WIDTH
+
+
+def tile_adaptivelstmcell_pb_kernel(
+    tc,
+    x,
+    hx,
+    cx,
+    zw,
+    zb,
+    w_ih_words,
+    w_ih_scales,
+    w_hh_words,
+    w_hh_scales,
+    b_ih,
+    b_hh,
+    norm_alpha_w,
+    bias_beta_w,
+    ln_i_w,
+    ln_i_b,
+    ln_h_w,
+    ln_h_b,
+    ln_c_w,
+    ln_c_b,
+    out_0,
+    out_1,
+):
+    nc = tc.nc
+    path_words = (w_ih_words, w_hh_words)
+    path_scales = (w_ih_scales, w_hh_scales)
+    path_bias = (b_ih, b_hh)
+    path_gain = (ln_i_w, ln_h_w)
+    path_shift = (ln_i_b, ln_h_b)
+
+    with ExitStack() as ctx:
+        const = ctx.enter_context(tc.tile_pool(name="const", bufs=1))
+        raw_pool = ctx.enter_context(tc.tile_pool(name="raw", bufs=8))
+        operand_pool = ctx.enter_context(tc.tile_pool(name="operand", bufs=2))
+        slab_pool = ctx.enter_context(tc.tile_pool(name="slab", bufs=12))
+        alpha_pool = ctx.enter_context(tc.tile_pool(name="alpha", bufs=2))
+        unread_pool = ctx.enter_context(tc.tile_pool(name="unread", bufs=2))
+        stat_pool = ctx.enter_context(tc.tile_pool(name="stat", bufs=2))
+        psum = ctx.enter_context(tc.psum_pool(name="psum", bufs=2))
+        ctx.enter_context(tc.manual_schedule())
+
+        ident_bf16 = const.tile([P, P], BF16, name="ident_bf16")
+        make_identity(nc, ident_bf16[:])
+        ident_f32 = const.tile([P, P], F32, name="ident_f32")
+        make_identity(nc, ident_f32[:])
+        ones = const.tile([P, P], BF16, name="ones")
+        nc.vector.memset(ones[:], 1.0)
+        eps = const.tile([P, 1], F32, name="eps")
+        nc.vector.memset(eps[:], EPS)
+
+        words = []
+        planes = []
+        for path in range(PATHS):
+            words.append(const.tile([P, PASSES, 2 * ROW], U8, name="words%d" % path, align_bytes=64))
+            planes.append(const.tile([P, PASSES, ROW], U8, name="planes%d" % path, align_bytes=64))
+            nc.vector.memset(planes[path][:].bitcast(I32), 0)
+
+        alpha_wT = const.tile([P, SLABS, WIDTH], BF16, name="alpha_wT")
+        beta_wT = const.tile([P, SLABS, WIDTH], BF16, name="beta_wT")
+        bias_rep = const.tile([P, PATHS, ROW], BF16, name="bias_rep")
+        gain_rep = const.tile([P, PATHS, ROW], BF16, name="gain_rep")
+        shift_rep = const.tile([P, ROW], F32, name="shift_rep")
+        cell_gain_rep = const.tile([P, WIDTH], BF16, name="cell_gain_rep")
+        cell_shift_rep = const.tile([P, WIDTH], BF16, name="cell_shift_rep")
+
+        raw = {}
+        operands = {}
+        banks = {}
+        slabs = {}
+        stats = {}
+
+        def load_batch_tile(bt):
+            rows = slice(bt * P, (bt + 1) * P)
+            sources = {
+                "x": x[rows, :],
+                "hx": hx[rows, :],
+                "cx": cx[rows, :],
+                "zw": zw[rows, :, :].rearrange("b s a -> b (s a)"),
+                "zb": zb[rows, :, :].rearrange("b s a -> b (s a)"),
+            }
+            for key in ("x", "hx", "zw", "zb", "cx"):
+                loaded = raw_pool.tile([P, WIDTH], BF16, name="raw_" + key, tag="raw")
+                nc.sync.dma_start(out=loaded[:], in_=sources[key])
+                raw[(bt, key)] = loaded
+
+        def load_scale_planes(path):
+            for g in range(PASSES):
+                for q in range(8):
+                    first = 32 * (q // 4) + q % 4
+                    nc.sync.dma_start(
+                        out=planes[path][first:P:64, g, :].bitcast(I32),
+                        in_=path_scales[path][g, q:16:8, :].bitcast(I32),
+                    )
+
+        def load_slab_weights(s8):
+            path, gate = divmod(s8, GATES)
+            cols = slice(gate * WIDTH, (gate + 1) * WIDTH)
+            byte_cols = slice(2 * gate * WIDTH, 2 * (gate + 1) * WIDTH)
+            for key, source in (("alpha_w", norm_alpha_w), ("beta_w", bias_beta_w)):
+                loaded = raw_pool.tile([P, BLOCKS, EMB], BF16, name="raw_" + key, tag="raw")
+                nc.sync.dma_start(out=loaded[:], in_=source[s8].rearrange("(blk p) a -> p blk a", p=P))
+                raw[(s8, key)] = loaded
+            for g in range(PASSES):
+                nc.sync.dma_start(
+                    out=words[path][:, g, byte_cols].bitcast(I32),
+                    in_=path_words[path][g, :, byte_cols].bitcast(I32),
+                )
+            nc.sync.dma_start(out=bias_rep[:, path, cols], in_=path_bias[path][cols].partition_broadcast(P))
+
+        def load_gains():
+            for gate in range(GATES):
+                cols = slice(gate * WIDTH, (gate + 1) * WIDTH)
+                for path in range(PATHS):
+                    nc.sync.dma_start(
+                        out=gain_rep[:, path, cols], in_=path_gain[path][cols].partition_broadcast(P)
+                    )
+            nc.sync.dma_start(out=cell_gain_rep[:], in_=ln_c_w.partition_broadcast(P))
+            nc.sync.dma_start(out=cell_shift_rep[:], in_=ln_c_b.partition_broadcast(P))
+
+        def load_shifts(gate):
+            cols = slice(gate * WIDTH, (gate + 1) * WIDTH)
+            for path in range(PATHS):
+                loaded = raw_pool.tile([P, WIDTH], BF16, name="raw_shift", tag="raw")
+                nc.sync.dma_start(out=loaded[:], in_=path_shift[path][cols].partition_broadcast(P))
+                raw[(gate, "shift%d" % path)] = loaded
+
+        def add_shifts(gate):
+            cols = slice(gate * WIDTH, (gate + 1) * WIDTH)
+            nc.vector.tensor_tensor(
+                out=shift_rep[:, cols], in0=raw[(gate, "shift0")][:], in1=raw[(gate, "shift1")][:], op=ALU.add
+            )
+
+        def prepare_batch_tile(bt):
+            grouped = []
+            for key in ("x", "hx"):
+                pairs = raw[(bt, key)][:].bitcast(F32)
+                turned = psum.tile([P, PASSES, 2, P], F32, name="turned_" + key, tag="turn")
+                for g in range(PASSES):
+                    for u in range(2):
+                        nc.tensor.transpose(
+                            out=turned[:, g, u, :],
+                            in_=pairs[:, (K_PASS // 2) * g + u : (K_PASS // 2) * (g + 1) : 2],
+                            identity=ident_f32[:],
+                        )
+                side_by_side = operand_pool.tile(
+                    [P, PASSES * P * 4], BF16, name="side_by_side_" + key, tag="side_by_side", align_bytes=64
+                )
+                nc.scalar.copy(
+                    out=side_by_side[:].bitcast(F32).rearrange("p (g b u) -> p g b u", g=PASSES, u=2),
+                    in_=turned[:].rearrange("p g u b -> p g b u"),
+                )
+                grouped.append(side_by_side)
+            for key in ("zw", "zb"):
+                turned = psum.tile([P, SLABS, P], BF16, name="turned_" + key, tag="turn")
+                for s8 in range(SLABS):
+                    nc.tensor.transpose(
+                        out=turned[:, s8, :], in_=raw[(bt, key)][:, s8 * EMB : (s8 + 1) * EMB], identity=ident_bf16[:]
+                    )
+                embT = operand_pool.tile([P, SLABS, P], BF16, name=key + "T")
+                nc.scalar.copy(out=embT[:], in_=turned[:])
+                operands[(bt, key)] = embT
+            for path in range(PATHS):
+                codes = operand_pool.tile([P, PASSES * P], U32, name="codes%d" % path, align_bytes=64)
+                code_scales = operand_pool.tile([P, PASSES * P], U8, name="code_scales%d" % path, align_bytes=64)
+                nc.vector.quantize_mx(out=codes[:].bitcast(FP8X4), scales=code_scales[:], in_=grouped[path][:])
+                operands[(bt, "codes%d" % path)] = codes
+                operands[(bt, "code_scales%d" % path)] = code_scales
+
+        def turn_hyper_weights(s8):
+            turned_alpha = psum.tile([P, BLOCKS, P], BF16, name="turned_alpha_w", tag="turn")
+            for blk in range(BLOCKS):
+                nc.tensor.transpose(out=turned_alpha[:, blk, :], in_=raw[(s8, "alpha_w")][:, blk, :], identity=ident_bf16[:])
+            nc.vector.tensor_copy(out=alpha_wT[:, s8, :], in_=turned_alpha[:].rearrange("a blk p -> a (blk p)"))
+            turned_beta = psum.tile([P, BLOCKS, P], BF16, name="turned_beta_w", tag="turn")
+            for blk in range(BLOCKS):
+                nc.tensor.transpose(out=turned_beta[:, blk, :], in_=raw[(s8, "beta_w")][:, blk, :], identity=ident_bf16[:])
+            nc.scalar.copy(out=beta_wT[:, s8, :], in_=turned_beta[:].rearrange("a blk p -> a (blk p)"))
+
+        def slab_matmuls(n):
+            bt, s8 = divmod(n, SLABS)
+            path, gate = divmod(s8, GATES)
+            alpha_banks, xh_banks, beta_banks = [], [], []
+            for half in range(HALVES):
+                bank = psum.tile([P, BANK], F32, name="alpha_bank", tag="alpha")
+                nc.tensor.matmul(
+                    bank[:],
+                    lhsT=operands[(bt, "zw")][:, s8, :],
+                    rhs=alpha_wT[:, s8, half * BANK : (half + 1) * BANK],
+                    start=True,
+                    stop=True,
+                )
+                alpha_banks.append(bank)
+            for half in range(HALVES):
+                first = gate * WIDTH + half * BANK
+                bank = psum.tile([P, BANK], F32, name="xh_bank", tag="xh")
+                for g in range(PASSES):
+                    nc.tensor.matmul_mx(
+                        out=bank[:],
+                        lhsT=operands[(bt, "codes%d" % path)][:, g * P : (g + 1) * P].bitcast(FP8X4),
+                        lhsT_scale=operands[(bt, "code_scales%d" % path)][:, g * P : (g + 1) * P],
+                        rhs=words[path][:, g, 2 * first : 2 * (first + BANK)].bitcast(FP4X4),
+                        rhs_scale=planes[path][:, g, first : first + BANK],
+                        start=(g == 0),
+                        stop=(g == PASSES - 1),
+                    )
+                xh_banks.append(bank)
+            for half in range(HALVES):
+                bank = psum.tile([P, BANK], F32, name="beta_bank", tag="beta")
+                nc.tensor.matmul(
+                    bank[:],
+                    lhsT=operands[(bt, "zb")][:, s8, :],
+                    rhs=beta_wT[:, s8, half * BANK : (half + 1) * BANK],
+                    start=True,
+                    stop=True,
+                )
+                beta_banks.append(bank)
+            alpha_sb = alpha_pool.tile([P, HALVES, BANK], F32, name="alpha_sb")
+            for half in range(HALVES):
+                nc.scalar.copy(out=alpha_sb[:, half, :], in_=alpha_banks[half][:])
+            banks[n] = (alpha_sb, xh_banks, beta_banks)
+
+        def slab_combine(n):
+            bt, s8 = divmod(n, SLABS)
+            path, gate = divmod(s8, GATES)
+            if s8 == 0:
+                stats[(bt, "sum_parts")] = stat_pool.tile([P, PATHS, GATES * HALVES], F32, name="sum_parts")
+                stats[(bt, "square_parts")] = stat_pool.tile([P, PATHS, GATES], F32, name="square_parts")
+            alpha_sb, xh_banks, beta_banks = banks[n]
+            pre = slab_pool.tile([P, WIDTH], F32, name="pre", tag="slab")
+            for half in range(HALVES):
+                nc.vector.tensor_tensor(
+                    out=pre[:, half * BANK : (half + 1) * BANK], in0=xh_banks[half][:], in1=alpha_sb[:, half, :], op=ALU.mult
+                )
+            for half in range(HALVES):
+                part = gate * HALVES + half
+                nc.vector.scalar_tensor_tensor(
+                    out=pre[:, half * BANK : (half + 1) * BANK],
+                    in0=pre[:, half * BANK : (half + 1) * BANK],
+                    scalar=1.0,
+                    in1=beta_banks[half][:],
+                    op0=ALU.mult,
+                    op1=ALU.add,
+                    accum_out=stats[(bt, "sum_parts")][:, path, part : part + 1],
+                )
+            nc.gpsimd.tensor_tensor(
+                out=pre[:], in0=pre[:], in1=bias_rep[:, path, gate * WIDTH : (gate + 1) * WIDTH], op=ALU.add
+            )
+            slabs[(bt, s8)] = pre
+
+        def slab_squares(n):
+            bt, s8 = divmod(n, SLABS)
+            path, gate = divmod(s8, GATES)
+            unread = unread_pool.tile([P, WIDTH], BF16, name="unread")
+            nc.scalar.activation(
+                out=unread[:],
+                in_=slabs[(bt, s8)][:],
+                func=FUNC.Square,
+                accum_out=stats[(bt, "square_parts")][:, path, gate : gate + 1],
+            )
+
+        def small(bt, name, width):
+            stats[(bt, name)] = stat_pool.tile([P, width], F32, name=name)
+            return stats[(bt, name)]
+
+        def row_statistics(bt):
+            sums = small(bt, "sums", PATHS)
+            nc.vector.tensor_reduce(out=sums[:], in_=stats[(bt, "sum_parts")][:], axis=AXIS.X, op=ALU.add)
+            squares = small(bt, "squares", PATHS)
+            nc.vector.tensor_reduce(out=squares[:], in_=stats[(bt, "square_parts")][:], axis=AXIS.X, op=ALU.add)
+            mean = small(bt, "mean", PATHS)
+            nc.vector.scalar_tensor_tensor(
+                out=mean[:], in0=sums[:], scalar=1.0 / ROW, in1=bias_mean[:], op0=ALU.mult, op1=ALU.add
+            )
+            mean_squared = small(bt, "mean_squared", PATHS)
+            nc.vector.tensor_tensor(out=mean_squared[:], in0=mean[:], in1=mean[:], op=ALU.mult)
+            variance = small(bt, "variance", PATHS)
+            nc.vector.scalar_tensor_tensor(
+                out=variance[:], in0=squares[:], scalar=1.0 / ROW, in1=mean_squared[:], op0=ALU.mult, op1=ALU.subtract
+            )
+            deviation = small(bt, "deviation", PATHS)
+            nc.scalar.activation(out=deviation[:], in_=variance[:], func=FUNC.Sqrt, bias=eps[:], scale=1.0)
+
+        def row_inverse_deviation(bt):
+            nc.vector.reciprocal(out=small(bt, "inverse", PATHS)[:], in_=stats[(bt, "deviation")][:])
+
+        def gate_values(bt, gate):
+            cols = slice(gate * WIDTH, (gate + 1) * WIDTH)
+            pre_in = slabs[(bt, gate)]
+            pre_hid = slabs[(bt, GATES + gate)]
+            mean = stats[(bt, "mean")]
+            inverse = stats[(bt, "inverse")]
+            nc.vector.scalar_tensor_tensor(
+                out=pre_hid[:], in0=pre_hid[:], scalar=mean[:, 1:2], in1=gain_rep[:, 1, cols], op0=ALU.subtract, op1=ALU.mult
+            )
+            nc.vector.scalar_tensor_tensor(
+                out=pre_in[:], in0=pre_in[:], scalar=mean[:, 0:1], in1=gain_rep[:, 0, cols], op0=ALU.subtract, op1=ALU.mult
+            )
+            nc.vector.scalar_tensor_tensor(
+                out=pre_hid[:], in0=pre_hid[:], scalar=inverse[:, 1:2], in1=shift_rep[:, cols], op0=ALU.mult, op1=ALU.add
+            )
+            nc.vector.scalar_tensor_tensor(
+                out=pre_in[:], in0=pre_in[:], scalar=inverse[:, 0:1], in1=pre_hid[:], op0=ALU.mult, op1=ALU.add
+            )
+            nc.scalar.activation(out=pre_in[:], in_=pre_in[:], func=(FUNC.Tanh if gate == 1 else FUNC.Sigmoid))
+
+        def cell_sum(bt):
+            gate_i, gate_j, gate_f = slabs[(bt, 0)], slabs[(bt, 1)], slabs[(bt, 2)]
+            nc.vector.tensor_tensor(out=gate_i[:], in0=gate_i[:], in1=gate_j[:], op=ALU.mult)
+            nc.vector.tensor_tensor(out=gate_f[:], in0=gate_f[:], in1=raw[(bt, "cx")][:], op=ALU.mult)
+            nc.vector.scalar_tensor_tensor(
+                out=gate_i[:],
+                in0=gate_i[:],
+                scalar=1.0,
+                in1=gate_f[:],
+                op0=ALU.mult,
+                op1=ALU.add,
+                accum_out=small(bt, "cell_sum", 1)[:],
+            )
+            unread = unread_pool.tile([P, WIDTH], BF16, name="unread")
+            nc.scalar.activation(out=unread[:], in_=gate_i[:], func=FUNC.Square, accum_out=small(bt, "cell_squares", 1)[:])
+
+        def cell_statistics(bt):
+            mean = small(bt, "cell_mean", 1)
+            nc.vector.tensor_scalar(out=mean[:], in0=stats[(bt, "cell_sum")][:], scalar1=1.0 / WIDTH, scalar2=None, op0=ALU.mult)
+            mean_squared = small(bt, "cell_mean_squared", 1)
+            nc.vector.tensor_tensor(out=mean_squared[:], in0=mean[:], in1=mean[:], op=ALU.mult)
+            variance = small(bt, "cell_variance", 1)
+            nc.vector.scalar_tensor_tensor(
+                out=variance[:],
+                in0=stats[(bt, "cell_squares")][:],
+                scalar=1.0 / WIDTH,
+                in1=mean_squared[:],
+                op0=ALU.mult,
+                op1=ALU.subtract,
+            )
+            nc.scalar.activation(
+                out=small(bt, "cell_deviation", 1)[:], in_=variance[:], func=FUNC.Sqrt, bias=eps[:], scale=1.0
+            )
+
+        def cell_norm(bt):
+            rows = slice(bt * P, (bt + 1) * P)
+            cell = slabs[(bt, 0)]
+            inverse = small(bt, "cell_inverse", 1)
+            nc.vector.reciprocal(out=inverse[:], in_=stats[(bt, "cell_deviation")][:])
+            nc.vector.scalar_tensor_tensor(
+                out=cell[:], in0=cell[:], scalar=stats[(bt, "cell_mean")][:], in1=cell_gain_rep[:], op0=ALU.subtract, op1=ALU.mult
+            )
+            nc.vector.scalar_tensor_tensor(
+                out=cell[:], in0=cell[:], scalar=inverse[:], in1=cell_shift_rep[:], op0=ALU.mult, op1=ALU.add
+            )
+            nc.sync.dma_start(out=out_1[rows, :], in_=cell[:])
+            tanh_cy = slab_pool.tile([P, WIDTH], F32, name="tanh_cy", tag="slab")
+            nc.scalar.activation(out=tanh_cy[:], in_=cell[:], func=FUNC.Tanh)
+            slabs[(bt, "tanh_cy")] = tanh_cy
+
+        def hidden_state(bt):
+            rows = slice(bt * P, (bt + 1) * P)
+            gate_o = slabs[(bt, 3)]
+            nc.vector.tensor_tensor(out=gate_o[:], in0=gate_o[:], in1=slabs[(bt, "tanh_cy")][:], op=ALU.mult)
+            nc.sync.dma_start(out=out_0[rows, :], in_=gate_o[:])
+
+        load_batch_tile(0)
+        bias_rows = const.tile([P, PATHS, ROW // P], BF16, name="bias_rows")
+        for path in range(PATHS):
+            nc.sync.dma_start(out=bias_rows[:, path, :], in_=path_bias[path].rearrange("(k j) -> k j", k=P))
+        load_scale_planes(0)
+        load_slab_weights(0)
+        prepare_batch_tile(0)
+        bias_columns = psum.tile([P, PATHS, ROW // P], F32, name="bias_columns", tag="turn")
+        nc.tensor.matmul(
+            bias_columns[:].rearrange("p u j -> p (u j)"),
+            lhsT=ones[:],
+            rhs=bias_rows[:].rearrange("p u j -> p (u j)"),
+            start=True,
+            stop=True,
+        )
+        bias_total = const.tile([P, PATHS], F32, name="bias_total")
+        nc.vector.tensor_reduce(out=bias_total[:], in_=bias_columns[:], axis=AXIS.X, op=ALU.add)
+        bias_mean = const.tile([P, PATHS], F32, name="bias_mean")
+        nc.vector.tensor_scalar(out=bias_mean[:], in0=bias_total[:], scalar1=1.0 / ROW, scalar2=None, op0=ALU.mult)
+        load_slab_weights(1)
+        turn_hyper_weights(0)
+        load_slab_weights(2)
+        turn_hyper_weights(1)
+        slab_matmuls(0)
+
+        for n in range(ALL_SLABS + SLABS):
+            bt, k = divmod(n, SLABS)
+            tail = bt - 1
+            if n < ALL_SLABS:
+                slab_combine(n)
+            if n + 1 < ALL_SLABS:
+                slab_matmuls(n + 1)
+            if 1 <= n <= ALL_SLABS:
+                slab_squares(n - 1)
+
+            if n == 0:
+                load_scale_planes(1)
+            if n + 3 < SLABS:
+                load_slab_weights(n + 3)
+            if n + 2 < SLABS:
+                turn_hyper_weights(n + 2)
+            if n == SLABS - 3:
+                load_gains()
+            if bt == 1 and k < GATES:
+                load_shifts(k)
+            if bt == 1 and 1 <= k <= GATES:
+                add_shifts(k - 1)
+
+            if k == 4 and bt + 1 < BATCH_TILES:
+                load_batch_tile(bt + 1)
+            if k == 6 and bt + 1 < BATCH_TILES:
+                prepare_batch_tile(bt + 1)
+
+            if tail >= 0:
+                if k == 1:
+                    row_statistics(tail)
+                if k == 2:
+                    row_inverse_deviation(tail)
+                if 2 <= k <= 4:
+                    gate_values(tail, k - 2)
+                if k == 5:
+                    cell_sum(tail)
+                    gate_values(tail, 3)
+                    cell_statistics(tail)
+                if k == 6:
+                    cell_norm(tail)
+                if k == 7:
+                    hidden_state(tail)

@@ -279,7 +279,7 @@ def tile_adaptivelstmcell_pb_kernel(
                     op1=ALU.add,
                     accum_out=stats[(bt, "sum_parts")][:, path, part : part + 1],
                 )
-            nc.gpsimd.tensor_tensor(
+            nc.vector.tensor_tensor(
                 out=pre[:], in0=pre[:], in1=bias_rep[:, path, gate * WIDTH : (gate + 1) * WIDTH], op=ALU.add
             )
             slabs[(bt, s8)] = pre

@@ -59,11 +59,10 @@ def tile_adaptivelstmcell_pb_kernel(
     out_1,
 ):
     nc = tc.nc
-    path_words = (w_ih_words, w_hh_words)
-    path_scales = (w_ih_scales, w_hh_scales)
-    path_bias = (b_ih, b_hh)
-    path_gain = (ln_i_w, ln_h_w)
-    path_shift = (ln_i_b, ln_h_b)
+    path_words = (w_hh_words, w_ih_words)
+    path_scales = (w_hh_scales, w_ih_scales)
+    path_gain = (ln_h_w, ln_i_w)
+    path_shift = (ln_h_b, ln_i_b)
 
     with ExitStack() as ctx:
         const = ctx.enter_context(tc.tile_pool(name="const", bufs=1))
@@ -94,11 +93,13 @@ def tile_adaptivelstmcell_pb_kernel(
 
         alpha_wT = const.tile([P, SLABS, WIDTH], BF16, name="alpha_wT")
         beta_wT = const.tile([P, SLABS, WIDTH], BF16, name="beta_wT")
-        bias_rep = const.tile([P, PATHS, ROW], BF16, name="bias_rep")
+        hidden_bias_rep = const.tile([P, ROW], BF16, name="hidden_bias_rep")
         gain_rep = const.tile([P, PATHS, ROW], BF16, name="gain_rep")
         shift_rep = const.tile([P, ROW], F32, name="shift_rep")
         cell_gain_rep = const.tile([P, WIDTH], BF16, name="cell_gain_rep")
         cell_shift_rep = const.tile([P, WIDTH], BF16, name="cell_shift_rep")
+        input_bias_row = const.tile([P, ROW], BF16, name="input_bias_row")
+        nc.gpsimd.memset(input_bias_row[:], 0.0)
 
         raw = {}
         operands = {}
@@ -115,7 +116,7 @@ def tile_adaptivelstmcell_pb_kernel(
                 "zw": zw[rows, :, :].rearrange("b s a -> b (s a)"),
                 "zb": zb[rows, :, :].rearrange("b s a -> b (s a)"),
             }
-            for key in ("x", "hx", "zw", "zb", "cx"):
+            for key in ("hx", "x", "zw", "zb", "cx"):
                 loaded = raw_pool.tile([P, WIDTH], BF16, name="raw_" + key, tag="raw")
                 nc.sync.dma_start(out=loaded[:], in_=sources[key])
                 raw[(bt, key)] = loaded
@@ -129,20 +130,23 @@ def tile_adaptivelstmcell_pb_kernel(
                         in_=path_scales[path][g, q:16:8, :].bitcast(I32),
                     )
 
-        def load_slab_weights(s8):
-            path, gate = divmod(s8, GATES)
+        def load_slab_weights(slot):
+            path, gate = divmod(slot, GATES)
             cols = slice(gate * WIDTH, (gate + 1) * WIDTH)
             byte_cols = slice(2 * gate * WIDTH, 2 * (gate + 1) * WIDTH)
             for key, source in (("alpha_w", norm_alpha_w), ("beta_w", bias_beta_w)):
                 loaded = raw_pool.tile([P, BLOCKS, EMB], BF16, name="raw_" + key, tag="raw")
-                nc.sync.dma_start(out=loaded[:], in_=source[s8].rearrange("(blk p) a -> p blk a", p=P))
-                raw[(s8, key)] = loaded
+                nc.sync.dma_start(
+                    out=loaded[:], in_=source[(slot + GATES) % SLABS].rearrange("(blk p) a -> p blk a", p=P)
+                )
+                raw[(slot, key)] = loaded
             for g in range(PASSES):
                 nc.sync.dma_start(
                     out=words[path][:, g, byte_cols].bitcast(I32),
                     in_=path_words[path][g, :, byte_cols].bitcast(I32),
                 )
-            nc.sync.dma_start(out=bias_rep[:, path, cols], in_=path_bias[path][cols].partition_broadcast(P))
+            if path == 0:
+                nc.sync.dma_start(out=hidden_bias_rep[:, cols], in_=b_hh[cols].partition_broadcast(P))
 
         def load_gains():
             for gate in range(GATES):
@@ -169,7 +173,7 @@ def tile_adaptivelstmcell_pb_kernel(
 
         def prepare_batch_tile(bt):
             grouped = []
-            for key in ("x", "hx"):
+            for key in ("hx", "x"):
                 pairs = raw[(bt, key)][:].bitcast(F32)
                 turned = psum.tile([P, PASSES, 2, P], F32, name="turned_" + key, tag="turn")
                 for g in range(PASSES):
@@ -189,9 +193,10 @@ def tile_adaptivelstmcell_pb_kernel(
                 grouped.append(side_by_side)
             for key in ("zw", "zb"):
                 turned = psum.tile([P, SLABS, P], BF16, name="turned_" + key, tag="turn")
-                for s8 in range(SLABS):
+                for slot in range(SLABS):
+                    emb = (slot + GATES) % SLABS
                     nc.tensor.transpose(
-                        out=turned[:, s8, :], in_=raw[(bt, key)][:, s8 * EMB : (s8 + 1) * EMB], identity=ident_bf16[:]
+                        out=turned[:, slot, :], in_=raw[(bt, key)][:, emb * EMB : (emb + 1) * EMB], identity=ident_bf16[:]
                     )
                 embT = operand_pool.tile([P, SLABS, P], BF16, name=key + "T")
                 nc.scalar.copy(out=embT[:], in_=turned[:])
@@ -203,26 +208,26 @@ def tile_adaptivelstmcell_pb_kernel(
                 operands[(bt, "codes%d" % path)] = codes
                 operands[(bt, "code_scales%d" % path)] = code_scales
 
-        def turn_hyper_weights(s8):
+        def turn_hyper_weights(slot):
             turned_alpha = psum.tile([P, BLOCKS, P], BF16, name="turned_alpha_w", tag="turn")
             for blk in range(BLOCKS):
-                nc.tensor.transpose(out=turned_alpha[:, blk, :], in_=raw[(s8, "alpha_w")][:, blk, :], identity=ident_bf16[:])
-            nc.vector.tensor_copy(out=alpha_wT[:, s8, :], in_=turned_alpha[:].rearrange("a blk p -> a (blk p)"))
+                nc.tensor.transpose(out=turned_alpha[:, blk, :], in_=raw[(slot, "alpha_w")][:, blk, :], identity=ident_bf16[:])
+            nc.vector.tensor_copy(out=alpha_wT[:, slot, :], in_=turned_alpha[:].rearrange("a blk p -> a (blk p)"))
             turned_beta = psum.tile([P, BLOCKS, P], BF16, name="turned_beta_w", tag="turn")
             for blk in range(BLOCKS):
-                nc.tensor.transpose(out=turned_beta[:, blk, :], in_=raw[(s8, "beta_w")][:, blk, :], identity=ident_bf16[:])
-            nc.scalar.copy(out=beta_wT[:, s8, :], in_=turned_beta[:].rearrange("a blk p -> a (blk p)"))
+                nc.tensor.transpose(out=turned_beta[:, blk, :], in_=raw[(slot, "beta_w")][:, blk, :], identity=ident_bf16[:])
+            nc.scalar.copy(out=beta_wT[:, slot, :], in_=turned_beta[:].rearrange("a blk p -> a (blk p)"))
 
         def slab_matmuls(n):
-            bt, s8 = divmod(n, SLABS)
-            path, gate = divmod(s8, GATES)
+            bt, slot = divmod(n, SLABS)
+            path, gate = divmod(slot, GATES)
             alpha_banks, xh_banks, beta_banks = [], [], []
             for half in range(HALVES):
                 bank = psum.tile([P, BANK], F32, name="alpha_bank", tag="alpha")
                 nc.tensor.matmul(
                     bank[:],
-                    lhsT=operands[(bt, "zw")][:, s8, :],
-                    rhs=alpha_wT[:, s8, half * BANK : (half + 1) * BANK],
+                    lhsT=operands[(bt, "zw")][:, slot, :],
+                    rhs=alpha_wT[:, slot, half * BANK : (half + 1) * BANK],
                     start=True,
                     stop=True,
                 )
@@ -245,11 +250,16 @@ def tile_adaptivelstmcell_pb_kernel(
                 bank = psum.tile([P, BANK], F32, name="beta_bank", tag="beta")
                 nc.tensor.matmul(
                     bank[:],
-                    lhsT=operands[(bt, "zb")][:, s8, :],
-                    rhs=beta_wT[:, s8, half * BANK : (half + 1) * BANK],
+                    lhsT=operands[(bt, "zb")][:, slot, :],
+                    rhs=beta_wT[:, slot, half * BANK : (half + 1) * BANK],
                     start=True,
-                    stop=True,
+                    stop=(path == 0),
                 )
+                if path == 1:
+                    first = gate * WIDTH + half * BANK
+                    nc.tensor.matmul(
+                        bank[:], lhsT=ones[:], rhs=input_bias_row[:, first : first + BANK], start=False, stop=True
+                    )
                 beta_banks.append(bank)
             alpha_sb = alpha_pool.tile([P, HALVES, BANK], F32, name="alpha_sb")
             for half in range(HALVES):
@@ -257,10 +267,11 @@ def tile_adaptivelstmcell_pb_kernel(
             banks[n] = (alpha_sb, xh_banks, beta_banks)
 
         def slab_combine(n):
-            bt, s8 = divmod(n, SLABS)
-            path, gate = divmod(s8, GATES)
-            if s8 == 0:
-                stats[(bt, "sum_parts")] = stat_pool.tile([P, PATHS, GATES * HALVES], F32, name="sum_parts")
+            bt, slot = divmod(n, SLABS)
+            path, gate = divmod(slot, GATES)
+            if slot == 0:
+                stats[(bt, "sum_parts0")] = stat_pool.tile([P, GATES], F32, name="sum_parts0")
+                stats[(bt, "sum_parts1")] = stat_pool.tile([P, GATES * HALVES], F32, name="sum_parts1")
                 stats[(bt, "square_parts")] = stat_pool.tile([P, PATHS, GATES], F32, name="square_parts")
             alpha_sb, xh_banks, beta_banks = banks[n]
             pre = slab_pool.tile([P, WIDTH], F32, name="pre", tag="slab")
@@ -269,28 +280,39 @@ def tile_adaptivelstmcell_pb_kernel(
                     out=pre[:, half * BANK : (half + 1) * BANK], in0=xh_banks[half][:], in1=alpha_sb[:, half, :], op=ALU.mult
                 )
             for half in range(HALVES):
-                part = gate * HALVES + half
+                half_cols = slice(half * BANK, (half + 1) * BANK)
+                if path == 1:
+                    part = gate * HALVES + half
+                    nc.vector.scalar_tensor_tensor(
+                        out=pre[:, half_cols],
+                        in0=pre[:, half_cols],
+                        scalar=1.0,
+                        in1=beta_banks[half][:],
+                        op0=ALU.mult,
+                        op1=ALU.add,
+                        accum_out=stats[(bt, "sum_parts1")][:, part : part + 1],
+                    )
+                else:
+                    nc.vector.tensor_tensor(out=pre[:, half_cols], in0=pre[:, half_cols], in1=beta_banks[half][:], op=ALU.add)
+            if path == 0:
                 nc.vector.scalar_tensor_tensor(
-                    out=pre[:, half * BANK : (half + 1) * BANK],
-                    in0=pre[:, half * BANK : (half + 1) * BANK],
+                    out=pre[:],
+                    in0=pre[:],
                     scalar=1.0,
-                    in1=beta_banks[half][:],
+                    in1=hidden_bias_rep[:, gate * WIDTH : (gate + 1) * WIDTH],
                     op0=ALU.mult,
                     op1=ALU.add,
-                    accum_out=stats[(bt, "sum_parts")][:, path, part : part + 1],
+                    accum_out=stats[(bt, "sum_parts0")][:, gate : gate + 1],
                 )
-            nc.vector.tensor_tensor(
-                out=pre[:], in0=pre[:], in1=bias_rep[:, path, gate * WIDTH : (gate + 1) * WIDTH], op=ALU.add
-            )
-            slabs[(bt, s8)] = pre
+            slabs[(bt, slot)] = pre
 
         def slab_squares(n):
-            bt, s8 = divmod(n, SLABS)
-            path, gate = divmod(s8, GATES)
+            bt, slot = divmod(n, SLABS)
+            path, gate = divmod(slot, GATES)
             unread = unread_pool.tile([P, WIDTH], BF16, name="unread")
             nc.scalar.activation(
                 out=unread[:],
-                in_=slabs[(bt, s8)][:],
+                in_=slabs[(bt, slot)][:],
                 func=FUNC.Square,
                 accum_out=stats[(bt, "square_parts")][:, path, gate : gate + 1],
             )
@@ -299,84 +321,115 @@ def tile_adaptivelstmcell_pb_kernel(
             stats[(bt, name)] = stat_pool.tile([P, width], F32, name=name)
             return stats[(bt, name)]
 
-        def row_statistics(bt):
-            sums = small(bt, "sums", PATHS)
-            nc.vector.tensor_reduce(out=sums[:], in_=stats[(bt, "sum_parts")][:], axis=AXIS.X, op=ALU.add)
-            squares = small(bt, "squares", PATHS)
-            nc.vector.tensor_reduce(out=squares[:], in_=stats[(bt, "square_parts")][:], axis=AXIS.X, op=ALU.add)
+        def row_means(bt):
             mean = small(bt, "mean", PATHS)
-            nc.vector.scalar_tensor_tensor(
-                out=mean[:], in0=sums[:], scalar=1.0 / ROW, in1=bias_mean[:], op0=ALU.mult, op1=ALU.add
-            )
-            mean_squared = small(bt, "mean_squared", PATHS)
-            nc.vector.tensor_tensor(out=mean_squared[:], in0=mean[:], in1=mean[:], op=ALU.mult)
-            variance = small(bt, "variance", PATHS)
-            nc.vector.scalar_tensor_tensor(
-                out=variance[:], in0=squares[:], scalar=1.0 / ROW, in1=mean_squared[:], op0=ALU.mult, op1=ALU.subtract
-            )
-            deviation = small(bt, "deviation", PATHS)
-            nc.scalar.activation(out=deviation[:], in_=variance[:], func=FUNC.Sqrt, bias=eps[:], scale=1.0)
+            for path in range(PATHS):
+                parts = stats[(bt, "sum_parts%d" % path)]
+                nc.scalar.activation(
+                    out=small(bt, "scaled_sums%d" % path, parts.shape[1])[:],
+                    in_=parts[:],
+                    func=FUNC.Identity,
+                    scale=1.0 / ROW,
+                    accum_out=mean[:, path : path + 1],
+                )
 
-        def row_inverse_deviation(bt):
+        def row_deviations(bt):
+            mean_squared = small(bt, "mean_squared", PATHS)
+            nc.scalar.activation(out=mean_squared[:], in_=stats[(bt, "mean")][:], func=FUNC.Square)
+            eps_less_mean_squared = small(bt, "eps_less_mean_squared", PATHS)
+            nc.scalar.activation(
+                out=eps_less_mean_squared[:], in_=mean_squared[:], func=FUNC.Identity, scale=-1.0, bias=eps[:]
+            )
+            mean_of_squares = small(bt, "mean_of_squares", PATHS)
+            deviation = small(bt, "deviation", PATHS)
+            for path in range(PATHS):
+                one = slice(path, path + 1)
+                nc.scalar.activation(
+                    out=small(bt, "scaled_squares%d" % path, GATES)[:],
+                    in_=stats[(bt, "square_parts")][:, path, :],
+                    func=FUNC.Identity,
+                    scale=1.0 / ROW,
+                    accum_out=mean_of_squares[:, one],
+                )
+            for path in range(PATHS):
+                one = slice(path, path + 1)
+                nc.scalar.activation(
+                    out=deviation[:, one], in_=mean_of_squares[:, one], func=FUNC.Sqrt, bias=eps_less_mean_squared[:, one]
+                )
+
+        def row_inverse_deviations(bt):
             nc.vector.reciprocal(out=small(bt, "inverse", PATHS)[:], in_=stats[(bt, "deviation")][:])
 
-        def gate_values(bt, gate):
-            cols = slice(gate * WIDTH, (gate + 1) * WIDTH)
-            pre_in = slabs[(bt, gate)]
-            pre_hid = slabs[(bt, GATES + gate)]
+        def center_and_gain(bt, pair):
             mean = stats[(bt, "mean")]
+            for gate in (2 * pair, 2 * pair + 1):
+                cols = slice(gate * WIDTH, (gate + 1) * WIDTH)
+                for path in range(PATHS):
+                    pre = slabs[(bt, path * GATES + gate)]
+                    nc.vector.scalar_tensor_tensor(
+                        out=pre[:],
+                        in0=pre[:],
+                        scalar=mean[:, path : path + 1],
+                        in1=gain_rep[:, path, cols],
+                        op0=ALU.subtract,
+                        op1=ALU.mult,
+                    )
+
+        def scale_and_add(bt, pair):
             inverse = stats[(bt, "inverse")]
-            nc.vector.scalar_tensor_tensor(
-                out=pre_hid[:], in0=pre_hid[:], scalar=mean[:, 1:2], in1=gain_rep[:, 1, cols], op0=ALU.subtract, op1=ALU.mult
-            )
-            nc.vector.scalar_tensor_tensor(
-                out=pre_in[:], in0=pre_in[:], scalar=mean[:, 0:1], in1=gain_rep[:, 0, cols], op0=ALU.subtract, op1=ALU.mult
-            )
-            nc.vector.scalar_tensor_tensor(
-                out=pre_hid[:], in0=pre_hid[:], scalar=inverse[:, 1:2], in1=shift_rep[:, cols], op0=ALU.mult, op1=ALU.add
-            )
-            nc.vector.scalar_tensor_tensor(
-                out=pre_in[:], in0=pre_in[:], scalar=inverse[:, 0:1], in1=pre_hid[:], op0=ALU.mult, op1=ALU.add
-            )
-            nc.scalar.activation(out=pre_in[:], in_=pre_in[:], func=(FUNC.Tanh if gate == 1 else FUNC.Sigmoid))
+            gates = (2 * pair, 2 * pair + 1)
+            for gate in gates:
+                pre_hid = slabs[(bt, gate)]
+                nc.vector.scalar_tensor_tensor(
+                    out=pre_hid[:],
+                    in0=pre_hid[:],
+                    scalar=inverse[:, 0:1],
+                    in1=shift_rep[:, gate * WIDTH : (gate + 1) * WIDTH],
+                    op0=ALU.mult,
+                    op1=ALU.add,
+                )
+            for gate in gates:
+                pre_in = slabs[(bt, GATES + gate)]
+                nc.vector.scalar_tensor_tensor(
+                    out=pre_in[:],
+                    in0=pre_in[:],
+                    scalar=inverse[:, 1:2],
+                    in1=slabs[(bt, gate)][:],
+                    op0=ALU.mult,
+                    op1=ALU.add,
+                )
+                nc.scalar.activation(out=pre_in[:], in_=pre_in[:], func=(FUNC.Tanh if gate == 1 else FUNC.Sigmoid))
 
         def cell_sum(bt):
-            gate_i, gate_j, gate_f = slabs[(bt, 0)], slabs[(bt, 1)], slabs[(bt, 2)]
+            gate_i, gate_j, gate_f = slabs[(bt, GATES)], slabs[(bt, GATES + 1)], slabs[(bt, GATES + 2)]
             nc.vector.tensor_tensor(out=gate_i[:], in0=gate_i[:], in1=gate_j[:], op=ALU.mult)
             nc.vector.tensor_tensor(out=gate_f[:], in0=gate_f[:], in1=raw[(bt, "cx")][:], op=ALU.mult)
+            total = small(bt, "cell_total", 1)
             nc.vector.scalar_tensor_tensor(
-                out=gate_i[:],
-                in0=gate_i[:],
-                scalar=1.0,
-                in1=gate_f[:],
-                op0=ALU.mult,
-                op1=ALU.add,
-                accum_out=small(bt, "cell_sum", 1)[:],
+                out=gate_i[:], in0=gate_i[:], scalar=1.0, in1=gate_f[:], op0=ALU.mult, op1=ALU.add, accum_out=total[:]
+            )
+            mean = small(bt, "cell_mean", 1)
+            nc.scalar.activation(out=mean[:], in_=total[:], func=FUNC.Identity, scale=1.0 / WIDTH)
+            mean_squared = small(bt, "cell_mean_squared", 1)
+            nc.scalar.activation(out=mean_squared[:], in_=mean[:], func=FUNC.Square)
+            eps_less_mean_squared = small(bt, "cell_eps_less_mean_squared", 1)
+            nc.scalar.activation(
+                out=eps_less_mean_squared[:], in_=mean_squared[:], func=FUNC.Identity, scale=-1.0, bias=eps[:]
             )
             unread = unread_pool.tile([P, WIDTH], BF16, name="unread")
-            nc.scalar.activation(out=unread[:], in_=gate_i[:], func=FUNC.Square, accum_out=small(bt, "cell_squares", 1)[:])
-
-        def cell_statistics(bt):
-            mean = small(bt, "cell_mean", 1)
-            nc.vector.tensor_scalar(out=mean[:], in0=stats[(bt, "cell_sum")][:], scalar1=1.0 / WIDTH, scalar2=None, op0=ALU.mult)
-            mean_squared = small(bt, "cell_mean_squared", 1)
-            nc.vector.tensor_tensor(out=mean_squared[:], in0=mean[:], in1=mean[:], op=ALU.mult)
-            variance = small(bt, "cell_variance", 1)
-            nc.vector.scalar_tensor_tensor(
-                out=variance[:],
-                in0=stats[(bt, "cell_squares")][:],
-                scalar=1.0 / WIDTH,
-                in1=mean_squared[:],
-                op0=ALU.mult,
-                op1=ALU.subtract,
-            )
+            squares = small(bt, "cell_squares", 1)
+            nc.scalar.activation(out=unread[:], in_=gate_i[:], func=FUNC.Square, accum_out=squares[:])
             nc.scalar.activation(
-                out=small(bt, "cell_deviation", 1)[:], in_=variance[:], func=FUNC.Sqrt, bias=eps[:], scale=1.0
+                out=small(bt, "cell_deviation", 1)[:],
+                in_=squares[:],
+                func=FUNC.Sqrt,
+                scale=1.0 / WIDTH,
+                bias=eps_less_mean_squared[:],
             )
 
         def cell_norm(bt):
             rows = slice(bt * P, (bt + 1) * P)
-            cell = slabs[(bt, 0)]
+            cell = slabs[(bt, GATES)]
             inverse = small(bt, "cell_inverse", 1)
             nc.vector.reciprocal(out=inverse[:], in_=stats[(bt, "cell_deviation")][:])
             nc.vector.scalar_tensor_tensor(
@@ -392,29 +445,15 @@ def tile_adaptivelstmcell_pb_kernel(
 
         def hidden_state(bt):
             rows = slice(bt * P, (bt + 1) * P)
-            gate_o = slabs[(bt, 3)]
+            gate_o = slabs[(bt, GATES + 3)]
             nc.vector.tensor_tensor(out=gate_o[:], in0=gate_o[:], in1=slabs[(bt, "tanh_cy")][:], op=ALU.mult)
             nc.sync.dma_start(out=out_0[rows, :], in_=gate_o[:])
 
         load_batch_tile(0)
-        bias_rows = const.tile([P, PATHS, ROW // P], BF16, name="bias_rows")
-        for path in range(PATHS):
-            nc.sync.dma_start(out=bias_rows[:, path, :], in_=path_bias[path].rearrange("(k j) -> k j", k=P))
+        nc.sync.dma_start(out=input_bias_row[0:1, :], in_=b_ih.rearrange("(o n) -> o n", o=1))
         load_scale_planes(0)
         load_slab_weights(0)
         prepare_batch_tile(0)
-        bias_columns = psum.tile([P, PATHS, ROW // P], F32, name="bias_columns", tag="turn")
-        nc.tensor.matmul(
-            bias_columns[:].rearrange("p u j -> p (u j)"),
-            lhsT=ones[:],
-            rhs=bias_rows[:].rearrange("p u j -> p (u j)"),
-            start=True,
-            stop=True,
-        )
-        bias_total = const.tile([P, PATHS], F32, name="bias_total")
-        nc.vector.tensor_reduce(out=bias_total[:], in_=bias_columns[:], axis=AXIS.X, op=ALU.add)
-        bias_mean = const.tile([P, PATHS], F32, name="bias_mean")
-        nc.vector.tensor_scalar(out=bias_mean[:], in0=bias_total[:], scalar1=1.0 / ROW, scalar2=None, op0=ALU.mult)
         load_slab_weights(1)
         turn_hyper_weights(0)
         load_slab_weights(2)
@@ -439,28 +478,35 @@ def tile_adaptivelstmcell_pb_kernel(
                 turn_hyper_weights(n + 2)
             if n == SLABS - 3:
                 load_gains()
-            if bt == 1 and k < GATES:
-                load_shifts(k)
-            if bt == 1 and 1 <= k <= GATES:
-                add_shifts(k - 1)
 
             if k == 4 and bt + 1 < BATCH_TILES:
                 load_batch_tile(bt + 1)
             if k == 6 and bt + 1 < BATCH_TILES:
                 prepare_batch_tile(bt + 1)
 
+            if n == SLABS - 1 or n == SLABS:
+                add_shifts(2 * (n - SLABS + 1))
+                add_shifts(2 * (n - SLABS + 1) + 1)
+            if n == SLABS - 2 or n == SLABS - 1:
+                load_shifts(2 * (n - SLABS + 2))
+                load_shifts(2 * (n - SLABS + 2) + 1)
+
+            if k == SLABS - 1 and bt < BATCH_TILES:
+                row_means(bt)
             if tail >= 0:
+                if k == 0:
+                    center_and_gain(tail, 0)
                 if k == 1:
-                    row_statistics(tail)
+                    row_deviations(tail)
+                    center_and_gain(tail, 1)
+                    row_inverse_deviations(tail)
                 if k == 2:
-                    row_inverse_deviation(tail)
-                if 2 <= k <= 4:
-                    gate_values(tail, k - 2)
-                if k == 5:
+                    scale_and_add(tail, 0)
+                if k == 3:
+                    scale_and_add(tail, 1)
+                if k == 4:
                     cell_sum(tail)
-                    gate_values(tail, 3)
-                    cell_statistics(tail)
-                if k == 6:
+                if k == 5:
                     cell_norm(tail)
-                if k == 7:
+                if k == 6:
                     hidden_state(tail)

@@ -101,6 +101,11 @@ def tile_adaptivelstmcell_pb_kernel(
         input_bias_row = const.tile([P, ROW], BF16, name="input_bias_row")
         nc.gpsimd.memset(input_bias_row[:], 0.0)
 
+        bias_share = const.tile([P, PATHS], F32, name="bias_share")
+        nc.vector.memset(bias_share[:], 0.0)
+        bias_share_parts = const.tile([P, GATES], F32, name="bias_share_parts")
+        bias_share_unread = const.tile([P, GATES], F32, name="bias_share_unread")
+
         raw = {}
         operands = {}
         banks = {}
@@ -270,8 +275,7 @@ def tile_adaptivelstmcell_pb_kernel(
             bt, slot = divmod(n, SLABS)
             path, gate = divmod(slot, GATES)
             if slot == 0:
-                stats[(bt, "sum_parts0")] = stat_pool.tile([P, GATES], F32, name="sum_parts0")
-                stats[(bt, "sum_parts1")] = stat_pool.tile([P, GATES * HALVES], F32, name="sum_parts1")
+                stats[(bt, "sum_parts")] = stat_pool.tile([P, PATHS, GATES * HALVES], F32, name="sum_parts")
                 stats[(bt, "square_parts")] = stat_pool.tile([P, PATHS, GATES], F32, name="square_parts")
             alpha_sb, xh_banks, beta_banks = banks[n]
             pre = slab_pool.tile([P, WIDTH], F32, name="pre", tag="slab")
@@ -281,28 +285,19 @@ def tile_adaptivelstmcell_pb_kernel(
                 )
             for half in range(HALVES):
                 half_cols = slice(half * BANK, (half + 1) * BANK)
-                if path == 1:
-                    part = gate * HALVES + half
-                    nc.vector.scalar_tensor_tensor(
-                        out=pre[:, half_cols],
-                        in0=pre[:, half_cols],
-                        scalar=1.0,
-                        in1=beta_banks[half][:],
-                        op0=ALU.mult,
-                        op1=ALU.add,
-                        accum_out=stats[(bt, "sum_parts1")][:, part : part + 1],
-                    )
-                else:
-                    nc.vector.tensor_tensor(out=pre[:, half_cols], in0=pre[:, half_cols], in1=beta_banks[half][:], op=ALU.add)
-            if path == 0:
+                part = gate * HALVES + half
                 nc.vector.scalar_tensor_tensor(
-                    out=pre[:],
-                    in0=pre[:],
+                    out=pre[:, half_cols],
+                    in0=pre[:, half_cols],
                     scalar=1.0,
-                    in1=hidden_bias_rep[:, gate * WIDTH : (gate + 1) * WIDTH],
+                    in1=beta_banks[half][:],
                     op0=ALU.mult,
                     op1=ALU.add,
-                    accum_out=stats[(bt, "sum_parts0")][:, gate : gate + 1],
+                    accum_out=stats[(bt, "sum_parts")][:, path, part : part + 1],
+                )
+            if path == 0:
+                nc.gpsimd.tensor_tensor(
+                    out=pre[:], in0=pre[:], in1=hidden_bias_rep[:, gate * WIDTH : (gate + 1) * WIDTH], op=ALU.add
                 )
             slabs[(bt, slot)] = pre
 
@@ -324,13 +319,27 @@ def tile_adaptivelstmcell_pb_kernel(
         def row_means(bt):
             mean = small(bt, "mean", PATHS)
             for path in range(PATHS):
-                parts = stats[(bt, "sum_parts%d" % path)]
                 nc.scalar.activation(
-                    out=small(bt, "scaled_sums%d" % path, parts.shape[1])[:],
-                    in_=parts[:],
+                    out=small(bt, "scaled_sums%d" % path, GATES * HALVES)[:],
+                    in_=stats[(bt, "sum_parts")][:, path, :],
                     func=FUNC.Identity,
                     scale=1.0 / ROW,
+                    bias=bias_share[:, path : path + 1],
                     accum_out=mean[:, path : path + 1],
+                )
+
+        def hidden_bias_share(gate):
+            unread = unread_pool.tile([P, WIDTH], BF16, name="unread")
+            nc.scalar.activation(
+                out=unread[:],
+                in_=hidden_bias_rep[:, gate * WIDTH : (gate + 1) * WIDTH],
+                func=FUNC.Identity,
+                scale=1.0 / (ROW * GATES * HALVES),
+                accum_out=bias_share_parts[:, gate : gate + 1],
+            )
+            if gate == GATES - 1:
+                nc.scalar.activation(
+                    out=bias_share_unread[:], in_=bias_share_parts[:], func=FUNC.Identity, accum_out=bias_share[:, 0:1]
                 )
 
         def row_deviations(bt):
@@ -478,6 +487,8 @@ def tile_adaptivelstmcell_pb_kernel(
                 turn_hyper_weights(n + 2)
             if n == SLABS - 3:
                 load_gains()
+            if n < GATES:
+                hidden_bias_share(n)
 
             if k == 4 and bt + 1 < BATCH_TILES:
                 load_batch_tile(bt + 1)

@@ -66,7 +66,7 @@ def tile_adaptivelstmcell_pb_kernel(
 
     with ExitStack() as ctx:
         const = ctx.enter_context(tc.tile_pool(name="const", bufs=1))
-        raw_pool = ctx.enter_context(tc.tile_pool(name="raw", bufs=8))
+        raw_pool = ctx.enter_context(tc.tile_pool(name="raw", bufs=11))
         operand_pool = ctx.enter_context(tc.tile_pool(name="operand", bufs=2))
         slab_pool = ctx.enter_context(tc.tile_pool(name="slab", bufs=12))
         alpha_pool = ctx.enter_context(tc.tile_pool(name="alpha", bufs=2))
@@ -79,10 +79,12 @@ def tile_adaptivelstmcell_pb_kernel(
         make_identity(nc, ident_bf16[:])
         ident_f32 = const.tile([P, P], F32, name="ident_f32")
         make_identity(nc, ident_f32[:])
-        ones = const.tile([P, P], BF16, name="ones")
-        nc.vector.memset(ones[:], 1.0)
         eps = const.tile([P, 1], F32, name="eps")
         nc.vector.memset(eps[:], EPS)
+        quarter_eps = const.tile([P, 1], F32, name="quarter_eps")
+        nc.vector.memset(quarter_eps[:], EPS / GATES)
+        minus_half = const.tile([P, PATHS], F32, name="minus_half")
+        nc.vector.memset(minus_half[:], -0.5)
 
         words = []
         planes = []
@@ -98,8 +100,8 @@ def tile_adaptivelstmcell_pb_kernel(
         shift_rep = const.tile([P, ROW], F32, name="shift_rep")
         cell_gain_rep = const.tile([P, WIDTH], BF16, name="cell_gain_rep")
         cell_shift_rep = const.tile([P, WIDTH], BF16, name="cell_shift_rep")
-        input_bias_row = const.tile([P, ROW], BF16, name="input_bias_row")
-        nc.gpsimd.memset(input_bias_row[:], 0.0)
+        input_bias_rows = const.tile([P, WIDTH], BF16, name="input_bias_rows")
+        nc.gpsimd.memset(input_bias_rows[:], 0.0)
 
         bias_share = const.tile([P, PATHS], F32, name="bias_share")
         nc.vector.memset(bias_share[:], 0.0)
@@ -117,14 +119,18 @@ def tile_adaptivelstmcell_pb_kernel(
             sources = {
                 "x": x[rows, :],
                 "hx": hx[rows, :],
-                "cx": cx[rows, :],
                 "zw": zw[rows, :, :].rearrange("b s a -> b (s a)"),
                 "zb": zb[rows, :, :].rearrange("b s a -> b (s a)"),
             }
-            for key in ("hx", "x", "zw", "zb", "cx"):
+            for key in ("hx", "zw", "zb", "x"):
                 loaded = raw_pool.tile([P, WIDTH], BF16, name="raw_" + key, tag="raw")
                 nc.sync.dma_start(out=loaded[:], in_=sources[key])
                 raw[(bt, key)] = loaded
+
+        def load_cell_state(bt):
+            loaded = raw_pool.tile([P, WIDTH], BF16, name="raw_cx", tag="raw")
+            nc.sync.dma_start(out=loaded[:], in_=cx[bt * P : (bt + 1) * P, :])
+            raw[(bt, "cx")] = loaded
 
         def load_scale_planes(path):
             for g in range(PASSES):
@@ -172,12 +178,11 @@ def tile_adaptivelstmcell_pb_kernel(
 
         def add_shifts(gate):
             cols = slice(gate * WIDTH, (gate + 1) * WIDTH)
-            nc.vector.tensor_tensor(
+            nc.gpsimd.tensor_tensor(
                 out=shift_rep[:, cols], in0=raw[(gate, "shift0")][:], in1=raw[(gate, "shift1")][:], op=ALU.add
             )
 
-        def prepare_batch_tile(bt):
-            grouped = []
+        def turn_activations(bt):
             for key in ("hx", "x"):
                 pairs = raw[(bt, key)][:].bitcast(F32)
                 turned = psum.tile([P, PASSES, 2, P], F32, name="turned_" + key, tag="turn")
@@ -195,7 +200,17 @@ def tile_adaptivelstmcell_pb_kernel(
                     out=side_by_side[:].bitcast(F32).rearrange("p (g b u) -> p g b u", g=PASSES, u=2),
                     in_=turned[:].rearrange("p g u b -> p g b u"),
                 )
-                grouped.append(side_by_side)
+                operands[(bt, "side_by_side_" + key)] = side_by_side
+
+        def quantise_activations(bt):
+            for path, key in enumerate(("hx", "x")):
+                codes = operand_pool.tile([P, PASSES * P], U32, name="codes%d" % path, align_bytes=64)
+                code_scales = operand_pool.tile([P, PASSES * P], U8, name="code_scales%d" % path, align_bytes=64)
+                nc.vector.quantize_mx(out=codes[:].bitcast(FP8X4), scales=code_scales[:], in_=operands[(bt, "side_by_side_" + key)][:])
+                operands[(bt, "codes%d" % path)] = codes
+                operands[(bt, "code_scales%d" % path)] = code_scales
+
+        def turn_embeddings(bt):
             for key in ("zw", "zb"):
                 turned = psum.tile([P, SLABS, P], BF16, name="turned_" + key, tag="turn")
                 for slot in range(SLABS):
@@ -206,12 +221,6 @@ def tile_adaptivelstmcell_pb_kernel(
                 embT = operand_pool.tile([P, SLABS, P], BF16, name=key + "T")
                 nc.scalar.copy(out=embT[:], in_=turned[:])
                 operands[(bt, key)] = embT
-            for path in range(PATHS):
-                codes = operand_pool.tile([P, PASSES * P], U32, name="codes%d" % path, align_bytes=64)
-                code_scales = operand_pool.tile([P, PASSES * P], U8, name="code_scales%d" % path, align_bytes=64)
-                nc.vector.quantize_mx(out=codes[:].bitcast(FP8X4), scales=code_scales[:], in_=grouped[path][:])
-                operands[(bt, "codes%d" % path)] = codes
-                operands[(bt, "code_scales%d" % path)] = code_scales
 
         def turn_hyper_weights(slot):
             turned_alpha = psum.tile([P, BLOCKS, P], BF16, name="turned_alpha_w", tag="turn")
@@ -261,9 +270,12 @@ def tile_adaptivelstmcell_pb_kernel(
                     stop=(path == 0),
                 )
                 if path == 1:
-                    first = gate * WIDTH + half * BANK
                     nc.tensor.matmul(
-                        bank[:], lhsT=ones[:], rhs=input_bias_row[:, first : first + BANK], start=False, stop=True
+                        bank[:],
+                        lhsT=ident_bf16[:, gate : gate + 1].to_broadcast([P, P]),
+                        rhs=input_bias_rows[:, half * BANK : (half + 1) * BANK],
+                        start=False,
+                        stop=True,
                     )
                 beta_banks.append(bank)
             alpha_sb = alpha_pool.tile([P, HALVES, BANK], F32, name="alpha_sb")
@@ -342,32 +354,24 @@ def tile_adaptivelstmcell_pb_kernel(
                     out=bias_share_unread[:], in_=bias_share_parts[:], func=FUNC.Identity, accum_out=bias_share[:, 0:1]
                 )
 
-        def row_deviations(bt):
+        def row_inverse_deviations(bt):
             mean_squared = small(bt, "mean_squared", PATHS)
             nc.scalar.activation(out=mean_squared[:], in_=stats[(bt, "mean")][:], func=FUNC.Square)
-            eps_less_mean_squared = small(bt, "eps_less_mean_squared", PATHS)
+            quarter_rest = small(bt, "quarter_rest", PATHS)
             nc.scalar.activation(
-                out=eps_less_mean_squared[:], in_=mean_squared[:], func=FUNC.Identity, scale=-1.0, bias=eps[:]
+                out=quarter_rest[:], in_=mean_squared[:], func=FUNC.Identity, scale=-1.0 / GATES, bias=quarter_eps[:]
             )
-            mean_of_squares = small(bt, "mean_of_squares", PATHS)
-            deviation = small(bt, "deviation", PATHS)
+            variance = small(bt, "variance", PATHS)
             for path in range(PATHS):
-                one = slice(path, path + 1)
                 nc.scalar.activation(
                     out=small(bt, "scaled_squares%d" % path, GATES)[:],
                     in_=stats[(bt, "square_parts")][:, path, :],
                     func=FUNC.Identity,
                     scale=1.0 / ROW,
-                    accum_out=mean_of_squares[:, one],
+                    bias=quarter_rest[:, path : path + 1],
+                    accum_out=variance[:, path : path + 1],
                 )
-            for path in range(PATHS):
-                one = slice(path, path + 1)
-                nc.scalar.activation(
-                    out=deviation[:, one], in_=mean_of_squares[:, one], func=FUNC.Sqrt, bias=eps_less_mean_squared[:, one]
-                )
-
-        def row_inverse_deviations(bt):
-            nc.vector.reciprocal(out=small(bt, "inverse", PATHS)[:], in_=stats[(bt, "deviation")][:])
+            nc.gpsimd.tensor_tensor(out=small(bt, "inverse", PATHS)[:], in0=variance[:], in1=minus_half[:], op=ALU.pow)
 
         def center_and_gain(bt, pair):
             mean = stats[(bt, "mean")]
@@ -409,43 +413,49 @@ def tile_adaptivelstmcell_pb_kernel(
                 )
                 nc.scalar.activation(out=pre_in[:], in_=pre_in[:], func=(FUNC.Tanh if gate == 1 else FUNC.Sigmoid))
 
+        def cell_products(bt, first, engine):
+            if first:
+                gate_i = slabs[(bt, GATES)]
+                engine.tensor_tensor(out=gate_i[:], in0=gate_i[:], in1=slabs[(bt, GATES + 1)][:], op=ALU.mult)
+            else:
+                gate_f = slabs[(bt, GATES + 2)]
+                engine.tensor_tensor(out=gate_f[:], in0=gate_f[:], in1=raw[(bt, "cx")][:], op=ALU.mult)
+
         def cell_sum(bt):
-            gate_i, gate_j, gate_f = slabs[(bt, GATES)], slabs[(bt, GATES + 1)], slabs[(bt, GATES + 2)]
-            nc.vector.tensor_tensor(out=gate_i[:], in0=gate_i[:], in1=gate_j[:], op=ALU.mult)
-            nc.vector.tensor_tensor(out=gate_f[:], in0=gate_f[:], in1=raw[(bt, "cx")][:], op=ALU.mult)
+            cell = slabs[(bt, GATES)]
             total = small(bt, "cell_total", 1)
             nc.vector.scalar_tensor_tensor(
-                out=gate_i[:], in0=gate_i[:], scalar=1.0, in1=gate_f[:], op0=ALU.mult, op1=ALU.add, accum_out=total[:]
+                out=cell[:],
+                in0=cell[:],
+                scalar=1.0,
+                in1=slabs[(bt, GATES + 2)][:],
+                op0=ALU.mult,
+                op1=ALU.add,
+                accum_out=total[:],
             )
             mean = small(bt, "cell_mean", 1)
             nc.scalar.activation(out=mean[:], in_=total[:], func=FUNC.Identity, scale=1.0 / WIDTH)
             mean_squared = small(bt, "cell_mean_squared", 1)
             nc.scalar.activation(out=mean_squared[:], in_=mean[:], func=FUNC.Square)
-            eps_less_mean_squared = small(bt, "cell_eps_less_mean_squared", 1)
-            nc.scalar.activation(
-                out=eps_less_mean_squared[:], in_=mean_squared[:], func=FUNC.Identity, scale=-1.0, bias=eps[:]
-            )
+            rest = small(bt, "cell_rest", 1)
+            nc.scalar.activation(out=rest[:], in_=mean_squared[:], func=FUNC.Identity, scale=-1.0, bias=eps[:])
             unread = unread_pool.tile([P, WIDTH], BF16, name="unread")
             squares = small(bt, "cell_squares", 1)
-            nc.scalar.activation(out=unread[:], in_=gate_i[:], func=FUNC.Square, accum_out=squares[:])
-            nc.scalar.activation(
-                out=small(bt, "cell_deviation", 1)[:],
-                in_=squares[:],
-                func=FUNC.Sqrt,
-                scale=1.0 / WIDTH,
-                bias=eps_less_mean_squared[:],
+            nc.scalar.activation(out=unread[:], in_=cell[:], func=FUNC.Square, accum_out=squares[:])
+            variance = small(bt, "cell_variance", 1)
+            nc.scalar.activation(out=variance[:], in_=squares[:], func=FUNC.Identity, scale=1.0 / WIDTH, bias=rest[:])
+            nc.gpsimd.tensor_tensor(
+                out=small(bt, "cell_inverse", 1)[:], in0=variance[:], in1=minus_half[:, 0:1], op=ALU.pow
             )
 
         def cell_norm(bt):
             rows = slice(bt * P, (bt + 1) * P)
             cell = slabs[(bt, GATES)]
-            inverse = small(bt, "cell_inverse", 1)
-            nc.vector.reciprocal(out=inverse[:], in_=stats[(bt, "cell_deviation")][:])
             nc.vector.scalar_tensor_tensor(
                 out=cell[:], in0=cell[:], scalar=stats[(bt, "cell_mean")][:], in1=cell_gain_rep[:], op0=ALU.subtract, op1=ALU.mult
             )
             nc.vector.scalar_tensor_tensor(
-                out=cell[:], in0=cell[:], scalar=inverse[:], in1=cell_shift_rep[:], op0=ALU.mult, op1=ALU.add
+                out=cell[:], in0=cell[:], scalar=stats[(bt, "cell_inverse")][:], in1=cell_shift_rep[:], op0=ALU.mult, op1=ALU.add
             )
             nc.sync.dma_start(out=out_1[rows, :], in_=cell[:])
             tanh_cy = slab_pool.tile([P, WIDTH], F32, name="tanh_cy", tag="slab")
@@ -459,25 +469,32 @@ def tile_adaptivelstmcell_pb_kernel(
             nc.sync.dma_start(out=out_0[rows, :], in_=gate_o[:])
 
         load_batch_tile(0)
-        nc.sync.dma_start(out=input_bias_row[0:1, :], in_=b_ih.rearrange("(o n) -> o n", o=1))
+        nc.sync.dma_start(out=input_bias_rows[0:GATES, :], in_=b_ih.rearrange("(g n) -> g n", g=GATES))
         load_scale_planes(0)
         load_slab_weights(0)
-        prepare_batch_tile(0)
+        turn_activations(0)
+        turn_embeddings(0)
+        quantise_activations(0)
         load_slab_weights(1)
         turn_hyper_weights(0)
         load_slab_weights(2)
         turn_hyper_weights(1)
         slab_matmuls(0)
 
-        for n in range(ALL_SLABS + SLABS):
+        for n in range(ALL_SLABS + SLABS + 1):
             bt, k = divmod(n, SLABS)
             tail = bt - 1
             if n < ALL_SLABS:
                 slab_combine(n)
             if n + 1 < ALL_SLABS:
                 slab_matmuls(n + 1)
-            if 1 <= n <= ALL_SLABS:
+            if 1 <= k <= GATES and bt < BATCH_TILES:
                 slab_squares(n - 1)
+            if k >= GATES and bt < BATCH_TILES:
+                slab_squares(n)
+            if k == SLABS - 1 and bt < BATCH_TILES:
+                row_means(bt)
+                row_inverse_deviations(bt)
 
             if n == 0:
                 load_scale_planes(1)
@@ -485,39 +502,45 @@ def tile_adaptivelstmcell_pb_kernel(
                 load_slab_weights(n + 3)
             if n + 2 < SLABS:
                 turn_hyper_weights(n + 2)
-            if n == SLABS - 3:
-                load_gains()
             if n < GATES:
                 hidden_bias_share(n)
+            if n == SLABS - 4:
+                for gate in range(GATES):
+                    load_shifts(gate)
+            if n == SLABS - 3:
+                load_gains()
+            if n == SLABS - 3 or n == SLABS - 2:
+                add_shifts(2 * (n - SLABS + 3))
+                add_shifts(2 * (n - SLABS + 3) + 1)
 
-            if k == 4 and bt + 1 < BATCH_TILES:
-                load_batch_tile(bt + 1)
-            if k == 6 and bt + 1 < BATCH_TILES:
-                prepare_batch_tile(bt + 1)
-
-            if n == SLABS - 1 or n == SLABS:
-                add_shifts(2 * (n - SLABS + 1))
-                add_shifts(2 * (n - SLABS + 1) + 1)
-            if n == SLABS - 2 or n == SLABS - 1:
-                load_shifts(2 * (n - SLABS + 2))
-                load_shifts(2 * (n - SLABS + 2) + 1)
-
-            if k == SLABS - 1 and bt < BATCH_TILES:
-                row_means(bt)
-            if tail >= 0:
+            if bt + 1 < BATCH_TILES:
                 if k == 0:
+                    load_batch_tile(bt + 1)
+                if k == 2:
+                    turn_activations(bt + 1)
+                if k == 3:
+                    turn_embeddings(bt + 1)
+
+            if k == 0 and bt >= 2:
+                hidden_state(bt - 2)
+            if 0 <= tail < BATCH_TILES:
+                product_engine = nc.vector if tail == BATCH_TILES - 1 else nc.gpsimd
+                if k == 0:
+                    load_cell_state(tail)
                     center_and_gain(tail, 0)
                 if k == 1:
-                    row_deviations(tail)
                     center_and_gain(tail, 1)
-                    row_inverse_deviations(tail)
                 if k == 2:
                     scale_and_add(tail, 0)
                 if k == 3:
                     scale_and_add(tail, 1)
                 if k == 4:
-                    cell_sum(tail)
+                    cell_products(tail, True, product_engine)
                 if k == 5:
-                    cell_norm(tail)
+                    cell_products(tail, False, product_engine)
                 if k == 6:
-                    hidden_state(tail)
+                    cell_sum(tail)
+                if k == 7:
+                    cell_norm(tail)
+            if k == 2 and bt + 1 < BATCH_TILES:
+                quantise_activations(bt + 1)

@@ -134,11 +134,10 @@ def tile_adaptivelstmcell_pb_kernel(
 
         def load_scale_planes(path):
             for g in range(PASSES):
-                for q in range(8):
-                    first = 32 * (q // 4) + q % 4
+                for r in range(4):
                     nc.sync.dma_start(
-                        out=planes[path][first:P:64, g, :].bitcast(I32),
-                        in_=path_scales[path][g, q:16:8, :].bitcast(I32),
+                        out=planes[path][r:P:32, g, :].bitcast(I32),
+                        in_=path_scales[path][g, r:16:4, :].bitcast(I32),
                     )
 
         def load_slab_weights(slot):
@@ -469,9 +468,9 @@ def tile_adaptivelstmcell_pb_kernel(
             nc.sync.dma_start(out=out_0[rows, :], in_=gate_o[:])
 
         load_batch_tile(0)
-        nc.sync.dma_start(out=input_bias_rows[0:GATES, :], in_=b_ih.rearrange("(g n) -> g n", g=GATES))
-        load_scale_planes(0)
         load_slab_weights(0)
+        load_scale_planes(0)
+        nc.sync.dma_start(out=input_bias_rows[0:GATES, :], in_=b_ih.rearrange("(g n) -> g n", g=GATES))
         turn_activations(0)
         turn_embeddings(0)
         quantise_activations(0)
@@ -490,10 +489,11 @@ def tile_adaptivelstmcell_pb_kernel(
                 slab_matmuls(n + 1)
             if 1 <= k <= GATES and bt < BATCH_TILES:
                 slab_squares(n - 1)
+            if k == SLABS - 1 and bt < BATCH_TILES:
+                row_means(bt)
             if k >= GATES and bt < BATCH_TILES:
                 slab_squares(n)
             if k == SLABS - 1 and bt < BATCH_TILES:
-                row_means(bt)
                 row_inverse_deviations(bt)
 
             if n == 0:

@@ -30,6 +30,10 @@ BATCH_TILES = BATCH // P
 SLABS = PATHS * GATES
 ALL_SLABS = BATCH_TILES * SLABS
 EPS = 1e-5
+QUARTERS = BANK // P
+GATE_F = 2
+GATE_O = 3
+ROW_GATES = (0, 1)
 
 FLOPS = 2 * BATCH * WIDTH * ROW * PATHS + 2 * SLABS * 2 * BATCH * EMB * WIDTH
 
@@ -72,6 +76,7 @@ def tile_adaptivelstmcell_pb_kernel(
         alpha_pool = ctx.enter_context(tc.tile_pool(name="alpha", bufs=2))
         unread_pool = ctx.enter_context(tc.tile_pool(name="unread", bufs=2))
         stat_pool = ctx.enter_context(tc.tile_pool(name="stat", bufs=2))
+        scaled_pool = ctx.enter_context(tc.tile_pool(name="scaled", bufs=4))
         psum = ctx.enter_context(tc.psum_pool(name="psum", bufs=2))
         ctx.enter_context(tc.manual_schedule())
 
@@ -96,8 +101,11 @@ def tile_adaptivelstmcell_pb_kernel(
         alpha_wT = const.tile([P, SLABS, WIDTH], BF16, name="alpha_wT")
         beta_wT = const.tile([P, SLABS, WIDTH], BF16, name="beta_wT")
         hidden_bias_rep = const.tile([P, ROW], BF16, name="hidden_bias_rep")
-        gain_rep = const.tile([P, PATHS, ROW], BF16, name="gain_rep")
-        shift_rep = const.tile([P, ROW], F32, name="shift_rep")
+        gain_rep = const.tile([P, PATHS, len(ROW_GATES) * WIDTH], BF16, name="gain_rep")
+        shift_rep = const.tile([P, len(ROW_GATES) * WIDTH], F32, name="shift_rep")
+        vector_rows = const.tile([P, P], BF16, name="vector_rows")
+        vector_cols = const.tile([P, P], F32, name="vector_cols")
+        shift_cols = const.tile([P, ROW // P], F32, name="shift_cols")
         cell_gain_rep = const.tile([P, WIDTH], BF16, name="cell_gain_rep")
         cell_shift_rep = const.tile([P, WIDTH], BF16, name="cell_shift_rep")
         input_bias_rows = const.tile([P, WIDTH], BF16, name="input_bias_rows")
@@ -113,6 +121,9 @@ def tile_adaptivelstmcell_pb_kernel(
         banks = {}
         slabs = {}
         stats = {}
+        turned_slabs = {}
+        scaled_slabs = {}
+        summed_slabs = {}
 
         def load_batch_tile(bt):
             rows = slice(bt * P, (bt + 1) * P)
@@ -159,7 +170,7 @@ def tile_adaptivelstmcell_pb_kernel(
                 nc.sync.dma_start(out=hidden_bias_rep[:, cols], in_=b_hh[cols].partition_broadcast(P))
 
         def load_gains():
-            for gate in range(GATES):
+            for gate in ROW_GATES:
                 cols = slice(gate * WIDTH, (gate + 1) * WIDTH)
                 for path in range(PATHS):
                     nc.sync.dma_start(
@@ -192,12 +203,16 @@ def tile_adaptivelstmcell_pb_kernel(
                             in_=pairs[:, (K_PASS // 2) * g + u : (K_PASS // 2) * (g + 1) : 2],
                             identity=ident_f32[:],
                         )
+                operands[(bt, "turned_" + key)] = turned
+
+        def copy_activations(bt):
+            for key in ("hx", "x"):
                 side_by_side = operand_pool.tile(
                     [P, PASSES * P * 4], BF16, name="side_by_side_" + key, tag="side_by_side", align_bytes=64
                 )
                 nc.scalar.copy(
                     out=side_by_side[:].bitcast(F32).rearrange("p (g b u) -> p g b u", g=PASSES, u=2),
-                    in_=turned[:].rearrange("p g u b -> p g b u"),
+                    in_=operands[(bt, "turned_" + key)][:].rearrange("p g u b -> p g b u"),
                 )
                 operands[(bt, "side_by_side_" + key)] = side_by_side
 
@@ -217,9 +232,28 @@ def tile_adaptivelstmcell_pb_kernel(
                     nc.tensor.transpose(
                         out=turned[:, slot, :], in_=raw[(bt, key)][:, emb * EMB : (emb + 1) * EMB], identity=ident_bf16[:]
                     )
+                operands[(bt, "turned_" + key)] = turned
+
+        def copy_embeddings(bt):
+            for key in ("zw", "zb"):
                 embT = operand_pool.tile([P, SLABS, P], BF16, name=key + "T")
-                nc.scalar.copy(out=embT[:], in_=turned[:])
+                nc.scalar.copy(out=embT[:], in_=operands[(bt, "turned_" + key)][:])
                 operands[(bt, key)] = embT
+
+        def load_vector_rows():
+            for v, vector in enumerate((ln_i_w, ln_h_w, ln_i_b, ln_h_b)):
+                nc.sync.dma_start(
+                    out=vector_rows[(ROW // P) * v : (ROW // P) * (v + 1), :], in_=vector.rearrange("(c p) -> c p", p=P)
+                )
+
+        def turn_vectors():
+            turned = psum.tile([P, P], BF16, name="turned_vectors", tag="turn")
+            nc.tensor.transpose(out=turned[:], in_=vector_rows[:], identity=ident_bf16[:])
+            nc.scalar.copy(out=vector_cols[:], in_=turned[:])
+            blocks = ROW // P
+            nc.vector.tensor_tensor(
+                out=shift_cols[:], in0=vector_cols[:, 2 * blocks : 3 * blocks], in1=vector_cols[:, 3 * blocks : 4 * blocks], op=ALU.add
+            )
 
         def turn_hyper_weights(slot):
             turned_alpha = psum.tile([P, BLOCKS, P], BF16, name="turned_alpha_w", tag="turn")
@@ -372,45 +406,97 @@ def tile_adaptivelstmcell_pb_kernel(
                 )
             nc.gpsimd.tensor_tensor(out=small(bt, "inverse", PATHS)[:], in0=variance[:], in1=minus_half[:], op=ALU.pow)
 
-        def center_and_gain(bt, pair):
-            mean = stats[(bt, "mean")]
-            for gate in (2 * pair, 2 * pair + 1):
-                cols = slice(gate * WIDTH, (gate + 1) * WIDTH)
-                for path in range(PATHS):
-                    pre = slabs[(bt, path * GATES + gate)]
-                    nc.vector.scalar_tensor_tensor(
-                        out=pre[:],
-                        in0=pre[:],
-                        scalar=mean[:, path : path + 1],
-                        in1=gain_rep[:, path, cols],
-                        op0=ALU.subtract,
-                        op1=ALU.mult,
-                    )
+        def center_and_gain(bt, gate, path):
+            pre = slabs[(bt, path * GATES + gate)]
+            nc.vector.scalar_tensor_tensor(
+                out=pre[:],
+                in0=pre[:],
+                scalar=stats[(bt, "mean")][:, path : path + 1],
+                in1=gain_rep[:, path, gate * WIDTH : (gate + 1) * WIDTH],
+                op0=ALU.subtract,
+                op1=ALU.mult,
+            )
 
-        def scale_and_add(bt, pair):
+        def scale_and_add(bt, gate, path):
             inverse = stats[(bt, "inverse")]
-            gates = (2 * pair, 2 * pair + 1)
-            for gate in gates:
-                pre_hid = slabs[(bt, gate)]
-                nc.vector.scalar_tensor_tensor(
-                    out=pre_hid[:],
-                    in0=pre_hid[:],
-                    scalar=inverse[:, 0:1],
-                    in1=shift_rep[:, gate * WIDTH : (gate + 1) * WIDTH],
-                    op0=ALU.mult,
-                    op1=ALU.add,
+            pre = slabs[(bt, path * GATES + gate)]
+            nc.vector.scalar_tensor_tensor(
+                out=pre[:],
+                in0=pre[:],
+                scalar=inverse[:, path : path + 1],
+                in1=(shift_rep[:, gate * WIDTH : (gate + 1) * WIDTH] if path == 0 else slabs[(bt, gate)][:]),
+                op0=ALU.mult,
+                op1=ALU.add,
+            )
+            if path == 1:
+                nc.scalar.activation(out=pre[:], in_=pre[:], func=(FUNC.Tanh if gate == 1 else FUNC.Sigmoid))
+
+        def normalise(bt, gate):
+            for path in range(PATHS):
+                pre = slabs[(bt, path * GATES + gate)]
+                nc.vector.tensor_scalar(
+                    out=pre[:],
+                    in0=pre[:],
+                    scalar1=stats[(bt, "mean")][:, path : path + 1],
+                    scalar2=stats[(bt, "inverse")][:, path : path + 1],
+                    op0=ALU.subtract,
+                    op1=ALU.mult,
                 )
-            for gate in gates:
-                pre_in = slabs[(bt, GATES + gate)]
-                nc.vector.scalar_tensor_tensor(
-                    out=pre_in[:],
-                    in0=pre_in[:],
-                    scalar=inverse[:, 1:2],
-                    in1=slabs[(bt, gate)][:],
-                    op0=ALU.mult,
-                    op1=ALU.add,
-                )
-                nc.scalar.activation(out=pre_in[:], in_=pre_in[:], func=(FUNC.Tanh if gate == 1 else FUNC.Sigmoid))
+
+        def turn_forward(bt, gate, half, tags=("turn", "turn")):
+            for path in range(PATHS):
+                pre = slabs[(bt, path * GATES + gate)]
+                turned = psum.tile([P, QUARTERS, P], F32, name="turned_slab", tag=tags[path])
+                for q in range(QUARTERS):
+                    first = half * BANK + q * P
+                    nc.tensor.transpose(out=turned[:, q, :], in_=pre[:, first : first + P], identity=ident_f32[:])
+                turned_slabs[(bt, gate, half, path)] = turned
+
+        def gain_and_shift(bt, gate, half):
+            blocks = ROW // P
+            for path in range(PATHS):
+                turned = turned_slabs[(bt, gate, half, path)]
+                scaled = scaled_pool.tile([P, QUARTERS, P], F32, name="scaled")
+                for q in range(QUARTERS):
+                    col = gate * BLOCKS + half * QUARTERS + q
+                    gain_col = (1 - path) * blocks + col
+                    if path == 0:
+                        nc.scalar.activation(
+                            out=scaled[:, q, :],
+                            in_=turned[:, q, :],
+                            func=FUNC.Identity,
+                            scale=vector_cols[:, gain_col : gain_col + 1],
+                            bias=shift_cols[:, col : col + 1],
+                        )
+                    else:
+                        nc.scalar.activation(
+                            out=scaled[:, q, :],
+                            in_=turned[:, q, :],
+                            func=FUNC.Identity,
+                            scale=vector_cols[:, gain_col : gain_col + 1],
+                        )
+                scaled_slabs[(bt, gate, half, path)] = scaled
+
+        def turn_back(bt, gate, half, tag="turn"):
+            summed = psum.tile([P, BANK], F32, name="summed", tag=tag)
+            for q in range(QUARTERS):
+                for path in range(PATHS):
+                    nc.tensor.matmul(
+                        summed[:, q * P : (q + 1) * P],
+                        lhsT=scaled_slabs[(bt, gate, half, path)][:, q, :],
+                        rhs=ident_f32[:],
+                        is_transpose=True,
+                        start=(path == 0),
+                        stop=(path == PATHS - 1),
+                    )
+            summed_slabs[(bt, gate, half)] = summed
+
+        def activate(bt, gate, half):
+            nc.scalar.activation(
+                out=slabs[(bt, GATES + gate)][:, half * BANK : (half + 1) * BANK],
+                in_=summed_slabs[(bt, gate, half)][:],
+                func=FUNC.Sigmoid,
+            )
 
         def cell_products(bt, first, engine):
             if first:
@@ -450,29 +536,36 @@ def tile_adaptivelstmcell_pb_kernel(
         def cell_norm(bt):
             rows = slice(bt * P, (bt + 1) * P)
             cell = slabs[(bt, GATES)]
-            nc.vector.scalar_tensor_tensor(
-                out=cell[:], in0=cell[:], scalar=stats[(bt, "cell_mean")][:], in1=cell_gain_rep[:], op0=ALU.subtract, op1=ALU.mult
-            )
-            nc.vector.scalar_tensor_tensor(
-                out=cell[:], in0=cell[:], scalar=stats[(bt, "cell_inverse")][:], in1=cell_shift_rep[:], op0=ALU.mult, op1=ALU.add
-            )
-            nc.sync.dma_start(out=out_1[rows, :], in_=cell[:])
-            tanh_cy = slab_pool.tile([P, WIDTH], F32, name="tanh_cy", tag="slab")
-            nc.scalar.activation(out=tanh_cy[:], in_=cell[:], func=FUNC.Tanh)
-            slabs[(bt, "tanh_cy")] = tanh_cy
+            tanh_cy = slabs[(bt, GATES + 2)]
+            for half in range(HALVES):
+                cols = slice(half * BANK, (half + 1) * BANK)
+                nc.vector.scalar_tensor_tensor(
+                    out=cell[:, cols], in0=cell[:, cols], scalar=stats[(bt, "cell_mean")][:], in1=cell_gain_rep[:, cols], op0=ALU.subtract, op1=ALU.mult
+                )
+            for half in range(HALVES):
+                cols = slice(half * BANK, (half + 1) * BANK)
+                nc.vector.scalar_tensor_tensor(
+                    out=cell[:, cols], in0=cell[:, cols], scalar=stats[(bt, "cell_inverse")][:], in1=cell_shift_rep[:, cols], op0=ALU.mult, op1=ALU.add
+                )
+                nc.sync.dma_start(out=out_1[rows, cols], in_=cell[:, cols])
+                nc.scalar.activation(out=tanh_cy[:, cols], in_=cell[:, cols], func=FUNC.Tanh)
 
         def hidden_state(bt):
             rows = slice(bt * P, (bt + 1) * P)
             gate_o = slabs[(bt, GATES + 3)]
-            nc.vector.tensor_tensor(out=gate_o[:], in0=gate_o[:], in1=slabs[(bt, "tanh_cy")][:], op=ALU.mult)
-            nc.sync.dma_start(out=out_0[rows, :], in_=gate_o[:])
+            for half in range(HALVES):
+                cols = slice(half * BANK, (half + 1) * BANK)
+                nc.vector.tensor_tensor(out=gate_o[:, cols], in0=gate_o[:, cols], in1=slabs[(bt, GATES + 2)][:, cols], op=ALU.mult)
+                nc.sync.dma_start(out=out_0[rows, cols], in_=gate_o[:, cols])
 
         load_batch_tile(0)
         load_slab_weights(0)
         load_scale_planes(0)
         nc.sync.dma_start(out=input_bias_rows[0:GATES, :], in_=b_ih.rearrange("(g n) -> g n", g=GATES))
         turn_activations(0)
+        copy_activations(0)
         turn_embeddings(0)
+        copy_embeddings(0)
         quantise_activations(0)
         load_slab_weights(1)
         turn_hyper_weights(0)
@@ -480,20 +573,44 @@ def tile_adaptivelstmcell_pb_kernel(
         turn_hyper_weights(1)
         slab_matmuls(0)
 
-        for n in range(ALL_SLABS + SLABS + 1):
+        last = BATCH_TILES - 1
+        for n in range(ALL_SLABS):
             bt, k = divmod(n, SLABS)
             tail = bt - 1
-            if n < ALL_SLABS:
-                slab_combine(n)
+            has_tail = tail >= 0
+            has_next = bt < last
+            slab_combine(n)
             if n + 1 < ALL_SLABS:
                 slab_matmuls(n + 1)
-            if 1 <= k <= GATES and bt < BATCH_TILES:
+
+            if k == 0 and tail >= 1:
+                activate(tail - 1, GATE_O, 0)
+                activate(tail - 1, GATE_O, 1)
+            if has_tail:
+                if k == 1:
+                    gain_and_shift(tail, GATE_F, 0)
+                if k == 2:
+                    gain_and_shift(tail, GATE_F, 1)
+                if k == 3:
+                    activate(tail, GATE_F, 0)
+                    activate(tail, GATE_F, 1)
+                if k == 6:
+                    gain_and_shift(tail, GATE_O, 0)
+                if k == 7:
+                    gain_and_shift(tail, GATE_O, 1)
+            if has_next:
+                if k == 4:
+                    copy_activations(bt + 1)
+                if k == 5:
+                    copy_embeddings(bt + 1)
+
+            if 1 <= k <= GATES:
                 slab_squares(n - 1)
-            if k == SLABS - 1 and bt < BATCH_TILES:
+            if k == SLABS - 1:
                 row_means(bt)
-            if k >= GATES and bt < BATCH_TILES:
+            if k >= GATES:
                 slab_squares(n)
-            if k == SLABS - 1 and bt < BATCH_TILES:
+            if k == SLABS - 1:
                 row_inverse_deviations(bt)
 
             if n == 0:
@@ -505,42 +622,105 @@ def tile_adaptivelstmcell_pb_kernel(
             if n < GATES:
                 hidden_bias_share(n)
             if n == SLABS - 4:
-                for gate in range(GATES):
+                load_vector_rows()
+                for gate in ROW_GATES:
                     load_shifts(gate)
             if n == SLABS - 3:
                 load_gains()
-            if n == SLABS - 3 or n == SLABS - 2:
-                add_shifts(2 * (n - SLABS + 3))
-                add_shifts(2 * (n - SLABS + 3) + 1)
+                for gate in ROW_GATES:
+                    add_shifts(gate)
+            if n == SLABS - 2:
+                turn_vectors()
 
-            if bt + 1 < BATCH_TILES:
+            if k == 0 and has_next:
+                load_batch_tile(bt + 1)
+            if k == 0 and has_tail:
+                load_cell_state(tail)
+            if k == 1 and bt == last:
+                load_cell_state(last)
+
+            if has_tail and k == 0:
+                normalise(tail, GATE_F)
+            if has_tail and k == 5:
+                normalise(tail, GATE_O)
+
+            if has_tail:
                 if k == 0:
-                    load_batch_tile(bt + 1)
+                    turn_forward(tail, GATE_F, 0)
+                if k == 1:
+                    turn_forward(tail, GATE_F, 1)
                 if k == 2:
-                    turn_activations(bt + 1)
+                    turn_back(tail, GATE_F, 0)
+                    turn_back(tail, GATE_F, 1)
+                if k == 5:
+                    turn_forward(tail, GATE_O, 0)
+                if k == 6:
+                    turn_forward(tail, GATE_O, 1)
+                if k == 7:
+                    turn_back(tail, GATE_O, 0)
+                    turn_back(tail, GATE_O, 1)
+            if has_next:
                 if k == 3:
+                    turn_activations(bt + 1)
+                if k == 4:
                     turn_embeddings(bt + 1)
 
-            if k == 0 and bt >= 2:
-                hidden_state(bt - 2)
-            if 0 <= tail < BATCH_TILES:
-                product_engine = nc.vector if tail == BATCH_TILES - 1 else nc.gpsimd
-                if k == 0:
-                    load_cell_state(tail)
-                    center_and_gain(tail, 0)
+            if k == 0 and tail >= 1:
+                hidden_state(tail - 1)
+            if has_tail:
                 if k == 1:
-                    center_and_gain(tail, 1)
+                    center_and_gain(tail, 0, 0)
+                    center_and_gain(tail, 0, 1)
                 if k == 2:
-                    scale_and_add(tail, 0)
+                    center_and_gain(tail, 1, 0)
+                    center_and_gain(tail, 1, 1)
                 if k == 3:
-                    scale_and_add(tail, 1)
+                    scale_and_add(tail, 0, 0)
+                    scale_and_add(tail, 1, 0)
                 if k == 4:
-                    cell_products(tail, True, product_engine)
+                    scale_and_add(tail, 0, 1)
+                    scale_and_add(tail, 1, 1)
+                    cell_products(tail, False, nc.gpsimd)
                 if k == 5:
-                    cell_products(tail, False, product_engine)
+                    cell_products(tail, True, nc.gpsimd)
                 if k == 6:
                     cell_sum(tail)
                 if k == 7:
                     cell_norm(tail)
-            if k == 2 and bt + 1 < BATCH_TILES:
+            if k == 5 and has_next:
                 quantise_activations(bt + 1)
+
+        activate(last - 1, GATE_O, 0)
+        activate(last - 1, GATE_O, 1)
+        normalise(last, GATE_F)
+        normalise(last, GATE_O)
+        turn_forward(last, GATE_F, 0, ("alpha", "alpha"))
+        turn_forward(last, GATE_F, 1, ("xh", "xh"))
+        turn_forward(last, GATE_O, 0, ("beta", "beta"))
+        turn_forward(last, GATE_O, 1, ("turn", "turn"))
+        hidden_state(last - 1)
+        gain_and_shift(last, GATE_F, 0)
+        gain_and_shift(last, GATE_F, 1)
+        turn_back(last, GATE_F, 0, "alpha")
+        turn_back(last, GATE_F, 1, "alpha")
+        center_and_gain(last, 0, 0)
+        center_and_gain(last, 0, 1)
+        center_and_gain(last, 1, 0)
+        center_and_gain(last, 1, 1)
+        gain_and_shift(last, GATE_O, 0)
+        activate(last, GATE_F, 0)
+        activate(last, GATE_F, 1)
+        gain_and_shift(last, GATE_O, 1)
+        turn_back(last, GATE_O, 0, "xh")
+        turn_back(last, GATE_O, 1, "xh")
+        scale_and_add(last, 0, 0)
+        scale_and_add(last, 1, 0)
+        scale_and_add(last, 0, 1)
+        scale_and_add(last, 1, 1)
+        cell_products(last, False, nc.vector)
+        cell_products(last, True, nc.vector)
+        activate(last, GATE_O, 0)
+        activate(last, GATE_O, 1)
+        cell_sum(last)
+        cell_norm(last)
+        hidden_state(last)

@@ -31,9 +31,19 @@ SLABS = PATHS * GATES
 ALL_SLABS = BATCH_TILES * SLABS
 EPS = 1e-5
 QUARTERS = BANK // P
+GATE_I = 0
+GATE_J = 1
 GATE_F = 2
 GATE_O = 3
-ROW_GATES = (0, 1)
+LOAD_AHEAD = 4
+TURN_AHEAD = 3
+
+
+def PRODUCT_ENGINE(nc):
+    return nc.gpsimd
+
+
+ROW_GATES = (GATE_J, GATE_F)
 
 FLOPS = 2 * BATCH * WIDTH * ROW * PATHS + 2 * SLABS * 2 * BATCH * EMB * WIDTH
 
@@ -72,7 +82,7 @@ def tile_adaptivelstmcell_pb_kernel(
         const = ctx.enter_context(tc.tile_pool(name="const", bufs=1))
         raw_pool = ctx.enter_context(tc.tile_pool(name="raw", bufs=11))
         operand_pool = ctx.enter_context(tc.tile_pool(name="operand", bufs=2))
-        slab_pool = ctx.enter_context(tc.tile_pool(name="slab", bufs=12))
+        slab_pool = ctx.enter_context(tc.tile_pool(name="slab", bufs=14))
         alpha_pool = ctx.enter_context(tc.tile_pool(name="alpha", bufs=2))
         unread_pool = ctx.enter_context(tc.tile_pool(name="unread", bufs=2))
         stat_pool = ctx.enter_context(tc.tile_pool(name="stat", bufs=2))
@@ -169,12 +179,16 @@ def tile_adaptivelstmcell_pb_kernel(
             if path == 0:
                 nc.sync.dma_start(out=hidden_bias_rep[:, cols], in_=b_hh[cols].partition_broadcast(P))
 
+        def row_cols(gate):
+            place = ROW_GATES.index(gate)
+            return slice(place * WIDTH, (place + 1) * WIDTH)
+
         def load_gains():
             for gate in ROW_GATES:
                 cols = slice(gate * WIDTH, (gate + 1) * WIDTH)
                 for path in range(PATHS):
                     nc.sync.dma_start(
-                        out=gain_rep[:, path, cols], in_=path_gain[path][cols].partition_broadcast(P)
+                        out=gain_rep[:, path, row_cols(gate)], in_=path_gain[path][cols].partition_broadcast(P)
                     )
             nc.sync.dma_start(out=cell_gain_rep[:], in_=ln_c_w.partition_broadcast(P))
             nc.sync.dma_start(out=cell_shift_rep[:], in_=ln_c_b.partition_broadcast(P))
@@ -187,9 +201,8 @@ def tile_adaptivelstmcell_pb_kernel(
                 raw[(gate, "shift%d" % path)] = loaded
 
         def add_shifts(gate):
-            cols = slice(gate * WIDTH, (gate + 1) * WIDTH)
             nc.gpsimd.tensor_tensor(
-                out=shift_rep[:, cols], in0=raw[(gate, "shift0")][:], in1=raw[(gate, "shift1")][:], op=ALU.add
+                out=shift_rep[:, row_cols(gate)], in0=raw[(gate, "shift0")][:], in1=raw[(gate, "shift1")][:], op=ALU.add
             )
 
         def turn_activations(bt):
@@ -251,19 +264,24 @@ def tile_adaptivelstmcell_pb_kernel(
             nc.tensor.transpose(out=turned[:], in_=vector_rows[:], identity=ident_bf16[:])
             nc.scalar.copy(out=vector_cols[:], in_=turned[:])
             blocks = ROW // P
-            nc.vector.tensor_tensor(
+            nc.gpsimd.tensor_tensor(
                 out=shift_cols[:], in0=vector_cols[:, 2 * blocks : 3 * blocks], in1=vector_cols[:, 3 * blocks : 4 * blocks], op=ALU.add
             )
 
         def turn_hyper_weights(slot):
-            turned_alpha = psum.tile([P, BLOCKS, P], BF16, name="turned_alpha_w", tag="turn")
-            for blk in range(BLOCKS):
-                nc.tensor.transpose(out=turned_alpha[:, blk, :], in_=raw[(slot, "alpha_w")][:, blk, :], identity=ident_bf16[:])
-            nc.vector.tensor_copy(out=alpha_wT[:, slot, :], in_=turned_alpha[:].rearrange("a blk p -> a (blk p)"))
-            turned_beta = psum.tile([P, BLOCKS, P], BF16, name="turned_beta_w", tag="turn")
-            for blk in range(BLOCKS):
-                nc.tensor.transpose(out=turned_beta[:, blk, :], in_=raw[(slot, "beta_w")][:, blk, :], identity=ident_bf16[:])
-            nc.scalar.copy(out=beta_wT[:, slot, :], in_=turned_beta[:].rearrange("a blk p -> a (blk p)"))
+            for key in ("alpha_w", "beta_w"):
+                turned = psum.tile([P, BLOCKS, P], BF16, name="turned_" + key, tag="turn")
+                for blk in range(BLOCKS):
+                    nc.tensor.transpose(out=turned[:, blk, :], in_=raw[(slot, key)][:, blk, :], identity=ident_bf16[:])
+                operands[(slot, "turned_" + key)] = turned
+
+        def copy_hyper_weights(slot):
+            nc.vector.tensor_copy(
+                out=alpha_wT[:, slot, :], in_=operands[(slot, "turned_alpha_w")][:].rearrange("a blk p -> a (blk p)")
+            )
+            nc.scalar.copy(
+                out=beta_wT[:, slot, :], in_=operands[(slot, "turned_beta_w")][:].rearrange("a blk p -> a (blk p)")
+            )
 
         def slab_matmuls(n):
             bt, slot = divmod(n, SLABS)
@@ -412,7 +430,7 @@ def tile_adaptivelstmcell_pb_kernel(
                 out=pre[:],
                 in0=pre[:],
                 scalar=stats[(bt, "mean")][:, path : path + 1],
-                in1=gain_rep[:, path, gate * WIDTH : (gate + 1) * WIDTH],
+                in1=gain_rep[:, path, row_cols(gate)],
                 op0=ALU.subtract,
                 op1=ALU.mult,
             )
@@ -424,7 +442,7 @@ def tile_adaptivelstmcell_pb_kernel(
                 out=pre[:],
                 in0=pre[:],
                 scalar=inverse[:, path : path + 1],
-                in1=(shift_rep[:, gate * WIDTH : (gate + 1) * WIDTH] if path == 0 else slabs[(bt, gate)][:]),
+                in1=(shift_rep[:, row_cols(gate)] if path == 0 else slabs[(bt, gate)][:]),
                 op0=ALU.mult,
                 op1=ALU.add,
             )
@@ -569,40 +587,96 @@ def tile_adaptivelstmcell_pb_kernel(
         quantise_activations(0)
         load_slab_weights(1)
         turn_hyper_weights(0)
+        copy_hyper_weights(0)
         load_slab_weights(2)
         turn_hyper_weights(1)
+        copy_hyper_weights(1)
+        for slot in range(3, LOAD_AHEAD):
+            load_slab_weights(slot)
         slab_matmuls(0)
+        turn_hyper_weights(2)
 
         last = BATCH_TILES - 1
+        product_engine = PRODUCT_ENGINE(nc)
+
+        def scalar_empties(t, r):
+            if r == 2:
+                gain_and_shift(t, GATE_I, 0)
+            if r == 3:
+                gain_and_shift(t, GATE_I, 1)
+            if r == 4:
+                activate(t, GATE_I, 0)
+                activate(t, GATE_I, 1)
+            if r == 7:
+                gain_and_shift(t, GATE_O, 0)
+            if r == 8:
+                gain_and_shift(t, GATE_O, 1)
+            if r == 9:
+                activate(t, GATE_O, 0)
+                activate(t, GATE_O, 1)
+
+        def vector_before(t, r):
+            if r == 1:
+                normalise(t, GATE_I)
+            if r == 6:
+                scale_and_add(t, GATE_J, 1)
+                cell_products(t, True, product_engine)
+                normalise(t, GATE_O)
+
+        def tensor_turns(t, r):
+            if r == 1:
+                turn_forward(t, GATE_I, 0)
+            if r == 2:
+                turn_forward(t, GATE_I, 1)
+            if r == 3:
+                turn_back(t, GATE_I, 0)
+                turn_back(t, GATE_I, 1)
+            if r == 6:
+                turn_forward(t, GATE_O, 0)
+            if r == 7:
+                turn_forward(t, GATE_O, 1)
+            if r == 8:
+                turn_back(t, GATE_O, 0)
+                turn_back(t, GATE_O, 1)
+
+        def vector_after(t, r):
+            if r == 2:
+                center_and_gain(t, GATE_F, 0)
+                center_and_gain(t, GATE_F, 1)
+            if r == 3:
+                center_and_gain(t, GATE_J, 0)
+                center_and_gain(t, GATE_J, 1)
+            if r == 4:
+                scale_and_add(t, GATE_F, 0)
+                scale_and_add(t, GATE_J, 0)
+            if r == 5:
+                scale_and_add(t, GATE_F, 1)
+                cell_products(t, False, product_engine)
+            if r == 7:
+                cell_sum(t)
+            if r == 8:
+                cell_norm(t)
+            if r == 9:
+                hidden_state(t)
+
         for n in range(ALL_SLABS):
             bt, k = divmod(n, SLABS)
-            tail = bt - 1
-            has_tail = tail >= 0
             has_next = bt < last
+            tails = [(t, n - SLABS * (t + 1)) for t in (bt - 2, bt - 1) if t >= 0]
+            first_turn = 5 if bt == 0 else 4
             slab_combine(n)
+
+            for t, r in tails:
+                scalar_empties(t, r)
+            if n + 2 < SLABS:
+                copy_hyper_weights(n + 2)
+            if has_next:
+                if k == first_turn + 1:
+                    copy_activations(bt + 1)
+                if k == first_turn + 2:
+                    copy_embeddings(bt + 1)
             if n + 1 < ALL_SLABS:
                 slab_matmuls(n + 1)
-
-            if k == 0 and tail >= 1:
-                activate(tail - 1, GATE_O, 0)
-                activate(tail - 1, GATE_O, 1)
-            if has_tail:
-                if k == 1:
-                    gain_and_shift(tail, GATE_F, 0)
-                if k == 2:
-                    gain_and_shift(tail, GATE_F, 1)
-                if k == 3:
-                    activate(tail, GATE_F, 0)
-                    activate(tail, GATE_F, 1)
-                if k == 6:
-                    gain_and_shift(tail, GATE_O, 0)
-                if k == 7:
-                    gain_and_shift(tail, GATE_O, 1)
-            if has_next:
-                if k == 4:
-                    copy_activations(bt + 1)
-                if k == 5:
-                    copy_embeddings(bt + 1)
 
             if 1 <= k <= GATES:
                 slab_squares(n - 1)
@@ -615,10 +689,10 @@ def tile_adaptivelstmcell_pb_kernel(
 
             if n == 0:
                 load_scale_planes(1)
-            if n + 3 < SLABS:
-                load_slab_weights(n + 3)
-            if n + 2 < SLABS:
-                turn_hyper_weights(n + 2)
+            if n + LOAD_AHEAD < SLABS:
+                load_slab_weights(n + LOAD_AHEAD)
+            if n + TURN_AHEAD < SLABS:
+                turn_hyper_weights(n + TURN_AHEAD)
             if n < GATES:
                 hidden_bias_share(n)
             if n == SLABS - 4:
@@ -629,94 +703,62 @@ def tile_adaptivelstmcell_pb_kernel(
                 load_gains()
                 for gate in ROW_GATES:
                     add_shifts(gate)
-            if n == SLABS - 2:
+            if n == SLABS - 1:
                 turn_vectors()
 
             if k == 0 and has_next:
                 load_batch_tile(bt + 1)
-            if k == 0 and has_tail:
-                load_cell_state(tail)
+            if k == 0 and bt >= 1:
+                load_cell_state(bt - 1)
             if k == 1 and bt == last:
                 load_cell_state(last)
 
-            if has_tail and k == 0:
-                normalise(tail, GATE_F)
-            if has_tail and k == 5:
-                normalise(tail, GATE_O)
-
-            if has_tail:
-                if k == 0:
-                    turn_forward(tail, GATE_F, 0)
-                if k == 1:
-                    turn_forward(tail, GATE_F, 1)
-                if k == 2:
-                    turn_back(tail, GATE_F, 0)
-                    turn_back(tail, GATE_F, 1)
-                if k == 5:
-                    turn_forward(tail, GATE_O, 0)
-                if k == 6:
-                    turn_forward(tail, GATE_O, 1)
-                if k == 7:
-                    turn_back(tail, GATE_O, 0)
-                    turn_back(tail, GATE_O, 1)
+            for t, r in tails:
+                vector_before(t, r)
+            for t, r in tails:
+                tensor_turns(t, r)
             if has_next:
-                if k == 3:
+                if k == first_turn:
                     turn_activations(bt + 1)
-                if k == 4:
+                if k == first_turn + 1:
                     turn_embeddings(bt + 1)
-
-            if k == 0 and tail >= 1:
-                hidden_state(tail - 1)
-            if has_tail:
-                if k == 1:
-                    center_and_gain(tail, 0, 0)
-                    center_and_gain(tail, 0, 1)
-                if k == 2:
-                    center_and_gain(tail, 1, 0)
-                    center_and_gain(tail, 1, 1)
-                if k == 3:
-                    scale_and_add(tail, 0, 0)
-                    scale_and_add(tail, 1, 0)
-                if k == 4:
-                    scale_and_add(tail, 0, 1)
-                    scale_and_add(tail, 1, 1)
-                    cell_products(tail, False, nc.gpsimd)
-                if k == 5:
-                    cell_products(tail, True, nc.gpsimd)
-                if k == 6:
-                    cell_sum(tail)
-                if k == 7:
-                    cell_norm(tail)
-            if k == 5 and has_next:
+            for t, r in tails:
+                vector_after(t, r)
+            if k == first_turn + 1 and has_next:
                 quantise_activations(bt + 1)
 
-        activate(last - 1, GATE_O, 0)
-        activate(last - 1, GATE_O, 1)
-        normalise(last, GATE_F)
+        before = last - 1
+        gain_and_shift(before, GATE_O, 1)
+        turn_back(before, GATE_O, 0)
+        turn_back(before, GATE_O, 1)
+        center_and_gain(last, GATE_F, 0)
+        center_and_gain(last, GATE_F, 1)
+        normalise(last, GATE_I)
         normalise(last, GATE_O)
-        turn_forward(last, GATE_F, 0, ("alpha", "alpha"))
-        turn_forward(last, GATE_F, 1, ("xh", "xh"))
+        turn_forward(last, GATE_I, 0, ("alpha", "alpha"))
+        turn_forward(last, GATE_I, 1, ("xh", "xh"))
         turn_forward(last, GATE_O, 0, ("beta", "beta"))
+        cell_norm(before)
+        activate(before, GATE_O, 0)
+        activate(before, GATE_O, 1)
         turn_forward(last, GATE_O, 1, ("turn", "turn"))
-        hidden_state(last - 1)
-        gain_and_shift(last, GATE_F, 0)
-        gain_and_shift(last, GATE_F, 1)
-        turn_back(last, GATE_F, 0, "alpha")
-        turn_back(last, GATE_F, 1, "alpha")
-        center_and_gain(last, 0, 0)
-        center_and_gain(last, 0, 1)
-        center_and_gain(last, 1, 0)
-        center_and_gain(last, 1, 1)
+        gain_and_shift(last, GATE_I, 0)
+        gain_and_shift(last, GATE_I, 1)
+        turn_back(last, GATE_I, 0, "alpha")
+        turn_back(last, GATE_I, 1, "alpha")
+        center_and_gain(last, GATE_J, 0)
+        center_and_gain(last, GATE_J, 1)
+        hidden_state(before)
         gain_and_shift(last, GATE_O, 0)
-        activate(last, GATE_F, 0)
-        activate(last, GATE_F, 1)
+        activate(last, GATE_I, 0)
+        activate(last, GATE_I, 1)
         gain_and_shift(last, GATE_O, 1)
         turn_back(last, GATE_O, 0, "xh")
         turn_back(last, GATE_O, 1, "xh")
-        scale_and_add(last, 0, 0)
-        scale_and_add(last, 1, 0)
-        scale_and_add(last, 0, 1)
-        scale_and_add(last, 1, 1)
+        scale_and_add(last, GATE_F, 0)
+        scale_and_add(last, GATE_J, 0)
+        scale_and_add(last, GATE_F, 1)
+        scale_and_add(last, GATE_J, 1)
         cell_products(last, False, nc.vector)
         cell_products(last, True, nc.vector)
         activate(last, GATE_O, 0)

@@ -35,6 +35,7 @@ GATE_I = 0
 GATE_J = 1
 GATE_F = 2
 GATE_O = 3
+INPUT_GAIN_ON_VECTOR = False
 LOAD_AHEAD = 4
 TURN_AHEAD = 3
 
@@ -86,7 +87,7 @@ def tile_adaptivelstmcell_pb_kernel(
         alpha_pool = ctx.enter_context(tc.tile_pool(name="alpha", bufs=2))
         unread_pool = ctx.enter_context(tc.tile_pool(name="unread", bufs=2))
         stat_pool = ctx.enter_context(tc.tile_pool(name="stat", bufs=2))
-        scaled_pool = ctx.enter_context(tc.tile_pool(name="scaled", bufs=4))
+        scaled_pool = ctx.enter_context(tc.tile_pool(name="scaled", bufs=6))
         psum = ctx.enter_context(tc.psum_pool(name="psum", bufs=2))
         ctx.enter_context(tc.manual_schedule())
 
@@ -435,7 +436,7 @@ def tile_adaptivelstmcell_pb_kernel(
                 op1=ALU.mult,
             )
 
-        def scale_and_add(bt, gate, path):
+        def scale_and_add(bt, gate, path, then_activate=True):
             inverse = stats[(bt, "inverse")]
             pre = slabs[(bt, path * GATES + gate)]
             nc.vector.scalar_tensor_tensor(
@@ -446,8 +447,12 @@ def tile_adaptivelstmcell_pb_kernel(
                 op0=ALU.mult,
                 op1=ALU.add,
             )
-            if path == 1:
-                nc.scalar.activation(out=pre[:], in_=pre[:], func=(FUNC.Tanh if gate == 1 else FUNC.Sigmoid))
+            if path == 1 and then_activate:
+                row_activate(bt, gate)
+
+        def row_activate(bt, gate):
+            pre = slabs[(bt, GATES + gate)]
+            nc.scalar.activation(out=pre[:], in_=pre[:], func=(FUNC.Tanh if gate == GATE_J else FUNC.Sigmoid))
 
         def normalise(bt, gate):
             for path in range(PATHS):
@@ -470,29 +475,34 @@ def tile_adaptivelstmcell_pb_kernel(
                     nc.tensor.transpose(out=turned[:, q, :], in_=pre[:, first : first + P], identity=ident_f32[:])
                 turned_slabs[(bt, gate, half, path)] = turned
 
-        def gain_and_shift(bt, gate, half):
+        def gain_and_shift(bt, gate, half, paths=(0, 1), on_vector=INPUT_GAIN_ON_VECTOR):
             blocks = ROW // P
-            for path in range(PATHS):
+            first = gate * BLOCKS + half * QUARTERS
+            for path in paths:
                 turned = turned_slabs[(bt, gate, half, path)]
                 scaled = scaled_pool.tile([P, QUARTERS, P], F32, name="scaled")
-                for q in range(QUARTERS):
-                    col = gate * BLOCKS + half * QUARTERS + q
-                    gain_col = (1 - path) * blocks + col
-                    if path == 0:
-                        nc.scalar.activation(
-                            out=scaled[:, q, :],
-                            in_=turned[:, q, :],
-                            func=FUNC.Identity,
-                            scale=vector_cols[:, gain_col : gain_col + 1],
-                            bias=shift_cols[:, col : col + 1],
-                        )
-                    else:
-                        nc.scalar.activation(
-                            out=scaled[:, q, :],
-                            in_=turned[:, q, :],
-                            func=FUNC.Identity,
-                            scale=vector_cols[:, gain_col : gain_col + 1],
-                        )
+                if path == 1 and on_vector:
+                    nc.vector.tensor_tensor(
+                        out=scaled[:],
+                        in0=turned[:],
+                        in1=vector_cols[:, first : first + QUARTERS].unsqueeze(2).to_broadcast([P, QUARTERS, P]),
+                        op=ALU.mult,
+                    )
+                else:
+                    for q in range(QUARTERS):
+                        col = (1 - path) * blocks + first + q
+                        if path == 0:
+                            nc.scalar.activation(
+                                out=scaled[:, q, :],
+                                in_=turned[:, q, :],
+                                func=FUNC.Identity,
+                                scale=vector_cols[:, col : col + 1],
+                                bias=shift_cols[:, first + q : first + q + 1],
+                            )
+                        else:
+                            nc.scalar.activation(
+                                out=scaled[:, q, :], in_=turned[:, q, :], func=FUNC.Identity, scale=vector_cols[:, col : col + 1]
+                            )
                 scaled_slabs[(bt, gate, half, path)] = scaled
 
         def turn_back(bt, gate, half, tag="turn"):
@@ -513,7 +523,7 @@ def tile_adaptivelstmcell_pb_kernel(
             nc.scalar.activation(
                 out=slabs[(bt, GATES + gate)][:, half * BANK : (half + 1) * BANK],
                 in_=summed_slabs[(bt, gate, half)][:],
-                func=FUNC.Sigmoid,
+                func=(FUNC.Tanh if gate == GATE_J else FUNC.Sigmoid),
             )
 
         def cell_products(bt, first, engine):
@@ -599,6 +609,9 @@ def tile_adaptivelstmcell_pb_kernel(
         last = BATCH_TILES - 1
         product_engine = PRODUCT_ENGINE(nc)
 
+        def o_round(t):
+            return 4 if t == last - 1 else 6
+
         def scalar_empties(t, r):
             if r == 2:
                 gain_and_shift(t, GATE_I, 0)
@@ -607,11 +620,11 @@ def tile_adaptivelstmcell_pb_kernel(
             if r == 4:
                 activate(t, GATE_I, 0)
                 activate(t, GATE_I, 1)
-            if r == 7:
+            if r == o_round(t) + 1:
                 gain_and_shift(t, GATE_O, 0)
-            if r == 8:
+            if r == o_round(t) + 2:
                 gain_and_shift(t, GATE_O, 1)
-            if r == 9:
+            if r == o_round(t) + 3:
                 activate(t, GATE_O, 0)
                 activate(t, GATE_O, 1)
 
@@ -621,6 +634,7 @@ def tile_adaptivelstmcell_pb_kernel(
             if r == 6:
                 scale_and_add(t, GATE_J, 1)
                 cell_products(t, True, product_engine)
+            if r == o_round(t):
                 normalise(t, GATE_O)
 
         def tensor_turns(t, r):
@@ -631,11 +645,11 @@ def tile_adaptivelstmcell_pb_kernel(
             if r == 3:
                 turn_back(t, GATE_I, 0)
                 turn_back(t, GATE_I, 1)
-            if r == 6:
+            if r == o_round(t):
                 turn_forward(t, GATE_O, 0)
-            if r == 7:
+            if r == o_round(t) + 1:
                 turn_forward(t, GATE_O, 1)
-            if r == 8:
+            if r == o_round(t) + 2:
                 turn_back(t, GATE_O, 0)
                 turn_back(t, GATE_O, 1)
 
@@ -652,7 +666,7 @@ def tile_adaptivelstmcell_pb_kernel(
             if r == 5:
                 scale_and_add(t, GATE_F, 1)
                 cell_products(t, False, product_engine)
-            if r == 7:
+            if r == 7 and t < last - 1:
                 cell_sum(t)
             if r == 8:
                 cell_norm(t)
@@ -728,41 +742,51 @@ def tile_adaptivelstmcell_pb_kernel(
                 quantise_activations(bt + 1)
 
         before = last - 1
-        gain_and_shift(before, GATE_O, 1)
-        turn_back(before, GATE_O, 0)
-        turn_back(before, GATE_O, 1)
+        free_tags = ["alpha", "alpha", "xh", "xh", "beta", "beta", "turn", "turn"]
+
+        def next_tags(count):
+            taken = free_tags[:count]
+            free_tags.extend(taken)
+            for tag in taken:
+                free_tags.remove(tag)
+            return taken
+
         center_and_gain(last, GATE_F, 0)
         center_and_gain(last, GATE_F, 1)
+        cell_sum(before)
         normalise(last, GATE_I)
+        normalise(last, GATE_J)
+        for gate in (GATE_I, GATE_J):
+            for half in range(HALVES):
+                turn_forward(last, gate, half, next_tags(2))
+        scale_and_add(last, GATE_F, 0)
+        gain_and_shift(last, GATE_I, 0, on_vector=True)
+        gain_and_shift(last, GATE_I, 1, on_vector=True)
+        turn_back(last, GATE_I, 0, next_tags(1)[0])
+        turn_back(last, GATE_I, 1, next_tags(1)[0])
+        scale_and_add(last, GATE_F, 1, then_activate=False)
+        gain_and_shift(last, GATE_J, 0, on_vector=True)
+        gain_and_shift(last, GATE_J, 1, on_vector=True)
+        turn_back(last, GATE_J, 0, next_tags(1)[0])
+        turn_back(last, GATE_J, 1, next_tags(1)[0])
+        row_activate(last, GATE_F)
         normalise(last, GATE_O)
-        turn_forward(last, GATE_I, 0, ("alpha", "alpha"))
-        turn_forward(last, GATE_I, 1, ("xh", "xh"))
-        turn_forward(last, GATE_O, 0, ("beta", "beta"))
-        cell_norm(before)
-        activate(before, GATE_O, 0)
-        activate(before, GATE_O, 1)
-        turn_forward(last, GATE_O, 1, ("turn", "turn"))
-        gain_and_shift(last, GATE_I, 0)
-        gain_and_shift(last, GATE_I, 1)
-        turn_back(last, GATE_I, 0, "alpha")
-        turn_back(last, GATE_I, 1, "alpha")
-        center_and_gain(last, GATE_J, 0)
-        center_and_gain(last, GATE_J, 1)
-        hidden_state(before)
-        gain_and_shift(last, GATE_O, 0)
+        for half in range(HALVES):
+            turn_forward(last, GATE_O, half, next_tags(2))
         activate(last, GATE_I, 0)
         activate(last, GATE_I, 1)
-        gain_and_shift(last, GATE_O, 1)
-        turn_back(last, GATE_O, 0, "xh")
-        turn_back(last, GATE_O, 1, "xh")
-        scale_and_add(last, GATE_F, 0)
-        scale_and_add(last, GATE_J, 0)
-        scale_and_add(last, GATE_F, 1)
-        scale_and_add(last, GATE_J, 1)
         cell_products(last, False, nc.vector)
+        activate(last, GATE_J, 0)
+        activate(last, GATE_J, 1)
         cell_products(last, True, nc.vector)
+        cell_sum(last)
+        gain_and_shift(last, GATE_O, 0, on_vector=True)
+        gain_and_shift(last, GATE_O, 1, on_vector=True)
+        turn_back(last, GATE_O, 0, next_tags(1)[0])
+        turn_back(last, GATE_O, 1, next_tags(1)[0])
+        cell_norm(before)
         activate(last, GATE_O, 0)
         activate(last, GATE_O, 1)
-        cell_sum(last)
+        hidden_state(before)
         cell_norm(last)
         hidden_state(last)

@@ -111,7 +111,9 @@ def tile_adaptivelstmcell_pb_kernel(
 
         alpha_wT = const.tile([P, SLABS, WIDTH], BF16, name="alpha_wT")
         beta_wT = const.tile([P, SLABS, WIDTH], BF16, name="beta_wT")
-        hidden_bias_rep = const.tile([P, ROW], BF16, name="hidden_bias_rep")
+        hidden_bias_rows = const.tile([P, P], BF16, name="hidden_bias_rows")
+        nc.gpsimd.memset(hidden_bias_rows[:], 0.0)
+        hidden_bias_cols = const.tile([P, P], F32, name="hidden_bias_cols")
         gain_rep = const.tile([P, PATHS, len(ROW_GATES) * WIDTH], BF16, name="gain_rep")
         shift_rep = const.tile([P, len(ROW_GATES) * WIDTH], F32, name="shift_rep")
         vector_rows = const.tile([P, P], BF16, name="vector_rows")
@@ -121,11 +123,6 @@ def tile_adaptivelstmcell_pb_kernel(
         cell_shift_rep = const.tile([P, WIDTH], BF16, name="cell_shift_rep")
         input_bias_rows = const.tile([P, WIDTH], BF16, name="input_bias_rows")
         nc.gpsimd.memset(input_bias_rows[:], 0.0)
-
-        bias_share = const.tile([P, PATHS], F32, name="bias_share")
-        nc.vector.memset(bias_share[:], 0.0)
-        bias_share_parts = const.tile([P, GATES], F32, name="bias_share_parts")
-        bias_share_unread = const.tile([P, GATES], F32, name="bias_share_unread")
 
         raw = {}
         operands = {}
@@ -164,7 +161,6 @@ def tile_adaptivelstmcell_pb_kernel(
 
         def load_slab_weights(slot):
             path, gate = divmod(slot, GATES)
-            cols = slice(gate * WIDTH, (gate + 1) * WIDTH)
             byte_cols = slice(2 * gate * WIDTH, 2 * (gate + 1) * WIDTH)
             for key, source in (("alpha_w", norm_alpha_w), ("beta_w", bias_beta_w)):
                 loaded = raw_pool.tile([P, BLOCKS, EMB], BF16, name="raw_" + key, tag="raw")
@@ -177,8 +173,6 @@ def tile_adaptivelstmcell_pb_kernel(
                     out=words[path][:, g, byte_cols].bitcast(I32),
                     in_=path_words[path][g, :, byte_cols].bitcast(I32),
                 )
-            if path == 0:
-                nc.sync.dma_start(out=hidden_bias_rep[:, cols], in_=b_hh[cols].partition_broadcast(P))
 
         def row_cols(gate):
             place = ROW_GATES.index(gate)
@@ -319,8 +313,19 @@ def tile_adaptivelstmcell_pb_kernel(
                     lhsT=operands[(bt, "zb")][:, slot, :],
                     rhs=beta_wT[:, slot, half * BANK : (half + 1) * BANK],
                     start=True,
-                    stop=(path == 0),
+                    stop=False,
                 )
+                if path == 0:
+                    for q in range(QUARTERS):
+                        col = gate * BLOCKS + half * QUARTERS + q
+                        nc.tensor.matmul(
+                            bank[:, q * P : (q + 1) * P],
+                            lhsT=hidden_bias_cols[:, col : col + 1].to_broadcast([P, P]),
+                            rhs=ident_f32[:],
+                            is_transpose=True,
+                            start=False,
+                            stop=(q == QUARTERS - 1),
+                        )
                 if path == 1:
                     nc.tensor.matmul(
                         bank[:],
@@ -359,10 +364,6 @@ def tile_adaptivelstmcell_pb_kernel(
                     op1=ALU.add,
                     accum_out=stats[(bt, "sum_parts")][:, path, part : part + 1],
                 )
-            if path == 0:
-                nc.gpsimd.tensor_tensor(
-                    out=pre[:], in0=pre[:], in1=hidden_bias_rep[:, gate * WIDTH : (gate + 1) * WIDTH], op=ALU.add
-                )
             slabs[(bt, slot)] = pre
 
         def slab_squares(n):
@@ -388,22 +389,7 @@ def tile_adaptivelstmcell_pb_kernel(
                     in_=stats[(bt, "sum_parts")][:, path, :],
                     func=FUNC.Identity,
                     scale=1.0 / ROW,
-                    bias=bias_share[:, path : path + 1],
                     accum_out=mean[:, path : path + 1],
-                )
-
-        def hidden_bias_share(gate):
-            unread = unread_pool.tile([P, WIDTH], BF16, name="unread")
-            nc.scalar.activation(
-                out=unread[:],
-                in_=hidden_bias_rep[:, gate * WIDTH : (gate + 1) * WIDTH],
-                func=FUNC.Identity,
-                scale=1.0 / (ROW * GATES * HALVES),
-                accum_out=bias_share_parts[:, gate : gate + 1],
-            )
-            if gate == GATES - 1:
-                nc.scalar.activation(
-                    out=bias_share_unread[:], in_=bias_share_parts[:], func=FUNC.Identity, accum_out=bias_share[:, 0:1]
                 )
 
         def row_inverse_deviations(bt):
@@ -586,10 +572,14 @@ def tile_adaptivelstmcell_pb_kernel(
                 nc.vector.tensor_tensor(out=gate_o[:, cols], in0=gate_o[:, cols], in1=slabs[(bt, GATES + 2)][:, cols], op=ALU.mult)
                 nc.sync.dma_start(out=out_0[rows, cols], in_=gate_o[:, cols])
 
+        nc.sync.dma_start(out=hidden_bias_rows[0 : ROW // P, :], in_=b_hh.rearrange("(c p) -> c p", p=P))
         load_batch_tile(0)
         load_slab_weights(0)
         load_scale_planes(0)
         nc.sync.dma_start(out=input_bias_rows[0:GATES, :], in_=b_ih.rearrange("(g n) -> g n", g=GATES))
+        turned_bias = psum.tile([P, P], BF16, name="turned_bias", tag="beta")
+        nc.tensor.transpose(out=turned_bias[:], in_=hidden_bias_rows[:], identity=ident_bf16[:])
+        nc.vector.tensor_copy(out=hidden_bias_cols[:], in_=turned_bias[:])
         turn_activations(0)
         copy_activations(0)
         turn_embeddings(0)
@@ -692,12 +682,9 @@ def tile_adaptivelstmcell_pb_kernel(
             if n + 1 < ALL_SLABS:
                 slab_matmuls(n + 1)
 
-            if 1 <= k <= GATES:
-                slab_squares(n - 1)
             if k == SLABS - 1:
                 row_means(bt)
-            if k >= GATES:
-                slab_squares(n)
+            slab_squares(n)
             if k == SLABS - 1:
                 row_inverse_deviations(bt)
 
@@ -707,8 +694,6 @@ def tile_adaptivelstmcell_pb_kernel(
                 load_slab_weights(n + LOAD_AHEAD)
             if n + TURN_AHEAD < SLABS:
                 turn_hyper_weights(n + TURN_AHEAD)
-            if n < GATES:
-                hidden_bias_share(n)
             if n == SLABS - 4:
                 load_vector_rows()
                 for gate in ROW_GATES:

@@ -315,17 +315,6 @@ def tile_adaptivelstmcell_pb_kernel(
                     start=True,
                     stop=False,
                 )
-                if path == 0:
-                    for q in range(QUARTERS):
-                        col = gate * BLOCKS + half * QUARTERS + q
-                        nc.tensor.matmul(
-                            bank[:, q * P : (q + 1) * P],
-                            lhsT=hidden_bias_cols[:, col : col + 1].to_broadcast([P, P]),
-                            rhs=ident_f32[:],
-                            is_transpose=True,
-                            start=False,
-                            stop=(q == QUARTERS - 1),
-                        )
                 if path == 1:
                     nc.tensor.matmul(
                         bank[:],
@@ -335,6 +324,18 @@ def tile_adaptivelstmcell_pb_kernel(
                         stop=True,
                     )
                 beta_banks.append(bank)
+            if path == 0:
+                for half in range(HALVES):
+                    for q in range(QUARTERS):
+                        col = gate * BLOCKS + half * QUARTERS + q
+                        nc.tensor.matmul(
+                            beta_banks[half][:, q * P : (q + 1) * P],
+                            lhsT=hidden_bias_cols[:, col : col + 1].to_broadcast([P, P]),
+                            rhs=ident_f32[:],
+                            is_transpose=True,
+                            start=False,
+                            stop=(q == QUARTERS - 1),
+                        )
             alpha_sb = alpha_pool.tile([P, HALVES, BANK], F32, name="alpha_sb")
             for half in range(HALVES):
                 nc.scalar.copy(out=alpha_sb[:, half, :], in_=alpha_banks[half][:])

@@ -81,7 +81,7 @@ def tile_adaptivelstmcell_pb_kernel(
 
     with ExitStack() as ctx:
         const = ctx.enter_context(tc.tile_pool(name="const", bufs=1))
-        raw_pool = ctx.enter_context(tc.tile_pool(name="raw", bufs=11))
+        raw_pool = ctx.enter_context(tc.tile_pool(name="raw", bufs=13))
         operand_pool = ctx.enter_context(tc.tile_pool(name="operand", bufs=2))
         slab_pool = ctx.enter_context(tc.tile_pool(name="slab", bufs=14))
         alpha_pool = ctx.enter_context(tc.tile_pool(name="alpha", bufs=2))
@@ -112,7 +112,7 @@ def tile_adaptivelstmcell_pb_kernel(
         alpha_wT = const.tile([P, SLABS, WIDTH], BF16, name="alpha_wT")
         beta_wT = const.tile([P, SLABS, WIDTH], BF16, name="beta_wT")
         hidden_bias_rows = const.tile([P, P], BF16, name="hidden_bias_rows")
-        nc.gpsimd.memset(hidden_bias_rows[:], 0.0)
+        nc.vector.memset(hidden_bias_rows[:], 0.0)
         hidden_bias_cols = const.tile([P, P], F32, name="hidden_bias_cols")
         gain_rep = const.tile([P, PATHS, len(ROW_GATES) * WIDTH], BF16, name="gain_rep")
         shift_rep = const.tile([P, len(ROW_GATES) * WIDTH], F32, name="shift_rep")
@@ -133,7 +133,7 @@ def tile_adaptivelstmcell_pb_kernel(
         scaled_slabs = {}
         summed_slabs = {}
 
-        def load_batch_tile(bt):
+        def load_batch_tile(bt, keys=("hx", "zw", "zb", "x")):
             rows = slice(bt * P, (bt + 1) * P)
             sources = {
                 "x": x[rows, :],
@@ -141,7 +141,7 @@ def tile_adaptivelstmcell_pb_kernel(
                 "zw": zw[rows, :, :].rearrange("b s a -> b (s a)"),
                 "zb": zb[rows, :, :].rearrange("b s a -> b (s a)"),
             }
-            for key in ("hx", "zw", "zb", "x"):
+            for key in keys:
                 loaded = raw_pool.tile([P, WIDTH], BF16, name="raw_" + key, tag="raw")
                 nc.sync.dma_start(out=loaded[:], in_=sources[key])
                 raw[(bt, key)] = loaded
@@ -159,15 +159,17 @@ def tile_adaptivelstmcell_pb_kernel(
                         in_=path_scales[path][g, r:16:4, :].bitcast(I32),
                     )
 
-        def load_slab_weights(slot):
-            path, gate = divmod(slot, GATES)
-            byte_cols = slice(2 * gate * WIDTH, 2 * (gate + 1) * WIDTH)
+        def load_hyper_weights(slot):
             for key, source in (("alpha_w", norm_alpha_w), ("beta_w", bias_beta_w)):
                 loaded = raw_pool.tile([P, BLOCKS, EMB], BF16, name="raw_" + key, tag="raw")
                 nc.sync.dma_start(
                     out=loaded[:], in_=source[(slot + GATES) % SLABS].rearrange("(blk p) a -> p blk a", p=P)
                 )
                 raw[(slot, key)] = loaded
+
+        def load_words(slot):
+            path, gate = divmod(slot, GATES)
+            byte_cols = slice(2 * gate * WIDTH, 2 * (gate + 1) * WIDTH)
             for g in range(PASSES):
                 nc.sync.dma_start(
                     out=words[path][:, g, byte_cols].bitcast(I32),
@@ -200,8 +202,8 @@ def tile_adaptivelstmcell_pb_kernel(
                 out=shift_rep[:, row_cols(gate)], in0=raw[(gate, "shift0")][:], in1=raw[(gate, "shift1")][:], op=ALU.add
             )
 
-        def turn_activations(bt):
-            for key in ("hx", "x"):
+        def turn_activations(bt, keys=("hx", "x")):
+            for key in keys:
                 pairs = raw[(bt, key)][:].bitcast(F32)
                 turned = psum.tile([P, PASSES, 2, P], F32, name="turned_" + key, tag="turn")
                 for g in range(PASSES):
@@ -213,8 +215,8 @@ def tile_adaptivelstmcell_pb_kernel(
                         )
                 operands[(bt, "turned_" + key)] = turned
 
-        def copy_activations(bt):
-            for key in ("hx", "x"):
+        def copy_activations(bt, keys=("hx", "x")):
+            for key in keys:
                 side_by_side = operand_pool.tile(
                     [P, PASSES * P * 4], BF16, name="side_by_side_" + key, tag="side_by_side", align_bytes=64
                 )
@@ -224,8 +226,9 @@ def tile_adaptivelstmcell_pb_kernel(
                 )
                 operands[(bt, "side_by_side_" + key)] = side_by_side
 
-        def quantise_activations(bt):
-            for path, key in enumerate(("hx", "x")):
+        def quantise_activations(bt, paths=(0, 1)):
+            for path in paths:
+                key = ("hx", "x")[path]
                 codes = operand_pool.tile([P, PASSES * P], U32, name="codes%d" % path, align_bytes=64)
                 code_scales = operand_pool.tile([P, PASSES * P], U8, name="code_scales%d" % path, align_bytes=64)
                 nc.vector.quantize_mx(out=codes[:].bitcast(FP8X4), scales=code_scales[:], in_=operands[(bt, "side_by_side_" + key)][:])
@@ -573,27 +576,30 @@ def tile_adaptivelstmcell_pb_kernel(
                 nc.vector.tensor_tensor(out=gate_o[:, cols], in0=gate_o[:, cols], in1=slabs[(bt, GATES + 2)][:, cols], op=ALU.mult)
                 nc.sync.dma_start(out=out_0[rows, cols], in_=gate_o[:, cols])
 
+        load_batch_tile(0, ("hx", "zw", "zb"))
         nc.sync.dma_start(out=hidden_bias_rows[0 : ROW // P, :], in_=b_hh.rearrange("(c p) -> c p", p=P))
-        load_batch_tile(0)
-        load_slab_weights(0)
+        load_hyper_weights(0)
+        load_words(0)
         load_scale_planes(0)
+        load_hyper_weights(1)
+        load_hyper_weights(2)
+        load_words(1)
+        load_batch_tile(0, ("x",))
         nc.sync.dma_start(out=input_bias_rows[0:GATES, :], in_=b_ih.rearrange("(g n) -> g n", g=GATES))
+        load_hyper_weights(3)
+        load_words(2)
+        turn_activations(0, ("hx",))
+        copy_activations(0, ("hx",))
         turned_bias = psum.tile([P, P], BF16, name="turned_bias", tag="beta")
         nc.tensor.transpose(out=turned_bias[:], in_=hidden_bias_rows[:], identity=ident_bf16[:])
         nc.vector.tensor_copy(out=hidden_bias_cols[:], in_=turned_bias[:])
-        turn_activations(0)
-        copy_activations(0)
+        quantise_activations(0, (0,))
         turn_embeddings(0)
         copy_embeddings(0)
-        quantise_activations(0)
-        load_slab_weights(1)
         turn_hyper_weights(0)
         copy_hyper_weights(0)
-        load_slab_weights(2)
         turn_hyper_weights(1)
         copy_hyper_weights(1)
-        for slot in range(3, LOAD_AHEAD):
-            load_slab_weights(slot)
         slab_matmuls(0)
         turn_hyper_weights(2)
 
@@ -689,10 +695,19 @@ def tile_adaptivelstmcell_pb_kernel(
             if k == SLABS - 1:
                 row_inverse_deviations(bt)
 
-            if n == 0:
+            if n + 4 < SLABS:
+                load_hyper_weights(n + 4)
+            if n == 1:
                 load_scale_planes(1)
-            if n + LOAD_AHEAD < SLABS:
-                load_slab_weights(n + LOAD_AHEAD)
+            if n + 3 < SLABS:
+                load_words(n + 3)
+            if n == 3:
+                load_batch_tile(1, ("hx", "x"))
+            if n == 4:
+                load_batch_tile(1, ("zw", "zb"))
+            if n == 1:
+                turn_activations(0, ("x",))
+                copy_activations(0, ("x",))
             if n + TURN_AHEAD < SLABS:
                 turn_hyper_weights(n + TURN_AHEAD)
             if n == SLABS - 4:
@@ -706,7 +721,7 @@ def tile_adaptivelstmcell_pb_kernel(
             if n == SLABS - 1:
                 turn_vectors()
 
-            if k == 0 and has_next:
+            if k == 0 and has_next and bt >= 1:
                 load_batch_tile(bt + 1)
             if k == 0 and bt >= 1:
                 load_cell_state(bt - 1)
@@ -724,6 +739,8 @@ def tile_adaptivelstmcell_pb_kernel(
                     turn_embeddings(bt + 1)
             for t, r in tails:
                 vector_after(t, r)
+            if n == 2:
+                quantise_activations(0, (1,))
             if k == first_turn + 1 and has_next:
                 quantise_activations(bt + 1)
 

@@ -163,7 +163,7 @@ def tile_adaptivelstmcell_pb_kernel(
             for key, source in (("alpha_w", norm_alpha_w), ("beta_w", bias_beta_w)):
                 loaded = raw_pool.tile([P, BLOCKS, EMB], BF16, name="raw_" + key, tag="raw")
                 nc.sync.dma_start(
-                    out=loaded[:], in_=source[(slot + GATES) % SLABS].rearrange("(blk p) a -> p blk a", p=P)
+                    out=loaded[:], in_=source[(slot + GATES) % SLABS].rearrange("(p blk) a -> p blk a", p=P)
                 )
                 raw[(slot, key)] = loaded
 
@@ -275,10 +275,12 @@ def tile_adaptivelstmcell_pb_kernel(
 
         def copy_hyper_weights(slot):
             nc.vector.tensor_copy(
-                out=alpha_wT[:, slot, :], in_=operands[(slot, "turned_alpha_w")][:].rearrange("a blk p -> a (blk p)")
+                out=alpha_wT[:, slot, :].rearrange("a (p blk) -> a p blk", blk=BLOCKS),
+                in_=operands[(slot, "turned_alpha_w")][:].rearrange("a blk p -> a p blk"),
             )
             nc.scalar.copy(
-                out=beta_wT[:, slot, :], in_=operands[(slot, "turned_beta_w")][:].rearrange("a blk p -> a (blk p)")
+                out=beta_wT[:, slot, :].rearrange("a (p blk) -> a p blk", blk=BLOCKS),
+                in_=operands[(slot, "turned_beta_w")][:].rearrange("a blk p -> a p blk"),
             )
 
         def slab_matmuls(n):

@@ -35,13 +35,7 @@ GATE_I = 0
 GATE_J = 1
 GATE_F = 2
 GATE_O = 3
-INPUT_GAIN_ON_VECTOR = False
-LOAD_AHEAD = 4
 TURN_AHEAD = 3
-
-
-def PRODUCT_ENGINE(nc):
-    return nc.gpsimd
 
 
 ROW_GATES = (GATE_J, GATE_F)
@@ -87,7 +81,7 @@ def tile_adaptivelstmcell_pb_kernel(
         alpha_pool = ctx.enter_context(tc.tile_pool(name="alpha", bufs=2))
         unread_pool = ctx.enter_context(tc.tile_pool(name="unread", bufs=2))
         stat_pool = ctx.enter_context(tc.tile_pool(name="stat", bufs=2))
-        scaled_pool = ctx.enter_context(tc.tile_pool(name="scaled", bufs=6))
+        scaled_pool = ctx.enter_context(tc.tile_pool(name="scaled", bufs=8))
         psum = ctx.enter_context(tc.psum_pool(name="psum", bufs=2))
         ctx.enter_context(tc.manual_schedule())
 
@@ -99,7 +93,7 @@ def tile_adaptivelstmcell_pb_kernel(
         nc.vector.memset(eps[:], EPS)
         quarter_eps = const.tile([P, 1], F32, name="quarter_eps")
         nc.vector.memset(quarter_eps[:], EPS / GATES)
-        minus_half = const.tile([P, PATHS], F32, name="minus_half")
+        minus_half = const.tile([P, 1], F32, name="minus_half")
         nc.vector.memset(minus_half[:], -0.5)
 
         words = []
@@ -151,12 +145,13 @@ def tile_adaptivelstmcell_pb_kernel(
             nc.sync.dma_start(out=loaded[:], in_=cx[bt * P : (bt + 1) * P, :])
             raw[(bt, "cx")] = loaded
 
-        def load_scale_planes(path):
+        def load_scale_planes(path, gates=(0, GATES)):
+            cols = slice(gates[0] * WIDTH, gates[1] * WIDTH)
             for g in range(PASSES):
                 for r in range(4):
                     nc.sync.dma_start(
-                        out=planes[path][r:P:32, g, :].bitcast(I32),
-                        in_=path_scales[path][g, r:16:4, :].bitcast(I32),
+                        out=planes[path][r:P:32, g, cols].bitcast(I32),
+                        in_=path_scales[path][g, r:16:4, cols].bitcast(I32),
                     )
 
         def load_hyper_weights(slot):
@@ -180,13 +175,11 @@ def tile_adaptivelstmcell_pb_kernel(
             place = ROW_GATES.index(gate)
             return slice(place * WIDTH, (place + 1) * WIDTH)
 
-        def load_gains():
-            for gate in ROW_GATES:
-                cols = slice(gate * WIDTH, (gate + 1) * WIDTH)
-                for path in range(PATHS):
-                    nc.sync.dma_start(
-                        out=gain_rep[:, path, row_cols(gate)], in_=path_gain[path][cols].partition_broadcast(P)
-                    )
+        def load_gains(path):
+            cols = slice(ROW_GATES[0] * WIDTH, (ROW_GATES[-1] + 1) * WIDTH)
+            nc.sync.dma_start(out=gain_rep[:, path, :], in_=path_gain[path][cols].partition_broadcast(P))
+
+        def load_cell_vectors():
             nc.sync.dma_start(out=cell_gain_rep[:], in_=ln_c_w.partition_broadcast(P))
             nc.sync.dma_start(out=cell_shift_rep[:], in_=ln_c_b.partition_broadcast(P))
 
@@ -387,93 +380,87 @@ def tile_adaptivelstmcell_pb_kernel(
             stats[(bt, name)] = stat_pool.tile([P, width], F32, name=name)
             return stats[(bt, name)]
 
-        def row_means(bt):
-            mean = small(bt, "mean", PATHS)
-            for path in range(PATHS):
-                nc.scalar.activation(
-                    out=small(bt, "scaled_sums%d" % path, GATES * HALVES)[:],
-                    in_=stats[(bt, "sum_parts")][:, path, :],
-                    func=FUNC.Identity,
-                    scale=1.0 / ROW,
-                    accum_out=mean[:, path : path + 1],
-                )
+        def row_mean(bt, path):
+            nc.scalar.activation(
+                out=small(bt, "scaled_sums%d" % path, GATES * HALVES)[:],
+                in_=stats[(bt, "sum_parts")][:, path, :],
+                func=FUNC.Identity,
+                scale=1.0 / ROW,
+                accum_out=small(bt, "mean%d" % path, 1)[:],
+            )
 
-        def row_inverse_deviations(bt):
-            mean_squared = small(bt, "mean_squared", PATHS)
-            nc.scalar.activation(out=mean_squared[:], in_=stats[(bt, "mean")][:], func=FUNC.Square)
-            quarter_rest = small(bt, "quarter_rest", PATHS)
+        def row_inverse_deviation(bt, path):
+            mean_squared = small(bt, "mean_squared%d" % path, 1)
+            nc.scalar.activation(out=mean_squared[:], in_=stats[(bt, "mean%d" % path)][:], func=FUNC.Square)
+            quarter_rest = small(bt, "quarter_rest%d" % path, 1)
             nc.scalar.activation(
                 out=quarter_rest[:], in_=mean_squared[:], func=FUNC.Identity, scale=-1.0 / GATES, bias=quarter_eps[:]
             )
-            variance = small(bt, "variance", PATHS)
-            for path in range(PATHS):
-                nc.scalar.activation(
-                    out=small(bt, "scaled_squares%d" % path, GATES)[:],
-                    in_=stats[(bt, "square_parts")][:, path, :],
-                    func=FUNC.Identity,
-                    scale=1.0 / ROW,
-                    bias=quarter_rest[:, path : path + 1],
-                    accum_out=variance[:, path : path + 1],
-                )
-            nc.gpsimd.tensor_tensor(out=small(bt, "inverse", PATHS)[:], in0=variance[:], in1=minus_half[:], op=ALU.pow)
+            variance = small(bt, "variance%d" % path, 1)
+            nc.scalar.activation(
+                out=small(bt, "scaled_squares%d" % path, GATES)[:],
+                in_=stats[(bt, "square_parts")][:, path, :],
+                func=FUNC.Identity,
+                scale=1.0 / ROW,
+                bias=quarter_rest[:],
+                accum_out=variance[:],
+            )
+            nc.gpsimd.tensor_tensor(
+                out=small(bt, "inverse%d" % path, 1)[:], in0=variance[:], in1=minus_half[:], op=ALU.pow
+            )
 
         def center_and_gain(bt, gate, path):
             pre = slabs[(bt, path * GATES + gate)]
             nc.vector.scalar_tensor_tensor(
                 out=pre[:],
                 in0=pre[:],
-                scalar=stats[(bt, "mean")][:, path : path + 1],
+                scalar=stats[(bt, "mean%d" % path)][:],
                 in1=gain_rep[:, path, row_cols(gate)],
                 op0=ALU.subtract,
                 op1=ALU.mult,
             )
 
-        def scale_and_add(bt, gate, path, then_activate=True):
-            inverse = stats[(bt, "inverse")]
+        def scale_and_add(bt, gate, path):
             pre = slabs[(bt, path * GATES + gate)]
             nc.vector.scalar_tensor_tensor(
                 out=pre[:],
                 in0=pre[:],
-                scalar=inverse[:, path : path + 1],
+                scalar=stats[(bt, "inverse%d" % path)][:],
                 in1=(shift_rep[:, row_cols(gate)] if path == 0 else slabs[(bt, gate)][:]),
                 op0=ALU.mult,
                 op1=ALU.add,
             )
-            if path == 1 and then_activate:
-                row_activate(bt, gate)
-
         def row_activate(bt, gate):
             pre = slabs[(bt, GATES + gate)]
             nc.scalar.activation(out=pre[:], in_=pre[:], func=(FUNC.Tanh if gate == GATE_J else FUNC.Sigmoid))
 
-        def normalise(bt, gate):
-            for path in range(PATHS):
-                pre = slabs[(bt, path * GATES + gate)]
-                nc.vector.tensor_scalar(
-                    out=pre[:],
-                    in0=pre[:],
-                    scalar1=stats[(bt, "mean")][:, path : path + 1],
-                    scalar2=stats[(bt, "inverse")][:, path : path + 1],
-                    op0=ALU.subtract,
-                    op1=ALU.mult,
-                )
+        def normalise(bt, gate, path):
+            pre = slabs[(bt, path * GATES + gate)]
+            nc.vector.tensor_scalar(
+                out=pre[:],
+                in0=pre[:],
+                scalar1=stats[(bt, "mean%d" % path)][:],
+                scalar2=stats[(bt, "inverse%d" % path)][:],
+                op0=ALU.subtract,
+                op1=ALU.mult,
+            )
 
-        def turn_forward(bt, gate, half, tags=("turn", "turn")):
-            for path in range(PATHS):
-                pre = slabs[(bt, path * GATES + gate)]
-                turned = psum.tile([P, QUARTERS, P], F32, name="turned_slab", tag=tags[path])
+        def turn_forward(bt, gate, path, tags=("turn", "turn")):
+            pre = slabs[(bt, path * GATES + gate)]
+            for half in range(HALVES):
+                turned = psum.tile([P, QUARTERS, P], F32, name="turned_slab", tag=tags[half])
                 for q in range(QUARTERS):
                     first = half * BANK + q * P
                     nc.tensor.transpose(out=turned[:, q, :], in_=pre[:, first : first + P], identity=ident_f32[:])
                 turned_slabs[(bt, gate, half, path)] = turned
 
-        def gain_and_shift(bt, gate, half, paths=(0, 1), on_vector=INPUT_GAIN_ON_VECTOR):
+        def gain_and_shift(bt, gate, path, on_vector=False):
             blocks = ROW // P
-            first = gate * BLOCKS + half * QUARTERS
-            for path in paths:
+            for half in range(HALVES):
+                first = gate * BLOCKS + half * QUARTERS
                 turned = turned_slabs[(bt, gate, half, path)]
                 scaled = scaled_pool.tile([P, QUARTERS, P], F32, name="scaled")
-                if path == 1 and on_vector:
+                if on_vector:
                     nc.vector.tensor_tensor(
                         out=scaled[:],
                         in0=turned[:],
@@ -497,26 +484,28 @@ def tile_adaptivelstmcell_pb_kernel(
                             )
                 scaled_slabs[(bt, gate, half, path)] = scaled
 
-        def turn_back(bt, gate, half, tag="turn"):
-            summed = psum.tile([P, BANK], F32, name="summed", tag=tag)
-            for q in range(QUARTERS):
-                for path in range(PATHS):
-                    nc.tensor.matmul(
-                        summed[:, q * P : (q + 1) * P],
-                        lhsT=scaled_slabs[(bt, gate, half, path)][:, q, :],
-                        rhs=ident_f32[:],
-                        is_transpose=True,
-                        start=(path == 0),
-                        stop=(path == PATHS - 1),
-                    )
-            summed_slabs[(bt, gate, half)] = summed
+        def turn_back(bt, gate, tags=("turn", "turn")):
+            for half in range(HALVES):
+                summed = psum.tile([P, BANK], F32, name="summed", tag=tags[half])
+                for q in range(QUARTERS):
+                    for path in range(PATHS):
+                        nc.tensor.matmul(
+                            summed[:, q * P : (q + 1) * P],
+                            lhsT=scaled_slabs[(bt, gate, half, path)][:, q, :],
+                            rhs=ident_f32[:],
+                            is_transpose=True,
+                            start=(path == 0),
+                            stop=(path == PATHS - 1),
+                        )
+                summed_slabs[(bt, gate, half)] = summed
 
-        def activate(bt, gate, half):
-            nc.scalar.activation(
-                out=slabs[(bt, GATES + gate)][:, half * BANK : (half + 1) * BANK],
-                in_=summed_slabs[(bt, gate, half)][:],
-                func=(FUNC.Tanh if gate == GATE_J else FUNC.Sigmoid),
-            )
+        def activate(bt, gate):
+            for half in range(HALVES):
+                nc.scalar.activation(
+                    out=slabs[(bt, GATES + gate)][:, half * BANK : (half + 1) * BANK],
+                    in_=summed_slabs[(bt, gate, half)][:],
+                    func=(FUNC.Tanh if gate == GATE_J else FUNC.Sigmoid),
+                )
 
         def cell_products(bt, first, engine):
             if first:
@@ -550,7 +539,7 @@ def tile_adaptivelstmcell_pb_kernel(
             variance = small(bt, "cell_variance", 1)
             nc.scalar.activation(out=variance[:], in_=squares[:], func=FUNC.Identity, scale=1.0 / WIDTH, bias=rest[:])
             nc.gpsimd.tensor_tensor(
-                out=small(bt, "cell_inverse", 1)[:], in0=variance[:], in1=minus_half[:, 0:1], op=ALU.pow
+                out=small(bt, "cell_inverse", 1)[:], in0=variance[:], in1=minus_half[:], op=ALU.pow
             )
 
         def cell_norm(bt):
@@ -581,10 +570,11 @@ def tile_adaptivelstmcell_pb_kernel(
         load_batch_tile(0, ("hx", "zw", "zb"))
         nc.sync.dma_start(out=hidden_bias_rows[0 : ROW // P, :], in_=b_hh.rearrange("(c p) -> c p", p=P))
         load_hyper_weights(0)
-        load_words(0)
-        load_scale_planes(0)
         load_hyper_weights(1)
+        load_words(0)
+        load_scale_planes(0, (0, 1))
         load_hyper_weights(2)
+        load_scale_planes(0, (1, GATES))
         load_words(1)
         load_batch_tile(0, ("x",))
         nc.sync.dma_start(out=input_bias_rows[0:GATES, :], in_=b_ih.rearrange("(g n) -> g n", g=GATES))
@@ -606,96 +596,50 @@ def tile_adaptivelstmcell_pb_kernel(
         turn_hyper_weights(2)
 
         last = BATCH_TILES - 1
-        product_engine = PRODUCT_ENGINE(nc)
-
-        def o_round(t):
-            return 4 if t == last - 1 else 6
-
-        def scalar_empties(t, r):
-            if r == 2:
-                gain_and_shift(t, GATE_I, 0)
-            if r == 3:
-                gain_and_shift(t, GATE_I, 1)
-            if r == 4:
-                activate(t, GATE_I, 0)
-                activate(t, GATE_I, 1)
-            if r == o_round(t) + 1:
-                gain_and_shift(t, GATE_O, 0)
-            if r == o_round(t) + 2:
-                gain_and_shift(t, GATE_O, 1)
-            if r == o_round(t) + 3:
-                activate(t, GATE_O, 0)
-                activate(t, GATE_O, 1)
-
-        def vector_before(t, r):
-            if r == 1:
-                normalise(t, GATE_I)
-            if r == 6:
-                scale_and_add(t, GATE_J, 1)
-                cell_products(t, True, product_engine)
-            if r == o_round(t):
-                normalise(t, GATE_O)
-
-        def tensor_turns(t, r):
-            if r == 1:
-                turn_forward(t, GATE_I, 0)
-            if r == 2:
-                turn_forward(t, GATE_I, 1)
-            if r == 3:
-                turn_back(t, GATE_I, 0)
-                turn_back(t, GATE_I, 1)
-            if r == o_round(t):
-                turn_forward(t, GATE_O, 0)
-            if r == o_round(t) + 1:
-                turn_forward(t, GATE_O, 1)
-            if r == o_round(t) + 2:
-                turn_back(t, GATE_O, 0)
-                turn_back(t, GATE_O, 1)
-
-        def vector_after(t, r):
-            if r == 2:
-                center_and_gain(t, GATE_F, 0)
-                center_and_gain(t, GATE_F, 1)
-            if r == 3:
-                center_and_gain(t, GATE_J, 0)
-                center_and_gain(t, GATE_J, 1)
-            if r == 4:
-                scale_and_add(t, GATE_F, 0)
-                scale_and_add(t, GATE_J, 0)
-            if r == 5:
-                scale_and_add(t, GATE_F, 1)
-                cell_products(t, False, product_engine)
-            if r == 7 and t < last - 1:
-                cell_sum(t)
-            if r == 8:
-                cell_norm(t)
-            if r == 9:
-                hidden_state(t)
 
         for n in range(ALL_SLABS):
             bt, k = divmod(n, SLABS)
             has_next = bt < last
             tails = [(t, n - SLABS * (t + 1)) for t in (bt - 2, bt - 1) if t >= 0]
-            first_turn = 5 if bt == 0 else 4
+            acts_round = 5
             slab_combine(n)
 
             for t, r in tails:
-                scalar_empties(t, r)
+                if r == 0:
+                    gain_and_shift(t, GATE_I, 0)
+                if r == 1:
+                    gain_and_shift(t, GATE_O, 0)
+                if r == 2:
+                    gain_and_shift(t, GATE_I, 1)
+                if r == 3:
+                    activate(t, GATE_I)
+                if r == 4:
+                    gain_and_shift(t, GATE_O, 1)
+                    row_activate(t, GATE_F)
+                if r == 5:
+                    activate(t, GATE_O)
+                    row_activate(t, GATE_J)
+            if bt == last and k == 6:
+                gain_and_shift(bt, GATE_I, 0)
+            if bt == last and k == 7:
+                gain_and_shift(bt, GATE_J, 0)
             if n + 2 < SLABS:
                 copy_hyper_weights(n + 2)
             if has_next:
-                if k == first_turn + 1:
+                if k == acts_round + 1:
                     copy_activations(bt + 1)
-                if k == first_turn + 2:
+                if k == acts_round + 2:
                     copy_embeddings(bt + 1)
             if n + 1 < ALL_SLABS:
                 slab_matmuls(n + 1)
 
-            if k == SLABS - 1:
-                row_means(bt)
+            for path in range(PATHS):
+                if k == (path + 1) * GATES - 1:
+                    row_mean(bt, path)
             slab_squares(n)
-            if k == SLABS - 1:
-                row_inverse_deviations(bt)
+            for path in range(PATHS):
+                if k == (path + 1) * GATES - 1:
+                    row_inverse_deviation(bt, path)
 
             if n + 4 < SLABS:
                 load_hyper_weights(n + 4)
@@ -703,24 +647,22 @@ def tile_adaptivelstmcell_pb_kernel(
                 load_scale_planes(1)
             if n + 3 < SLABS:
                 load_words(n + 3)
-            if n == 3:
-                load_batch_tile(1, ("hx", "x"))
+            if n == 1:
+                load_vector_rows()
             if n == 4:
+                for gate in ROW_GATES:
+                    load_shifts(gate)
+                load_batch_tile(1, ("hx", "x"))
                 load_batch_tile(1, ("zw", "zb"))
+                load_gains(0)
+                load_gains(1)
+                load_cell_vectors()
             if n == 1:
                 turn_activations(0, ("x",))
                 copy_activations(0, ("x",))
             if n + TURN_AHEAD < SLABS:
                 turn_hyper_weights(n + TURN_AHEAD)
-            if n == SLABS - 4:
-                load_vector_rows()
-                for gate in ROW_GATES:
-                    load_shifts(gate)
-            if n == SLABS - 3:
-                load_gains()
-                for gate in ROW_GATES:
-                    add_shifts(gate)
-            if n == SLABS - 1:
+            if n == 3:
                 turn_vectors()
 
             if k == 0 and has_next and bt >= 1:
@@ -731,67 +673,104 @@ def tile_adaptivelstmcell_pb_kernel(
                 load_cell_state(last)
 
             for t, r in tails:
-                vector_before(t, r)
+                if r == 0:
+                    normalise(t, GATE_O, 0)
+                if r == 1:
+                    normalise(t, GATE_I, 1)
+                if r == 3:
+                    normalise(t, GATE_O, 1)
+                if r == 5:
+                    cell_products(t, False, nc.gpsimd)
+                    cell_products(t, True, nc.gpsimd)
+            if k == 7 and has_next:
+                normalise(bt, GATE_I, 0)
+            if k == 5 and not has_next:
+                normalise(bt, GATE_I, 0)
+            if k == 6 and not has_next:
+                normalise(bt, GATE_J, 0)
+            if k == 7 and not has_next:
+                normalise(bt, GATE_O, 0)
+
             for t, r in tails:
-                tensor_turns(t, r)
+                if r == 0:
+                    turn_forward(t, GATE_O, 0)
+                if r == 1:
+                    turn_forward(t, GATE_I, 1)
+                if r == 2:
+                    turn_back(t, GATE_I)
+                if r == 3:
+                    turn_forward(t, GATE_O, 1)
+                if r == 4:
+                    turn_back(t, GATE_O)
             if has_next:
-                if k == first_turn:
+                if k == acts_round:
                     turn_activations(bt + 1)
-                if k == first_turn + 1:
+                if k == acts_round + 1:
                     turn_embeddings(bt + 1)
+                if k == acts_round + 2:
+                    turn_forward(bt, GATE_I, 0)
+            else:
+                if k == 5:
+                    turn_forward(bt, GATE_I, 0)
+                if k == 6:
+                    turn_forward(bt, GATE_J, 0)
+                if k == 7:
+                    turn_forward(bt, GATE_O, 0)
+
             for t, r in tails:
-                vector_after(t, r)
+                if r == 0:
+                    center_and_gain(t, GATE_J, 0)
+                if r == 1:
+                    scale_and_add(t, GATE_J, 0)
+                if r == 2:
+                    center_and_gain(t, GATE_F, 1)
+                    center_and_gain(t, GATE_J, 1)
+                if r == 3:
+                    scale_and_add(t, GATE_F, 1)
+                if r == 4:
+                    scale_and_add(t, GATE_J, 1)
+                if r == 6:
+                    cell_sum(t)
+                if r == 7:
+                    cell_norm(t)
+                if r == 8:
+                    hidden_state(t)
+            if k == (7 if bt == 0 else 5):
+                center_and_gain(bt, GATE_F, 0)
+            if k == 6 and bt > 0:
+                scale_and_add(bt, GATE_F, 0)
+            if n == SLABS + 1:
+                scale_and_add(0, GATE_F, 0)
+            if n == 5:
+                add_shifts(GATE_F)
+                add_shifts(GATE_J)
             if n == 2:
                 quantise_activations(0, (1,))
-            if k == first_turn + 1 and has_next:
+            if k == acts_round + 1 and has_next:
                 quantise_activations(bt + 1)
 
-        before = last - 1
-        free_tags = ["alpha", "alpha", "xh", "xh", "beta", "beta", "turn", "turn"]
-
-        def next_tags(count):
-            taken = free_tags[:count]
-            free_tags.extend(taken)
-            for tag in taken:
-                free_tags.remove(tag)
-            return taken
-
-        center_and_gain(last, GATE_F, 0)
+        gain_and_shift(last, GATE_O, 0)
         center_and_gain(last, GATE_F, 1)
-        cell_sum(before)
-        normalise(last, GATE_I)
-        normalise(last, GATE_J)
-        for gate in (GATE_I, GATE_J):
-            for half in range(HALVES):
-                turn_forward(last, gate, half, next_tags(2))
-        scale_and_add(last, GATE_F, 0)
-        gain_and_shift(last, GATE_I, 0, on_vector=True)
-        gain_and_shift(last, GATE_I, 1, on_vector=True)
-        turn_back(last, GATE_I, 0, next_tags(1)[0])
-        turn_back(last, GATE_I, 1, next_tags(1)[0])
-        scale_and_add(last, GATE_F, 1, then_activate=False)
-        gain_and_shift(last, GATE_J, 0, on_vector=True)
+        normalise(last, GATE_I, 1)
+        normalise(last, GATE_J, 1)
+        turn_forward(last, GATE_I, 1, ("alpha", "alpha"))
+        turn_forward(last, GATE_J, 1, ("xh", "xh"))
+        hidden_state(last - 1)
+        scale_and_add(last, GATE_F, 1)
+        gain_and_shift(last, GATE_I, 1)
+        turn_back(last, GATE_I, ("beta", "beta"))
         gain_and_shift(last, GATE_J, 1, on_vector=True)
-        turn_back(last, GATE_J, 0, next_tags(1)[0])
-        turn_back(last, GATE_J, 1, next_tags(1)[0])
+        turn_back(last, GATE_J, ("alpha", "alpha"))
         row_activate(last, GATE_F)
-        normalise(last, GATE_O)
-        for half in range(HALVES):
-            turn_forward(last, GATE_O, half, next_tags(2))
-        activate(last, GATE_I, 0)
-        activate(last, GATE_I, 1)
-        cell_products(last, False, nc.vector)
-        activate(last, GATE_J, 0)
-        activate(last, GATE_J, 1)
+        cell_products(last, False, nc.gpsimd)
+        normalise(last, GATE_O, 1)
+        turn_forward(last, GATE_O, 1, ("xh", "xh"))
+        activate(last, GATE_I)
+        activate(last, GATE_J)
+        gain_and_shift(last, GATE_O, 1, on_vector=True)
+        turn_back(last, GATE_O, ("beta", "beta"))
         cell_products(last, True, nc.vector)
         cell_sum(last)
-        gain_and_shift(last, GATE_O, 0, on_vector=True)
-        gain_and_shift(last, GATE_O, 1, on_vector=True)
-        turn_back(last, GATE_O, 0, next_tags(1)[0])
-        turn_back(last, GATE_O, 1, next_tags(1)[0])
-        cell_norm(before)
-        activate(last, GATE_O, 0)
-        activate(last, GATE_O, 1)
-        hidden_state(before)
+        activate(last, GATE_O)
         cell_norm(last)
         hidden_state(last)

@@ -89,6 +89,8 @@ def tile_adaptivelstmcell_pb_kernel(
         make_identity(nc, ident_bf16[:])
         ident_f32 = const.tile([P, P], F32, name="ident_f32")
         make_identity(nc, ident_f32[:])
+        hidden_bias_rows = const.tile([P, P], BF16, name="hidden_bias_rows")
+        nc.vector.memset(hidden_bias_rows[:], 0.0)
         eps = const.tile([P, 1], F32, name="eps")
         nc.vector.memset(eps[:], EPS)
         quarter_eps = const.tile([P, 1], F32, name="quarter_eps")
@@ -101,12 +103,11 @@ def tile_adaptivelstmcell_pb_kernel(
         for path in range(PATHS):
             words.append(const.tile([P, PASSES, 2 * ROW], U8, name="words%d" % path, align_bytes=64))
             planes.append(const.tile([P, PASSES, ROW], U8, name="planes%d" % path, align_bytes=64))
-            nc.vector.memset(planes[path][:].bitcast(I32), 0)
+
+        nc.vector.memset(planes[0][:].bitcast(I32), 0)
 
         alpha_wT = const.tile([P, SLABS, WIDTH], BF16, name="alpha_wT")
         beta_wT = const.tile([P, SLABS, WIDTH], BF16, name="beta_wT")
-        hidden_bias_rows = const.tile([P, P], BF16, name="hidden_bias_rows")
-        nc.vector.memset(hidden_bias_rows[:], 0.0)
         hidden_bias_cols = const.tile([P, P], F32, name="hidden_bias_cols")
         gain_rep = const.tile([P, PATHS, len(ROW_GATES) * WIDTH], BF16, name="gain_rep")
         shift_rep = const.tile([P, len(ROW_GATES) * WIDTH], F32, name="shift_rep")
@@ -570,9 +571,9 @@ def tile_adaptivelstmcell_pb_kernel(
         load_batch_tile(0, ("hx", "zw", "zb"))
         nc.sync.dma_start(out=hidden_bias_rows[0 : ROW // P, :], in_=b_hh.rearrange("(c p) -> c p", p=P))
         load_hyper_weights(0)
-        load_hyper_weights(1)
         load_words(0)
         load_scale_planes(0, (0, 1))
+        load_hyper_weights(1)
         load_hyper_weights(2)
         load_scale_planes(0, (1, GATES))
         load_words(1)
@@ -586,6 +587,7 @@ def tile_adaptivelstmcell_pb_kernel(
         nc.tensor.transpose(out=turned_bias[:], in_=hidden_bias_rows[:], identity=ident_bf16[:])
         nc.vector.tensor_copy(out=hidden_bias_cols[:], in_=turned_bias[:])
         quantise_activations(0, (0,))
+        nc.vector.memset(planes[1][:].bitcast(I32), 0)
         turn_embeddings(0)
         copy_embeddings(0)
         turn_hyper_weights(0)
@@ -650,11 +652,11 @@ def tile_adaptivelstmcell_pb_kernel(
             if n == 1:
                 load_vector_rows()
             if n == 4:
-                for gate in ROW_GATES:
-                    load_shifts(gate)
                 load_batch_tile(1, ("hx", "x"))
                 load_batch_tile(1, ("zw", "zb"))
                 load_gains(0)
+                for gate in ROW_GATES:
+                    load_shifts(gate)
                 load_gains(1)
                 load_cell_vectors()
             if n == 1:

@@ -101,7 +101,7 @@ def tile_adaptivelstmcell_pb_kernel(
         words = []
         planes = []
         for path in range(PATHS):
-            words.append(const.tile([P, PASSES, 2 * ROW], U8, name="words%d" % path, align_bytes=64))
+            words.append(const.tile([P, GATES, PASSES, 2 * WIDTH], U8, name="words%d" % path, align_bytes=64))
             planes.append(const.tile([P, PASSES, ROW], U8, name="planes%d" % path, align_bytes=64))
 
         nc.vector.memset(planes[0][:].bitcast(I32), 0)
@@ -166,11 +166,10 @@ def tile_adaptivelstmcell_pb_kernel(
         def load_words(slot):
             path, gate = divmod(slot, GATES)
             byte_cols = slice(2 * gate * WIDTH, 2 * (gate + 1) * WIDTH)
-            for g in range(PASSES):
-                nc.sync.dma_start(
-                    out=words[path][:, g, byte_cols].bitcast(I32),
-                    in_=path_words[path][g, :, byte_cols].bitcast(I32),
-                )
+            nc.sync.dma_start(
+                out=words[path][:, gate, :, :].bitcast(I32),
+                in_=path_words[path][:, :, byte_cols].bitcast(I32).rearrange("g p n -> p g n"),
+            )
 
         def row_cols(gate):
             place = ROW_GATES.index(gate)
@@ -299,7 +298,7 @@ def tile_adaptivelstmcell_pb_kernel(
                         out=bank[:],
                         lhsT=operands[(bt, "codes%d" % path)][:, g * P : (g + 1) * P].bitcast(FP8X4),
                         lhsT_scale=operands[(bt, "code_scales%d" % path)][:, g * P : (g + 1) * P],
-                        rhs=words[path][:, g, 2 * first : 2 * (first + BANK)].bitcast(FP4X4),
+                        rhs=words[path][:, gate, g, 2 * half * BANK : 2 * (half + 1) * BANK].bitcast(FP4X4),
                         rhs_scale=planes[path][:, g, first : first + BANK],
                         start=(g == 0),
                         stop=(g == PASSES - 1),
@@ -572,10 +571,9 @@ def tile_adaptivelstmcell_pb_kernel(
         nc.sync.dma_start(out=hidden_bias_rows[0 : ROW // P, :], in_=b_hh.rearrange("(c p) -> c p", p=P))
         load_hyper_weights(0)
         load_words(0)
-        load_scale_planes(0, (0, 1))
+        load_scale_planes(0)
         load_hyper_weights(1)
         load_hyper_weights(2)
-        load_scale_planes(0, (1, GATES))
         load_words(1)
         load_batch_tile(0, ("x",))
         nc.sync.dma_start(out=input_bias_rows[0:GATES, :], in_=b_ih.rearrange("(g n) -> g n", g=GATES))

@@ -559,12 +559,12 @@ def tile_adaptivelstmcell_pb_kernel(
                 nc.sync.dma_start(out=out_1[rows, cols], in_=cell[:, cols])
                 nc.scalar.activation(out=tanh_cy[:, cols], in_=cell[:, cols], func=FUNC.Tanh)
 
-        def hidden_state(bt):
+        def hidden_state(bt, engine=nc.vector):
             rows = slice(bt * P, (bt + 1) * P)
             gate_o = slabs[(bt, GATES + 3)]
             for half in range(HALVES):
                 cols = slice(half * BANK, (half + 1) * BANK)
-                nc.vector.tensor_tensor(out=gate_o[:, cols], in0=gate_o[:, cols], in1=slabs[(bt, GATES + 2)][:, cols], op=ALU.mult)
+                engine.tensor_tensor(out=gate_o[:, cols], in0=gate_o[:, cols], in1=slabs[(bt, GATES + 2)][:, cols], op=ALU.mult)
                 nc.sync.dma_start(out=out_0[rows, cols], in_=gate_o[:, cols])
 
         load_batch_tile(0, ("hx", "zw", "zb"))
@@ -734,7 +734,7 @@ def tile_adaptivelstmcell_pb_kernel(
                 if r == 7:
                     cell_norm(t)
                 if r == 8:
-                    hidden_state(t)
+                    hidden_state(t, nc.gpsimd)
             if k == (7 if bt == 0 else 5):
                 center_and_gain(bt, GATE_F, 0)
             if k == 6 and bt > 0:

from contextlib import ExitStack

import concourse.mybir as mybir
from concourse.masks import make_identity

F32 = mybir.dt.float32
BF16 = mybir.dt.bfloat16
I32 = mybir.dt.int32
U32 = mybir.dt.uint32
U8 = mybir.dt.uint8
FP8X4 = mybir.dt.float8_e4m3fn_x4
FP4X4 = mybir.dt.float4_e2m1fn_x4
ALU = mybir.AluOpType
FUNC = mybir.ActivationFunctionType
AXIS = mybir.AxisListType

P = 128
BATCH = 512
WIDTH = 1024
GATES = 4
PATHS = 2
ROW = GATES * WIDTH
EMB = 128
K_PASS = 512
PASSES = WIDTH // K_PASS
BANK = 512
HALVES = WIDTH // BANK
BLOCKS = WIDTH // P
BATCH_TILES = BATCH // P
SLABS = PATHS * GATES
ALL_SLABS = BATCH_TILES * SLABS
EPS = 1e-5
QUARTERS = BANK // P
GATE_I = 0
GATE_J = 1
GATE_F = 2
GATE_O = 3
TURN_AHEAD = 3


ROW_GATES = (GATE_J, GATE_F)

FLOPS = 2 * BATCH * WIDTH * ROW * PATHS + 2 * SLABS * 2 * BATCH * EMB * WIDTH


def tile_adaptivelstmcell_pb_kernel(
    tc,
    x,
    hx,
    cx,
    zw,
    zb,
    w_ih_words,
    w_ih_scales,
    w_hh_words,
    w_hh_scales,
    b_ih,
    b_hh,
    norm_alpha_w,
    bias_beta_w,
    ln_i_w,
    ln_i_b,
    ln_h_w,
    ln_h_b,
    ln_c_w,
    ln_c_b,
    out_0,
    out_1,
):
    nc = tc.nc
    path_words = (w_hh_words, w_ih_words)
    path_scales = (w_hh_scales, w_ih_scales)
    path_gain = (ln_h_w, ln_i_w)
    path_shift = (ln_h_b, ln_i_b)

    with ExitStack() as ctx:
        const = ctx.enter_context(tc.tile_pool(name="const", bufs=1))
        raw_pool = ctx.enter_context(tc.tile_pool(name="raw", bufs=13))
        operand_pool = ctx.enter_context(tc.tile_pool(name="operand", bufs=2))
        slab_pool = ctx.enter_context(tc.tile_pool(name="slab", bufs=14))
        alpha_pool = ctx.enter_context(tc.tile_pool(name="alpha", bufs=2))
        unread_pool = ctx.enter_context(tc.tile_pool(name="unread", bufs=2))
        stat_pool = ctx.enter_context(tc.tile_pool(name="stat", bufs=2))
        scaled_pool = ctx.enter_context(tc.tile_pool(name="scaled", bufs=8))
        psum = ctx.enter_context(tc.psum_pool(name="psum", bufs=2))
        ctx.enter_context(tc.manual_schedule())

        ident_bf16 = const.tile([P, P], BF16, name="ident_bf16")
        make_identity(nc, ident_bf16[:])
        ident_f32 = const.tile([P, P], F32, name="ident_f32")
        make_identity(nc, ident_f32[:])
        hidden_bias_rows = const.tile([P, P], BF16, name="hidden_bias_rows")
        nc.vector.memset(hidden_bias_rows[:], 0.0)
        eps = const.tile([P, 1], F32, name="eps")
        nc.vector.memset(eps[:], EPS)
        quarter_eps = const.tile([P, 1], F32, name="quarter_eps")
        nc.vector.memset(quarter_eps[:], EPS / GATES)
        minus_half = const.tile([P, 1], F32, name="minus_half")
        nc.vector.memset(minus_half[:], -0.5)

        words = []
        planes = []
        for path in range(PATHS):
            words.append(const.tile([P, GATES, PASSES, 2 * WIDTH], U8, name="words%d" % path, align_bytes=64))
            planes.append(const.tile([P, PASSES, ROW], U8, name="planes%d" % path, align_bytes=64))

        nc.vector.memset(planes[0][:].bitcast(I32), 0)

        alpha_wT = const.tile([P, SLABS, WIDTH], BF16, name="alpha_wT")
        beta_wT = const.tile([P, SLABS, WIDTH], BF16, name="beta_wT")
        hidden_bias_cols = const.tile([P, P], F32, name="hidden_bias_cols")
        gain_rep = const.tile([P, PATHS, len(ROW_GATES) * WIDTH], BF16, name="gain_rep")
        shift_rep = const.tile([P, len(ROW_GATES) * WIDTH], F32, name="shift_rep")
        vector_rows = const.tile([P, P], BF16, name="vector_rows")
        vector_cols = const.tile([P, P], F32, name="vector_cols")
        shift_cols = const.tile([P, ROW // P], F32, name="shift_cols")
        cell_gain_rep = const.tile([P, WIDTH], BF16, name="cell_gain_rep")
        cell_shift_rep = const.tile([P, WIDTH], BF16, name="cell_shift_rep")
        input_bias_rows = const.tile([P, WIDTH], BF16, name="input_bias_rows")
        nc.gpsimd.memset(input_bias_rows[:], 0.0)

        raw = {}
        operands = {}
        banks = {}
        slabs = {}
        stats = {}
        turned_slabs = {}
        scaled_slabs = {}
        summed_slabs = {}

        def load_batch_tile(bt, keys=("hx", "zw", "zb", "x")):
            rows = slice(bt * P, (bt + 1) * P)
            sources = {
                "x": x[rows, :],
                "hx": hx[rows, :],
                "zw": zw[rows, :, :].rearrange("b s a -> b (s a)"),
                "zb": zb[rows, :, :].rearrange("b s a -> b (s a)"),
            }
            for key in keys:
                loaded = raw_pool.tile([P, WIDTH], BF16, name="raw_" + key, tag="raw")
                nc.sync.dma_start(out=loaded[:], in_=sources[key])
                raw[(bt, key)] = loaded

        def load_cell_state(bt):
            loaded = raw_pool.tile([P, WIDTH], BF16, name="raw_cx", tag="raw")
            nc.sync.dma_start(out=loaded[:], in_=cx[bt * P : (bt + 1) * P, :])
            raw[(bt, "cx")] = loaded

        def load_scale_planes(path, gates=(0, GATES)):
            cols = slice(gates[0] * WIDTH, gates[1] * WIDTH)
            for g in range(PASSES):
                for r in range(4):
                    nc.sync.dma_start(
                        out=planes[path][r:P:32, g, cols].bitcast(I32),
                        in_=path_scales[path][g, r:16:4, cols].bitcast(I32),
                    )

        def load_hyper_weights(slot):
            for key, source in (("alpha_w", norm_alpha_w), ("beta_w", bias_beta_w)):
                loaded = raw_pool.tile([P, BLOCKS, EMB], BF16, name="raw_" + key, tag="raw")
                nc.sync.dma_start(
                    out=loaded[:], in_=source[(slot + GATES) % SLABS].rearrange("(p blk) a -> p blk a", p=P)
                )
                raw[(slot, key)] = loaded

        def load_words(slot):
            path, gate = divmod(slot, GATES)
            byte_cols = slice(2 * gate * WIDTH, 2 * (gate + 1) * WIDTH)
            nc.sync.dma_start(
                out=words[path][:, gate, :, :].bitcast(I32),
                in_=path_words[path][:, :, byte_cols].bitcast(I32).rearrange("g p n -> p g n"),
            )

        def row_cols(gate):
            place = ROW_GATES.index(gate)
            return slice(place * WIDTH, (place + 1) * WIDTH)

        def load_gains(path):
            cols = slice(ROW_GATES[0] * WIDTH, (ROW_GATES[-1] + 1) * WIDTH)
            nc.sync.dma_start(out=gain_rep[:, path, :], in_=path_gain[path][cols].partition_broadcast(P))

        def load_cell_vectors():
            nc.sync.dma_start(out=cell_gain_rep[:], in_=ln_c_w.partition_broadcast(P))
            nc.sync.dma_start(out=cell_shift_rep[:], in_=ln_c_b.partition_broadcast(P))

        def load_shifts(gate):
            cols = slice(gate * WIDTH, (gate + 1) * WIDTH)
            for path in range(PATHS):
                loaded = raw_pool.tile([P, WIDTH], BF16, name="raw_shift", tag="raw")
                nc.sync.dma_start(out=loaded[:], in_=path_shift[path][cols].partition_broadcast(P))
                raw[(gate, "shift%d" % path)] = loaded

        def add_shifts(gate):
            nc.gpsimd.tensor_tensor(
                out=shift_rep[:, row_cols(gate)], in0=raw[(gate, "shift0")][:], in1=raw[(gate, "shift1")][:], op=ALU.add
            )

        def turn_activations(bt, keys=("hx", "x")):
            for key in keys:
                pairs = raw[(bt, key)][:].bitcast(F32)
                turned = psum.tile([P, PASSES, 2, P], F32, name="turned_" + key, tag="turn")
                for g in range(PASSES):
                    for u in range(2):
                        nc.tensor.transpose(
                            out=turned[:, g, u, :],
                            in_=pairs[:, (K_PASS // 2) * g + u : (K_PASS // 2) * (g + 1) : 2],
                            identity=ident_f32[:],
                        )
                operands[(bt, "turned_" + key)] = turned

        def copy_activations(bt, keys=("hx", "x")):
            for key in keys:
                side_by_side = operand_pool.tile(
                    [P, PASSES * P * 4], BF16, name="side_by_side_" + key, tag="side_by_side", align_bytes=64
                )
                nc.scalar.copy(
                    out=side_by_side[:].bitcast(F32).rearrange("p (g b u) -> p g b u", g=PASSES, u=2),
                    in_=operands[(bt, "turned_" + key)][:].rearrange("p g u b -> p g b u"),
                )
                operands[(bt, "side_by_side_" + key)] = side_by_side

        def quantise_activations(bt, paths=(0, 1)):
            for path in paths:
                key = ("hx", "x")[path]
                codes = operand_pool.tile([P, PASSES * P], U32, name="codes%d" % path, align_bytes=64)
                code_scales = operand_pool.tile([P, PASSES * P], U8, name="code_scales%d" % path, align_bytes=64)
                nc.vector.quantize_mx(out=codes[:].bitcast(FP8X4), scales=code_scales[:], in_=operands[(bt, "side_by_side_" + key)][:])
                operands[(bt, "codes%d" % path)] = codes
                operands[(bt, "code_scales%d" % path)] = code_scales

        def turn_embeddings(bt):
            for key in ("zw", "zb"):
                turned = psum.tile([P, SLABS, P], BF16, name="turned_" + key, tag="turn")
                for slot in range(SLABS):
                    emb = (slot + GATES) % SLABS
                    nc.tensor.transpose(
                        out=turned[:, slot, :], in_=raw[(bt, key)][:, emb * EMB : (emb + 1) * EMB], identity=ident_bf16[:]
                    )
                operands[(bt, "turned_" + key)] = turned

        def copy_embeddings(bt):
            for key in ("zw", "zb"):
                embT = operand_pool.tile([P, SLABS, P], BF16, name=key + "T")
                nc.scalar.copy(out=embT[:], in_=operands[(bt, "turned_" + key)][:])
                operands[(bt, key)] = embT

        def load_vector_rows():
            for v, vector in enumerate((ln_i_w, ln_h_w, ln_i_b, ln_h_b)):
                nc.sync.dma_start(
                    out=vector_rows[(ROW // P) * v : (ROW // P) * (v + 1), :], in_=vector.rearrange("(c p) -> c p", p=P)
                )

        def turn_vectors():
            turned = psum.tile([P, P], BF16, name="turned_vectors", tag="turn")
            nc.tensor.transpose(out=turned[:], in_=vector_rows[:], identity=ident_bf16[:])
            nc.scalar.copy(out=vector_cols[:], in_=turned[:])
            blocks = ROW // P
            nc.gpsimd.tensor_tensor(
                out=shift_cols[:], in0=vector_cols[:, 2 * blocks : 3 * blocks], in1=vector_cols[:, 3 * blocks : 4 * blocks], op=ALU.add
            )

        def turn_hyper_weights(slot):
            for key in ("alpha_w", "beta_w"):
                turned = psum.tile([P, BLOCKS, P], BF16, name="turned_" + key, tag="turn")
                for blk in range(BLOCKS):
                    nc.tensor.transpose(out=turned[:, blk, :], in_=raw[(slot, key)][:, blk, :], identity=ident_bf16[:])
                operands[(slot, "turned_" + key)] = turned

        def copy_hyper_weights(slot):
            nc.vector.tensor_copy(
                out=alpha_wT[:, slot, :].rearrange("a (p blk) -> a p blk", blk=BLOCKS),
                in_=operands[(slot, "turned_alpha_w")][:].rearrange("a blk p -> a p blk"),
            )
            nc.scalar.copy(
                out=beta_wT[:, slot, :].rearrange("a (p blk) -> a p blk", blk=BLOCKS),
                in_=operands[(slot, "turned_beta_w")][:].rearrange("a blk p -> a p blk"),
            )

        def slab_matmuls(n):
            bt, slot = divmod(n, SLABS)
            path, gate = divmod(slot, GATES)
            alpha_banks, xh_banks, beta_banks = [], [], []
            for half in range(HALVES):
                bank = psum.tile([P, BANK], F32, name="alpha_bank", tag="alpha")
                nc.tensor.matmul(
                    bank[:],
                    lhsT=operands[(bt, "zw")][:, slot, :],
                    rhs=alpha_wT[:, slot, half * BANK : (half + 1) * BANK],
                    start=True,
                    stop=True,
                )
                alpha_banks.append(bank)
            for half in range(HALVES):
                first = gate * WIDTH + half * BANK
                bank = psum.tile([P, BANK], F32, name="xh_bank", tag="xh")
                for g in range(PASSES):
                    nc.tensor.matmul_mx(
                        out=bank[:],
                        lhsT=operands[(bt, "codes%d" % path)][:, g * P : (g + 1) * P].bitcast(FP8X4),
                        lhsT_scale=operands[(bt, "code_scales%d" % path)][:, g * P : (g + 1) * P],
                        rhs=words[path][:, gate, g, 2 * half * BANK : 2 * (half + 1) * BANK].bitcast(FP4X4),
                        rhs_scale=planes[path][:, g, first : first + BANK],
                        start=(g == 0),
                        stop=(g == PASSES - 1),
                    )
                xh_banks.append(bank)
            for half in range(HALVES):
                bank = psum.tile([P, BANK], F32, name="beta_bank", tag="beta")
                nc.tensor.matmul(
                    bank[:],
                    lhsT=operands[(bt, "zb")][:, slot, :],
                    rhs=beta_wT[:, slot, half * BANK : (half + 1) * BANK],
                    start=True,
                    stop=False,
                )
                if path == 1:
                    nc.tensor.matmul(
                        bank[:],
                        lhsT=ident_bf16[:, gate : gate + 1].to_broadcast([P, P]),
                        rhs=input_bias_rows[:, half * BANK : (half + 1) * BANK],
                        start=False,
                        stop=True,
                    )
                beta_banks.append(bank)
            if path == 0:
                for half in range(HALVES):
                    for q in range(QUARTERS):
                        col = gate * BLOCKS + half * QUARTERS + q
                        nc.tensor.matmul(
                            beta_banks[half][:, q * P : (q + 1) * P],
                            lhsT=hidden_bias_cols[:, col : col + 1].to_broadcast([P, P]),
                            rhs=ident_f32[:],
                            is_transpose=True,
                            start=False,
                            stop=(q == QUARTERS - 1),
                        )
            alpha_sb = alpha_pool.tile([P, HALVES, BANK], F32, name="alpha_sb")
            for half in range(HALVES):
                nc.scalar.copy(out=alpha_sb[:, half, :], in_=alpha_banks[half][:])
            banks[n] = (alpha_sb, xh_banks, beta_banks)

        def slab_combine(n):
            bt, slot = divmod(n, SLABS)
            path, gate = divmod(slot, GATES)
            if slot == 0:
                stats[(bt, "sum_parts")] = stat_pool.tile([P, PATHS, GATES * HALVES], F32, name="sum_parts")
                stats[(bt, "square_parts")] = stat_pool.tile([P, PATHS, GATES], F32, name="square_parts")
            alpha_sb, xh_banks, beta_banks = banks[n]
            pre = slab_pool.tile([P, WIDTH], F32, name="pre", tag="slab")
            for half in range(HALVES):
                nc.vector.tensor_tensor(
                    out=pre[:, half * BANK : (half + 1) * BANK], in0=xh_banks[half][:], in1=alpha_sb[:, half, :], op=ALU.mult
                )
            for half in range(HALVES):
                half_cols = slice(half * BANK, (half + 1) * BANK)
                part = gate * HALVES + half
                nc.vector.scalar_tensor_tensor(
                    out=pre[:, half_cols],
                    in0=pre[:, half_cols],
                    scalar=1.0,
                    in1=beta_banks[half][:],
                    op0=ALU.mult,
                    op1=ALU.add,
                    accum_out=stats[(bt, "sum_parts")][:, path, part : part + 1],
                )
            slabs[(bt, slot)] = pre

        def slab_squares(n):
            bt, slot = divmod(n, SLABS)
            path, gate = divmod(slot, GATES)
            unread = unread_pool.tile([P, WIDTH], BF16, name="unread")
            nc.scalar.activation(
                out=unread[:],
                in_=slabs[(bt, slot)][:],
                func=FUNC.Square,
                accum_out=stats[(bt, "square_parts")][:, path, gate : gate + 1],
            )

        def small(bt, name, width):
            stats[(bt, name)] = stat_pool.tile([P, width], F32, name=name)
            return stats[(bt, name)]

        def row_mean(bt, path):
            nc.scalar.activation(
                out=small(bt, "scaled_sums%d" % path, GATES * HALVES)[:],
                in_=stats[(bt, "sum_parts")][:, path, :],
                func=FUNC.Identity,
                scale=1.0 / ROW,
                accum_out=small(bt, "mean%d" % path, 1)[:],
            )

        def row_inverse_deviation(bt, path):
            mean_squared = small(bt, "mean_squared%d" % path, 1)
            nc.scalar.activation(out=mean_squared[:], in_=stats[(bt, "mean%d" % path)][:], func=FUNC.Square)
            quarter_rest = small(bt, "quarter_rest%d" % path, 1)
            nc.scalar.activation(
                out=quarter_rest[:], in_=mean_squared[:], func=FUNC.Identity, scale=-1.0 / GATES, bias=quarter_eps[:]
            )
            variance = small(bt, "variance%d" % path, 1)
            nc.scalar.activation(
                out=small(bt, "scaled_squares%d" % path, GATES)[:],
                in_=stats[(bt, "square_parts")][:, path, :],
                func=FUNC.Identity,
                scale=1.0 / ROW,
                bias=quarter_rest[:],
                accum_out=variance[:],
            )
            nc.gpsimd.tensor_tensor(
                out=small(bt, "inverse%d" % path, 1)[:], in0=variance[:], in1=minus_half[:], op=ALU.pow
            )

        def center_and_gain(bt, gate, path):
            pre = slabs[(bt, path * GATES + gate)]
            nc.vector.scalar_tensor_tensor(
                out=pre[:],
                in0=pre[:],
                scalar=stats[(bt, "mean%d" % path)][:],
                in1=gain_rep[:, path, row_cols(gate)],
                op0=ALU.subtract,
                op1=ALU.mult,
            )

        def scale_and_add(bt, gate, path):
            pre = slabs[(bt, path * GATES + gate)]
            nc.vector.scalar_tensor_tensor(
                out=pre[:],
                in0=pre[:],
                scalar=stats[(bt, "inverse%d" % path)][:],
                in1=(shift_rep[:, row_cols(gate)] if path == 0 else slabs[(bt, gate)][:]),
                op0=ALU.mult,
                op1=ALU.add,
            )
        def row_activate(bt, gate):
            pre = slabs[(bt, GATES + gate)]
            nc.scalar.activation(out=pre[:], in_=pre[:], func=(FUNC.Tanh if gate == GATE_J else FUNC.Sigmoid))

        def normalise(bt, gate, path):
            pre = slabs[(bt, path * GATES + gate)]
            nc.vector.tensor_scalar(
                out=pre[:],
                in0=pre[:],
                scalar1=stats[(bt, "mean%d" % path)][:],
                scalar2=stats[(bt, "inverse%d" % path)][:],
                op0=ALU.subtract,
                op1=ALU.mult,
            )

        def turn_forward(bt, gate, path, tags=("turn", "turn")):
            pre = slabs[(bt, path * GATES + gate)]
            for half in range(HALVES):
                turned = psum.tile([P, QUARTERS, P], F32, name="turned_slab", tag=tags[half])
                for q in range(QUARTERS):
                    first = half * BANK + q * P
                    nc.tensor.transpose(out=turned[:, q, :], in_=pre[:, first : first + P], identity=ident_f32[:])
                turned_slabs[(bt, gate, half, path)] = turned

        def gain_and_shift(bt, gate, path, on_vector=False):
            blocks = ROW // P
            for half in range(HALVES):
                first = gate * BLOCKS + half * QUARTERS
                turned = turned_slabs[(bt, gate, half, path)]
                scaled = scaled_pool.tile([P, QUARTERS, P], F32, name="scaled")
                if on_vector:
                    nc.vector.tensor_tensor(
                        out=scaled[:],
                        in0=turned[:],
                        in1=vector_cols[:, first : first + QUARTERS].unsqueeze(2).to_broadcast([P, QUARTERS, P]),
                        op=ALU.mult,
                    )
                else:
                    for q in range(QUARTERS):
                        col = (1 - path) * blocks + first + q
                        if path == 0:
                            nc.scalar.activation(
                                out=scaled[:, q, :],
                                in_=turned[:, q, :],
                                func=FUNC.Identity,
                                scale=vector_cols[:, col : col + 1],
                                bias=shift_cols[:, first + q : first + q + 1],
                            )
                        else:
                            nc.scalar.activation(
                                out=scaled[:, q, :], in_=turned[:, q, :], func=FUNC.Identity, scale=vector_cols[:, col : col + 1]
                            )
                scaled_slabs[(bt, gate, half, path)] = scaled

        def turn_back(bt, gate, tags=("turn", "turn")):
            for half in range(HALVES):
                summed = psum.tile([P, BANK], F32, name="summed", tag=tags[half])
                for q in range(QUARTERS):
                    for path in range(PATHS):
                        nc.tensor.matmul(
                            summed[:, q * P : (q + 1) * P],
                            lhsT=scaled_slabs[(bt, gate, half, path)][:, q, :],
                            rhs=ident_f32[:],
                            is_transpose=True,
                            start=(path == 0),
                            stop=(path == PATHS - 1),
                        )
                summed_slabs[(bt, gate, half)] = summed

        def activate(bt, gate):
            for half in range(HALVES):
                nc.scalar.activation(
                    out=slabs[(bt, GATES + gate)][:, half * BANK : (half + 1) * BANK],
                    in_=summed_slabs[(bt, gate, half)][:],
                    func=(FUNC.Tanh if gate == GATE_J else FUNC.Sigmoid),
                )

        def cell_products(bt, first, engine):
            if first:
                gate_i = slabs[(bt, GATES)]
                engine.tensor_tensor(out=gate_i[:], in0=gate_i[:], in1=slabs[(bt, GATES + 1)][:], op=ALU.mult)
            else:
                gate_f = slabs[(bt, GATES + 2)]
                engine.tensor_tensor(out=gate_f[:], in0=gate_f[:], in1=raw[(bt, "cx")][:], op=ALU.mult)

        def cell_sum(bt):
            cell = slabs[(bt, GATES)]
            total = small(bt, "cell_total", 1)
            nc.vector.scalar_tensor_tensor(
                out=cell[:],
                in0=cell[:],
                scalar=1.0,
                in1=slabs[(bt, GATES + 2)][:],
                op0=ALU.mult,
                op1=ALU.add,
                accum_out=total[:],
            )
            mean = small(bt, "cell_mean", 1)
            nc.scalar.activation(out=mean[:], in_=total[:], func=FUNC.Identity, scale=1.0 / WIDTH)
            mean_squared = small(bt, "cell_mean_squared", 1)
            nc.scalar.activation(out=mean_squared[:], in_=mean[:], func=FUNC.Square)
            rest = small(bt, "cell_rest", 1)
            nc.scalar.activation(out=rest[:], in_=mean_squared[:], func=FUNC.Identity, scale=-1.0, bias=eps[:])
            unread = unread_pool.tile([P, WIDTH], BF16, name="unread")
            squares = small(bt, "cell_squares", 1)
            nc.scalar.activation(out=unread[:], in_=cell[:], func=FUNC.Square, accum_out=squares[:])
            variance = small(bt, "cell_variance", 1)
            nc.scalar.activation(out=variance[:], in_=squares[:], func=FUNC.Identity, scale=1.0 / WIDTH, bias=rest[:])
            nc.gpsimd.tensor_tensor(
                out=small(bt, "cell_inverse", 1)[:], in0=variance[:], in1=minus_half[:], op=ALU.pow
            )

        def cell_norm(bt):
            rows = slice(bt * P, (bt + 1) * P)
            cell = slabs[(bt, GATES)]
            tanh_cy = slabs[(bt, GATES + 2)]
            for half in range(HALVES):
                cols = slice(half * BANK, (half + 1) * BANK)
                nc.vector.scalar_tensor_tensor(
                    out=cell[:, cols], in0=cell[:, cols], scalar=stats[(bt, "cell_mean")][:], in1=cell_gain_rep[:, cols], op0=ALU.subtract, op1=ALU.mult
                )
            for half in range(HALVES):
                cols = slice(half * BANK, (half + 1) * BANK)
                nc.vector.scalar_tensor_tensor(
                    out=cell[:, cols], in0=cell[:, cols], scalar=stats[(bt, "cell_inverse")][:], in1=cell_shift_rep[:, cols], op0=ALU.mult, op1=ALU.add
                )
                nc.sync.dma_start(out=out_1[rows, cols], in_=cell[:, cols])
                nc.scalar.activation(out=tanh_cy[:, cols], in_=cell[:, cols], func=FUNC.Tanh)

        def hidden_state(bt, engine=nc.vector):
            rows = slice(bt * P, (bt + 1) * P)
            gate_o = slabs[(bt, GATES + 3)]
            for half in range(HALVES):
                cols = slice(half * BANK, (half + 1) * BANK)
                engine.tensor_tensor(out=gate_o[:, cols], in0=gate_o[:, cols], in1=slabs[(bt, GATES + 2)][:, cols], op=ALU.mult)
                nc.sync.dma_start(out=out_0[rows, cols], in_=gate_o[:, cols])

        load_batch_tile(0, ("hx", "zw", "zb"))
        nc.sync.dma_start(out=hidden_bias_rows[0 : ROW // P, :], in_=b_hh.rearrange("(c p) -> c p", p=P))
        load_hyper_weights(0)
        load_words(0)
        load_scale_planes(0)
        load_hyper_weights(1)
        load_hyper_weights(2)
        load_words(1)
        load_batch_tile(0, ("x",))
        nc.sync.dma_start(out=input_bias_rows[0:GATES, :], in_=b_ih.rearrange("(g n) -> g n", g=GATES))
        load_hyper_weights(3)
        load_words(2)
        turn_activations(0, ("hx",))
        copy_activations(0, ("hx",))
        turned_bias = psum.tile([P, P], BF16, name="turned_bias", tag="beta")
        nc.tensor.transpose(out=turned_bias[:], in_=hidden_bias_rows[:], identity=ident_bf16[:])
        nc.vector.tensor_copy(out=hidden_bias_cols[:], in_=turned_bias[:])
        quantise_activations(0, (0,))
        nc.vector.memset(planes[1][:].bitcast(I32), 0)
        turn_embeddings(0)
        copy_embeddings(0)
        turn_hyper_weights(0)
        copy_hyper_weights(0)
        turn_hyper_weights(1)
        copy_hyper_weights(1)
        slab_matmuls(0)
        turn_hyper_weights(2)

        last = BATCH_TILES - 1

        for n in range(ALL_SLABS):
            bt, k = divmod(n, SLABS)
            has_next = bt < last
            tails = [(t, n - SLABS * (t + 1)) for t in (bt - 2, bt - 1) if t >= 0]
            acts_round = 5
            slab_combine(n)

            for t, r in tails:
                if r == 0:
                    gain_and_shift(t, GATE_I, 0)
                if r == 1:
                    gain_and_shift(t, GATE_O, 0)
                if r == 2:
                    gain_and_shift(t, GATE_I, 1)
                if r == 3:
                    activate(t, GATE_I)
                if r == 4:
                    gain_and_shift(t, GATE_O, 1)
                    row_activate(t, GATE_F)
                if r == 5:
                    activate(t, GATE_O)
                    row_activate(t, GATE_J)
            if bt == last and k == 6:
                gain_and_shift(bt, GATE_I, 0)
            if bt == last and k == 7:
                gain_and_shift(bt, GATE_J, 0)
            if n + 2 < SLABS:
                copy_hyper_weights(n + 2)
            if has_next:
                if k == acts_round + 1:
                    copy_activations(bt + 1)
                if k == acts_round + 2:
                    copy_embeddings(bt + 1)
            if n + 1 < ALL_SLABS:
                slab_matmuls(n + 1)

            for path in range(PATHS):
                if k == (path + 1) * GATES - 1:
                    row_mean(bt, path)
            slab_squares(n)
            for path in range(PATHS):
                if k == (path + 1) * GATES - 1:
                    row_inverse_deviation(bt, path)

            if n + 4 < SLABS:
                load_hyper_weights(n + 4)
            if n == 1:
                load_scale_planes(1)
            if n + 3 < SLABS:
                load_words(n + 3)
            if n == 1:
                load_vector_rows()
            if n == 4:
                load_batch_tile(1, ("hx", "x"))
                load_batch_tile(1, ("zw", "zb"))
                load_gains(0)
                for gate in ROW_GATES:
                    load_shifts(gate)
                load_gains(1)
                load_cell_vectors()
            if n == 1:
                turn_activations(0, ("x",))
                copy_activations(0, ("x",))
            if n + TURN_AHEAD < SLABS:
                turn_hyper_weights(n + TURN_AHEAD)
            if n == 3:
                turn_vectors()

            if k == 0 and has_next and bt >= 1:
                load_batch_tile(bt + 1)
            if k == 0 and bt >= 1:
                load_cell_state(bt - 1)
            if k == 1 and bt == last:
                load_cell_state(last)

            for t, r in tails:
                if r == 0:
                    normalise(t, GATE_O, 0)
                if r == 1:
                    normalise(t, GATE_I, 1)
                if r == 3:
                    normalise(t, GATE_O, 1)
                if r == 5:
                    cell_products(t, False, nc.gpsimd)
                    cell_products(t, True, nc.gpsimd)
            if k == 7 and has_next:
                normalise(bt, GATE_I, 0)
            if k == 5 and not has_next:
                normalise(bt, GATE_I, 0)
            if k == 6 and not has_next:
                normalise(bt, GATE_J, 0)
            if k == 7 and not has_next:
                normalise(bt, GATE_O, 0)

            for t, r in tails:
                if r == 0:
                    turn_forward(t, GATE_O, 0)
                if r == 1:
                    turn_forward(t, GATE_I, 1)
                if r == 2:
                    turn_back(t, GATE_I)
                if r == 3:
                    turn_forward(t, GATE_O, 1)
                if r == 4:
                    turn_back(t, GATE_O)
            if has_next:
                if k == acts_round:
                    turn_activations(bt + 1)
                if k == acts_round + 1:
                    turn_embeddings(bt + 1)
                if k == acts_round + 2:
                    turn_forward(bt, GATE_I, 0)
            else:
                if k == 5:
                    turn_forward(bt, GATE_I, 0)
                if k == 6:
                    turn_forward(bt, GATE_J, 0)
                if k == 7:
                    turn_forward(bt, GATE_O, 0)

            for t, r in tails:
                if r == 0:
                    center_and_gain(t, GATE_J, 0)
                if r == 1:
                    scale_and_add(t, GATE_J, 0)
                if r == 2:
                    center_and_gain(t, GATE_F, 1)
                    center_and_gain(t, GATE_J, 1)
                if r == 3:
                    scale_and_add(t, GATE_F, 1)
                if r == 4:
                    scale_and_add(t, GATE_J, 1)
                if r == 6:
                    cell_sum(t)
                if r == 7:
                    cell_norm(t)
                if r == 8:
                    hidden_state(t, nc.gpsimd)
            if k == (7 if bt == 0 else 5):
                center_and_gain(bt, GATE_F, 0)
            if k == 6 and bt > 0:
                scale_and_add(bt, GATE_F, 0)
            if n == SLABS + 1:
                scale_and_add(0, GATE_F, 0)
            if n == 5:
                add_shifts(GATE_F)
                add_shifts(GATE_J)
            if n == 2:
                quantise_activations(0, (1,))
            if k == acts_round + 1 and has_next:
                quantise_activations(bt + 1)

        gain_and_shift(last, GATE_O, 0)
        center_and_gain(last, GATE_F, 1)
        normalise(last, GATE_I, 1)
        normalise(last, GATE_J, 1)
        turn_forward(last, GATE_I, 1, ("alpha", "alpha"))
        turn_forward(last, GATE_J, 1, ("xh", "xh"))
        hidden_state(last - 1)
        scale_and_add(last, GATE_F, 1)
        gain_and_shift(last, GATE_I, 1)
        turn_back(last, GATE_I, ("beta", "beta"))
        gain_and_shift(last, GATE_J, 1, on_vector=True)
        turn_back(last, GATE_J, ("alpha", "alpha"))
        row_activate(last, GATE_F)
        cell_products(last, False, nc.gpsimd)
        normalise(last, GATE_O, 1)
        turn_forward(last, GATE_O, 1, ("xh", "xh"))
        activate(last, GATE_I)
        activate(last, GATE_J)
        gain_and_shift(last, GATE_O, 1, on_vector=True)
        turn_back(last, GATE_O, ("beta", "beta"))
        cell_products(last, True, nc.vector)
        cell_sum(last)
        activate(last, GATE_O)
        cell_norm(last)
        hidden_state(last)
